import numpy as np
import ml_dtypes


def mxq(x, axis, fmt="e4m3"):
    dtype, down = {"e4m3": (ml_dtypes.float8_e4m3fn, 7), "e5m2": (ml_dtypes.float8_e5m2, 14)}[fmt]
    v = np.moveaxis(np.asarray(x, np.float32).astype(ml_dtypes.bfloat16).astype(np.float64), axis, -1)
    blocks = v.reshape(v.shape[:-1] + (-1, 32))
    amax = np.abs(blocks).max(-1, keepdims=True)
    byte = np.maximum(np.where(amax > 0, np.frexp(amax)[1] - 1 + 127, 0) - down, 1)
    scale = np.exp2(byte - 127.0)
    codes = (blocks / scale).astype(np.float32).astype(dtype).astype(np.float64)
    return np.moveaxis((codes * scale).reshape(v.shape), -1, axis)


WIDE = False


def mx_kscale(k):
    if not WIDE:
        return np.ones(k)
    levels = np.array([10, -10, 5, -5, 0])
    if k % 512:
        return np.exp2(np.random.permutation(np.resize(levels, k // 32))).repeat(32)
    a = np.empty((k // 512, 16))
    for p in range(k // 512):
        a[p, :8] = np.random.permutation(np.resize(levels, 8))
        for g in range(8):
            far = levels[np.abs(levels - a[p, g]) >= 10]
            a[p, g + 8] = far[np.random.randint(len(far))]
    return np.exp2(a.ravel()).repeat(32)


BF16 = ml_dtypes.bfloat16


def bf(x):
    return np.asarray(x, np.float32).astype(BF16)


def f64(x):
    return np.asarray(x).astype(np.float64)


M, K, N = 1024, 2048, 2048
TINY = 1e-15
EPS = 1e-6
C = 1.0
S = 1.0 / np.sqrt(C)
SQRTC = np.sqrt(C)


def _asinh(t):
    return np.log(t + np.sqrt(t * t + 1.0))


def _sinh(t):
    return 0.5 * (np.exp(t) - np.exp(-t))


def _norm(p):
    return np.sqrt(np.sum(p * p, axis=-1, keepdims=True))


def _sinhc(z):
    y = _sinh(z) / np.maximum(z, EPS)
    y0 = 1.0 + z * z / 6.0
    return np.where(np.abs(z) < EPS, y0, y)


def _beta(x):
    denom = np.sqrt(1.0 + C * np.sum(x * x, axis=-1, keepdims=True))
    return 1.0 / np.maximum(denom, TINY)


def _log0(y):
    s = _norm(y)
    coef = _asinh(s / S) / np.maximum(s / S, EPS)
    return coef * y


def _exp0(v):
    r = _norm(v)
    coef = _sinh(r / S) / np.maximum(r / S, EPS)
    return coef * v


def _proj_tan0(v, max_norm=20.0):
    r = np.maximum(_norm(v), EPS)
    return np.minimum(max_norm / r, 1.0) * v


def _pt_0_to_y(y, v):
    b = _beta(y)
    coef = C * b / (1.0 + b)
    dot = np.sum(y * v, axis=-1, keepdims=True)
    return v + coef * dot * y


def _gyro_add(x, y):
    b_x = _beta(x)
    b_y = _beta(y)
    s2 = S * S
    xy = np.sum(x * y, axis=-1, keepdims=True)
    coef = b_x / (1.0 + b_x) * (xy / s2) + (1.0 - b_y) / b_y
    return x + y + coef * x


def _exp_map(x, v):
    s2 = S * S
    x_norm2 = np.sum(x * x, axis=-1, keepdims=True)
    v_norm2 = np.sum(v * v, axis=-1, keepdims=True)
    dot_x_v = np.sum(x * v, axis=-1, keepdims=True)
    g_pvv = np.maximum(v_norm2 - dot_x_v * dot_x_v / (s2 + x_norm2), TINY)
    r_g = np.sqrt(g_pvv)
    b_x = _beta(x)
    coef1 = b_x / (1.0 + b_x)
    coef2 = -(C * b_x ** 3) / np.maximum(1.0 + b_x, TINY) ** 2
    dpi_v = coef1 * v + coef2 * dot_x_v * x
    lambda_x = (1.0 + b_x) / np.maximum(b_x, TINY)
    z_arg = np.clip(SQRTC * r_g, -20.0, 20.0)
    w = lambda_x * _sinhc(z_arg) * dpi_v
    return _gyro_add(x, w)


def setup_inputs():
    xn, un, bn = 3.0, 2.0, 2.0
    ax, aw, ab = 0.5, 2.0, 0.75
    s = mx_kscale(K)
    s = s / np.sqrt(np.mean(s * s))
    xs = xn / np.sqrt(K * (1.0 + ax * ax))
    ws = un / (_asinh(xn) * np.sqrt(N * (1.0 + ax * ax + ax * ax * aw * aw) / (1.0 + ax * ax)))
    bs = bn / np.sqrt(N * (1.0 + ab * ab))
    return {"x": bf((np.random.standard_normal((M, K)) + ax) * xs * s),
            "W": bf((np.random.standard_normal((N, K)) + aw / np.sqrt(K)) * ws / s),
            "b": bf((np.random.standard_normal(N) + ab) * bs)}


def reference(x, W, b):
    x, W, b = f64(x), f64(W), f64(b)
    v = _log0(x)
    u = mxq(v, 1, "e4m3") @ mxq(W, 1, "e4m3").T
    u = _proj_tan0(u)
    y = _exp0(u)
    bt = _pt_0_to_y(y, b)
    return _exp_map(y, bt)

@@ -1,0 +1,462 @@
+from contextlib import ExitStack
+
+import concourse.mybir as mybir
+from concourse.masks import make_identity
+
+F32 = mybir.dt.float32
+BF16 = mybir.dt.bfloat16
+U32 = mybir.dt.uint32
+U8 = mybir.dt.uint8
+FP8X4 = mybir.dt.float8_e4m3fn_x4
+ALU = mybir.AluOpType
+ACT = mybir.ActivationFunctionType
+AX = mybir.AxisListType
+
+P = 128
+M, K, N = 1024, 2048, 2048
+MT = M // P
+KP = K // 512
+NCH = N // 512
+FLOPS = 2 * M * K * N
+
+V_EVERY = 99
+W_FIRST = 11
+LEAD = (15, 13, 8, 6, 5, 4)
+Q_LAG = 2
+MT1 = 4
+LATE_AT = {2: 32, 3: 40}
+XE1_ON_V = False
+
+
+def tile_pvfc_kernel(tc, x, W, b, out):
+    nc = tc.nc
+    with ExitStack() as ctx:
+        const = ctx.enter_context(tc.tile_pool(name="const", bufs=1))
+        xraw = ctx.enter_context(tc.tile_pool(name="xraw", bufs=4))
+        wraw = ctx.enter_context(tc.tile_pool(name="wraw", bufs=5))
+        vpool = ctx.enter_context(tc.tile_pool(name="vpool", bufs=4))
+        xgp = ctx.enter_context(tc.tile_pool(name="xgp", bufs=2))
+        wgp = ctx.enter_context(tc.tile_pool(name="wgp", bufs=6))
+        junk = ctx.enter_context(tc.tile_pool(name="junk", bufs=2))
+        junk1 = ctx.enter_context(tc.tile_pool(name="junk1", bufs=1))
+        opool = ctx.enter_context(tc.tile_pool(name="opool", bufs=3))
+        sm = ctx.enter_context(tc.tile_pool(name="sm", bufs=3))
+        psA = ctx.enter_context(tc.psum_pool(name="psA", bufs=4))
+        psB = ctx.enter_context(tc.psum_pool(name="psB", bufs=4))
+        ctx.enter_context(tc.manual_schedule())
+
+        warm = const.tile([P, 1], F32)
+        nc.vector.memset(warm[:], 1.0)
+        warm2 = const.tile([P, 1], F32)
+        nc.scalar.activation(out=warm2[:], in_=warm[:], func=ACT.Exp)
+        b_row = const.tile([P, N], BF16)
+        nc.vector.memset(b_row[:], 0.0)
+        nc.sync.dma_start(out=b_row[0:1, :], in_=b.unsqueeze(0))
+        ones_bf = const.tile([P, P], BF16)
+        nc.vector.memset(ones_bf[:], 1.0)
+        ident_f = const.tile([P, P], F32)
+        make_identity(nc, ident_f[:])
+        ident_bf = const.tile([P, P], BF16)
+        make_identity(nc, ident_bf[:])
+        expo3 = const.tile([P, 3, 2], F32)
+        nc.vector.memset(expo3[:, 0:2, :], 0.5)
+        nc.vector.memset(expo3[:, 2:3, :], -0.5)
+        expo2 = const.tile([P, 2], F32)
+        nc.vector.memset(expo2[:, 0:1], 0.5)
+        nc.vector.memset(expo2[:, 1:2], -0.5)
+
+        vcodes = const.tile([P, MT * 512], U32, align_bytes=64)
+        vscales = const.tile([P, MT * 512], U8, align_bytes=64)
+        wcodes = const.tile([P, NCH * KP * 512], U32, align_bytes=64)
+        wscales = const.tile([P, NCH * KP * 512], U8, align_bytes=64)
+        w_bc = const.tile([P, N], F32)
+        hwh = const.tile([P, 1], F32)
+        b2p = const.tile([P, NCH], F32)
+
+        x_v = x.rearrange("(p i) k -> p i k", i=MT)
+        W_v = W.rearrange("(g p) k -> p g k", p=P)
+        out_v = out.rearrange("(p i) n -> p i n", i=MT)
+        xr = []
+        wr = []
+        S = {}
+
+        def load_x(a):
+            t = xraw.tile([P, 2 * K], BF16, name="xr")
+            nc.sync.dma_start(out=t[:].rearrange("p (l k) -> p l k", l=2), in_=x_v[:, 2 * a : 2 * a + 2, :])
+            xr.append(t)
+
+        def load_w(h, pieces):
+            t = wraw.tile([P, 2 * K], BF16, name="wr")
+            kw = K // pieces
+            for s in range(pieces):
+                nc.sync.dma_start(out=t[:].rearrange("p (g k) -> p g k", g=2)[:, :, kw * s : kw * s + kw],
+                                  in_=W_v[:, 2 * h : 2 * h + 2, kw * s : kw * s + kw])
+            wr.append(t)
+
+        def b_mm(j):
+            S["bp", j] = psA.tile([P, 512], F32, tag="a", name="bp")
+            nc.tensor.matmul(S["bp", j][:], lhsT=ones_bf[:], rhs=b_row[:, 512 * j : 512 * j + 512], start=True, stop=True)
+
+        def b_cp(j):
+            nc.scalar.copy(out=w_bc[:, 512 * j : 512 * j + 512], in_=S["bp", j][:])
+
+        def b_sq(j):
+            sqt = junk.tile([P, 512], BF16, name="sqt")
+            nc.scalar.activation(out=sqt[:], in_=S["bp", j][:], func=ACT.Square, accum_out=b2p[:, j : j + 1])
+
+        def b_c1():
+            b2 = const.tile([P, 1], F32)
+            S["b2"] = b2
+            nc.vector.tensor_reduce(out=b2[:], in_=b2p[:], axis=AX.X, op=ALU.add)
+            zin = const.tile([P, 1], F32)
+            nc.vector.tensor_scalar(out=zin[:], in0=b2[:], scalar1=1e-15, scalar2=400.0, op0=ALU.max, op1=ALU.min)
+            z = const.tile([P, 1], F32)
+            S["z"] = z
+            nc.gpsimd.tensor_tensor(out=z[:], in0=zin[:], in1=expo2[:, 0:1], op=ALU.pow)
+
+        def b_c2():
+            z = S["z"]
+            eb = const.tile([P, 2], F32)
+            S["eb"] = eb
+            nc.scalar.activation(out=eb[:, 0:1], in_=z[:], func=ACT.Exp)
+            nc.scalar.activation(out=eb[:, 1:2], in_=z[:], func=ACT.Exp, scale=-1.0)
+
+        def b_c3():
+            z = S["z"]
+            eb = S["eb"]
+            b2 = S["b2"]
+            zm = const.tile([P, 1], F32)
+            nc.vector.tensor_scalar_max(zm[:], z[:], 1e-6)
+            rz = const.tile([P, 1], F32)
+            nc.vector.reciprocal(rz[:], zm[:])
+            zz = const.tile([P, 1], F32)
+            nc.vector.tensor_tensor(out=zz[:], in0=z[:], in1=z[:], op=ALU.mult)
+            y0 = const.tile([P, 1], F32)
+            nc.vector.tensor_scalar(out=y0[:], in0=zz[:], scalar1=1.0 / 6.0, scalar2=1.0, op0=ALU.mult, op1=ALU.add)
+            mk = const.tile([P, 1], F32)
+            nc.vector.tensor_scalar(out=mk[:], in0=z[:], scalar1=1e-6, scalar2=None, op0=ALU.is_lt)
+            shb = const.tile([P, 1], F32)
+            nc.vector.tensor_tensor(out=shb[:], in0=eb[:, 0:1], in1=eb[:, 1:2], op=ALU.subtract)
+            yb = const.tile([P, 1], F32)
+            nc.vector.scalar_tensor_tensor(out=yb[:], in0=shb[:], scalar=0.5, in1=rz[:], op0=ALU.mult, op1=ALU.mult)
+            df = const.tile([P, 1], F32)
+            nc.vector.tensor_tensor(out=df[:], in0=y0[:], in1=yb[:], op=ALU.subtract)
+            sc = const.tile([P, 1], F32)
+            nc.vector.scalar_tensor_tensor(out=sc[:], in0=df[:], scalar=mk[:], in1=yb[:], op0=ALU.mult, op1=ALU.add)
+            nc.vector.tensor_scalar(out=w_bc[:], in0=w_bc[:], scalar1=sc[:], scalar2=None, op0=ALU.mult)
+            q = const.tile([P, 1], F32)
+            nc.vector.tensor_tensor(out=q[:], in0=sc[:], in1=sc[:], op=ALU.mult)
+            hin = const.tile([P, 1], F32)
+            nc.vector.tensor_scalar(out=hin[:], in0=q[:], scalar1=b2[:], scalar2=1.0, op0=ALU.mult, op1=ALU.add)
+            hw = const.tile([P, 1], F32)
+            nc.gpsimd.tensor_tensor(out=hw[:], in0=hin[:], in1=expo2[:, 0:1], op=ALU.pow)
+            nc.vector.tensor_scalar_mul(hwh[:], hw[:], 0.5)
+
+        def xn(i):
+            a, l = divmod(i, 2)
+            if l == 0:
+                S["pin", a] = sm.tile([P, 3, 2], F32, name="pin")
+            xj = junk1.tile([P, K], F32, name="xj")
+            xs_ = xr[a][:, K * l : K * l + K]
+            nc.vector.scalar_tensor_tensor(out=xj[:], in0=xs_, scalar=1.0, in1=xs_, op0=ALU.mult, op1=ALU.mult,
+                                           accum_out=S["pin", a][:, 0, l : l + 1])
+
+        def xcA(a):
+            pin = S["pin", a]
+            nc.vector.tensor_scalar_add(pin[:, 1, :], pin[:, 0, :], 1.0)
+            nc.vector.tensor_scalar_max(pin[:, 2, :], pin[:, 0, :], 1e-12)
+            S["pw", a] = sm.tile([P, 3, 2], F32, name="pw")
+            nc.gpsimd.tensor_tensor(out=S["pw", a][:], in0=pin[:], in1=expo3[:], op=ALU.pow)
+
+        def xcB(a):
+            pw = S["pw", a]
+            sm2 = sm.tile([P, 2], F32, name="sm2")
+            S["sm2", a] = sm2
+            nc.vector.tensor_tensor(out=sm2[:], in0=pw[:, 0, :], in1=pw[:, 1, :], op=ALU.add)
+
+        def xcL(a):
+            S["ln", a] = sm.tile([P, 2], F32, name="ln2")
+            nc.scalar.activation(out=S["ln", a][:], in_=S["sm2", a][:], func=ACT.Ln)
+
+        def xcC(a):
+            S["coef", a] = sm.tile([P, 2], F32, name="coef")
+            nc.vector.tensor_tensor(out=S["coef", a][:], in0=S["ln", a][:], in1=S["pw", a][:, 2, :], op=ALU.mult)
+
+        def xs(i):
+            a, l = divmod(i, 2)
+            S["v", i] = vpool.tile([P, K], BF16, name="v")
+            nc.vector.tensor_scalar(out=S["v", i][:], in0=xr[a][:, K * l : K * l + K],
+                                    scalar1=S["coef", a][:, l : l + 1], scalar2=None, op0=ALU.mult)
+
+        def xt(i, half, even_pool):
+            vv = S["v", i][:].rearrange("p (c q t) -> p c q t", c=KP, q=P, t=4)
+            t = (psB if even_pool else psA).tile([P, 2, 4, P], BF16, tag="b" if even_pool else "a", name="xt")
+            S["xt", i, half] = t
+            for cl in range(2):
+                for tt in range(4):
+                    nc.tensor.matmul(t[:, cl, tt, :], lhsT=vv[:, 2 * half + cl, :, tt], rhs=ident_bf[:],
+                                     start=True, stop=True)
+
+        def xe(i, half, on_vector):
+            if half == 0:
+                S["xg", i] = xgp.tile([P, KP, P, 4], BF16, name="xg", align_bytes=64)
+            src = S["xt", i, half][:].rearrange("p c t r -> p c r t")
+            dst = S["xg", i][:, 2 * half : 2 * half + 2, :, :]
+            if on_vector:
+                nc.vector.tensor_copy(out=dst, in_=src)
+            else:
+                nc.scalar.copy(out=dst, in_=src)
+
+        def xq(i):
+            nc.vector.quantize_mx(out=vcodes[:, 512 * i : 512 * i + 512].bitcast(FP8X4),
+                                  scales=vscales[:, 512 * i : 512 * i + 512],
+                                  in_=S["xg", i][:].rearrange("p c r t -> p (c r t)"))
+
+        def wt(h, c):
+            w32 = wr[h][:].bitcast(F32)
+            t = psA.tile([P, 2, 2, P], F32, tag="a", name="wt")
+            S["wt", h, c] = t
+            for gl in range(2):
+                for u in range(2):
+                    col = 1024 * gl + 256 * c
+                    nc.tensor.transpose(t[:, gl, u, :], w32[:, col + u : col + 256 : 2], ident_f[:])
+
+        def we(h, c, on_vector):
+            S["wg", h, c] = wgp.tile([P, 1024], BF16, name="wg", align_bytes=64)
+            dst = S["wg", h, c][:].bitcast(F32).rearrange("p (g n u) -> p g n u", g=2, n=P, u=2)
+            src = S["wt", h, c][:].rearrange("p g u n -> p g n u")
+            if on_vector:
+                nc.vector.tensor_copy(out=dst, in_=src)
+            else:
+                nc.scalar.copy(out=dst, in_=src)
+
+        def wq(h, c):
+            col0 = ((h // 2) * KP + c) * 512 + 256 * (h % 2)
+            nc.vector.quantize_mx(out=wcodes[:, col0 : col0 + 256].bitcast(FP8X4),
+                                  scales=wscales[:, col0 : col0 + 256], in_=S["wg", h, c][:])
+
+        def mx(i, j):
+            acc = (psB if i % 2 == 0 else psA).tile([P, 512], F32, tag="b" if i % 2 == 0 else "a", name="acc")
+            S["acc", i, j] = acc
+            for c in range(KP):
+                lc = 512 * i + P * c
+                rc = (j * KP + c) * 512
+                nc.tensor.matmul_mx(out=acc[:], lhsT=vcodes[:, lc : lc + P].bitcast(FP8X4),
+                                    lhsT_scale=vscales[:, lc : lc + P],
+                                    rhs=wcodes[:, rc : rc + 512].bitcast(FP8X4),
+                                    rhs_scale=wscales[:, rc : rc + 512],
+                                    start=(c == 0), stop=(c == KP - 1))
+
+        def sq(i, j):
+            if j == 0:
+                S["s4", i] = sm.tile([P, NCH], F32, name="s4")
+            sqt = junk.tile([P, 512], BF16, name="sqt")
+            nc.scalar.activation(out=sqt[:], in_=S["acc", i, j][:], func=ACT.Square, accum_out=S["s4", i][:, j : j + 1])
+
+        def dot(i, j):
+            if j == 0:
+                S["d4", i] = sm.tile([P, NCH], F32, name="d4")
+            dj = junk.tile([P, 512], F32, name="dj")
+            nc.vector.scalar_tensor_tensor(out=dj[:], in0=S["acc", i, j][:], scalar=0.5, in1=w_bc[:, 512 * j : 512 * j + 512],
+                                           op0=ALU.mult, op1=ALU.mult, accum_out=S["d4", i][:, j : j + 1])
+
+        def e0(i):
+            S["s3", i] = sm.tile([P, 1], F32, name="s3")
+            j3 = sm.tile([P, 3], F32, name="j3")
+            nc.scalar.activation(out=j3[:], in_=S["s4", i][:, 0:3], func=ACT.Identity, accum_out=S["s3", i][:])
+
+        def e1(i):
+            pin = sm.tile([P, 2], F32, name="pin2")
+            nc.vector.tensor_scalar(out=pin[:, 0:1], in0=S["s4", i][:, 3:4], scalar1=S["s3", i][:], scalar2=400.0,
+                                    op0=ALU.add, op1=ALU.min)
+            nc.vector.tensor_scalar(out=pin[:, 1:2], in0=S["s4", i][:, 3:4], scalar1=S["s3", i][:], scalar2=1e-12,
+                                    op0=ALU.add, op1=ALU.max)
+            pw = sm.tile([P, 2], F32, name="pw2")
+            S["pw2", i] = pw
+            nc.gpsimd.tensor_tensor(out=pw[:], in0=pin[:], in1=expo2[:], op=ALU.pow)
+
+        def e2(i):
+            pw = S["pw2", i]
+            ee = sm.tile([P, 3], F32, name="ee")
+            S["ee", i] = ee
+            nc.scalar.activation(out=ee[:, 0:1], in_=pw[:, 0:1], func=ACT.Exp)
+            nc.scalar.activation(out=ee[:, 1:2], in_=pw[:, 0:1], func=ACT.Exp, scale=-1.0)
+            nc.scalar.activation(out=ee[:, 2:3], in_=pw[:, 0:1], func=ACT.Tanh, scale=0.5)
+
+        def ed(i):
+            S["d1", i] = sm.tile([P, 1], F32, name="d1")
+            j4 = sm.tile([P, NCH], F32, name="j4")
+            nc.scalar.activation(out=j4[:], in_=S["d4", i][:], func=ACT.Identity, accum_out=S["d1", i][:])
+
+        def e3(i):
+            pw = S["pw2", i]
+            ee = S["ee", i]
+            cy2 = sm.tile([P, 1], F32, name="cy2")
+            nc.vector.tensor_scalar(out=cy2[:], in0=ee[:, 0:1], scalar1=ee[:, 1:2], scalar2=pw[:, 1:2],
+                                    op0=ALU.subtract, op1=ALU.mult)
+            t1 = sm.tile([P, 1], F32, name="t1")
+            nc.vector.tensor_scalar(out=t1[:], in0=ee[:, 2:3], scalar1=pw[:, 1:2], scalar2=S["d1", i][:],
+                                    op0=ALU.mult, op1=ALU.mult)
+            aa = sm.tile([P, 1], F32, name="aa")
+            S["aa", i] = aa
+            nc.vector.scalar_tensor_tensor(out=aa[:], in0=t1[:], scalar=hwh[:], in1=cy2[:], op0=ALU.add, op1=ALU.mult)
+            S["o", i] = opool.tile([P, N], F32, name="o")
+
+        def fin(i, j, sg):
+            js = slice(512 * j, 512 * j + 512)
+            acc = S["acc", i, j]
+            o = S["o", i]
+            if sg:
+                ts = junk.tile([P, 512], F32, name="ts")
+                nc.scalar.activation(out=ts[:], in_=acc[:], func=ACT.Copy, scale=S["aa", i][:])
+                nc.gpsimd.tensor_tensor(out=o[:, js], in0=ts[:], in1=w_bc[:, js], op=ALU.add)
+            else:
+                nc.vector.scalar_tensor_tensor(out=o[:, js], in0=acc[:], scalar=S["aa", i][:], in1=w_bc[:, js],
+                                               op0=ALU.mult, op1=ALU.add)
+
+        def store(i, j0, j1):
+            hs = slice(512 * j0, 512 * j1)
+            nc.sync.dma_start(out=out_v[:, i, hs], in_=S["o", i][:, hs])
+
+        load_x(0)
+        load_w(0, 1)
+        load_w(1, 1)
+        load_w(2, 1)
+        load_x(1)
+        load_w(3, 1)
+        load_x(2)
+        load_w(4, 1)
+        load_x(3)
+        load_w(5, 1)
+        load_w(6, 1)
+        load_w(7, 1)
+
+        for j in range(NCH):
+            b_mm(j)
+        for j in range(NCH):
+            b_sq(j)
+        xn(0)
+        b_c1()
+        xn(1)
+        xcA(0)
+        for j in range(NCH):
+            b_cp(j)
+        b_c2()
+        nc.scalar.activation(out=warm2[:], in_=warm[:], func=ACT.Ln)
+        b_c3()
+
+        wbanks = [("w", h, c) for h in range(8) for c in range(KP)]
+        stream = wbanks[:W_FIRST]
+        rest = wbanks[W_FIRST:]
+        first_of = {}
+        for i in range(MT1):
+            first_of[i] = len(stream)
+            take = (len(rest) + (MT1 - i) - 1) // (MT1 - i)
+            stream.append(("x", i, 0))
+            stream.extend(rest[:1])
+            stream.append(("x", i, 1))
+            stream.extend(rest[1:take])
+            rest = rest[take:]
+        hooks = {}
+
+        def hook(pos, what, arg):
+            k = max(pos, 0)
+            hooks[k] = hooks.get(k, []) + [(what, arg)]
+
+        for q in range(4):
+            at = first_of[2 * q] if 2 * q < MT1 else LATE_AT[q]
+            if q > 0:
+                hook(at - LEAD[0], xn, 2 * q)
+                hook(at - LEAD[1], xn, 2 * q + 1)
+                hook(at - LEAD[1], xcA, q)
+            hook(at - LEAD[2], xcB, q)
+            hook(at - LEAD[3], xcL, q)
+            hook(at - LEAD[4], xcC, q)
+            hook(at - LEAD[4], xs, 2 * q)
+            hook(at - LEAD[5], xs, 2 * q + 1)
+        last_w = {}
+        for k in range(len(stream)):
+            if stream[k][0] == "w":
+                last_w[stream[k][1] // 2] = k
+        for j in range(3):
+            hook(max(last_w[j], first_of[0] + 2) + Q_LAG + 3, mx, j)
+
+        def quantise(bank):
+            if bank[0] == "w":
+                wq(bank[1], bank[2])
+            elif bank[2] == 1:
+                xq(bank[1])
+
+        for k in range(len(stream) + Q_LAG):
+            if k < len(stream):
+                bank = stream[k]
+                if bank[0] == "w":
+                    wt(bank[1], bank[2])
+                    we(bank[1], bank[2], (KP * bank[1] + bank[2]) % V_EVERY == V_EVERY - 1)
+                else:
+                    xt(bank[1], bank[2], False)
+                    xe(bank[1], bank[2], False)
+            if k >= Q_LAG:
+                quantise(stream[k - Q_LAG])
+            for what, arg in hooks.get(k, []):
+                if what == mx:
+                    mx(0, arg)
+                else:
+                    what(arg)
+        for j in range(3):
+            dot(0, j)
+        mx(0, 3)
+        for j in range(3):
+            sq(0, j)
+        e0(0)
+
+        for i in range(MT + 1):
+            p = i - 1
+            mid = 0 < i < MT
+            late = MT1 + p
+            fill = 0 <= p and late < MT
+            filled = 0 <= p - 1 and late - 1 < MT
+            if mid:
+                mx(i, 0)
+                sq(i, 0)
+            if p >= 0:
+                e2(p)
+                ed(p)
+            if filled:
+                xe(late - 1, 1, XE1_ON_V)
+            if mid:
+                dot(i, 0)
+            if p >= 0:
+                e3(p)
+                fin(p, 0, False)
+                fin(p, 1, False)
+            if mid:
+                mx(i, 1)
+                sq(i, 1)
+                dot(i, 1)
+            if filled:
+                xq(late - 1)
+            if mid:
+                mx(i, 2)
+                sq(i, 2)
+                e0(i)
+            if p >= 0:
+                fin(p, 2, p < MT - 1)
+                store(p, 0, 2)
+            if mid:
+                dot(i, 2)
+                mx(i, 3)
+            if i < MT:
+                sq(i, 3)
+                e1(i)
+            if p == MT - 1:
+                store(p, 2, 3)
+            if p >= 0:
+                fin(p, 3, True)
+                store(p, 2 if p < MT - 1 else 3, 4)
+            if i < MT:
+                dot(i, 3)
+            if fill:
+                xt(late, 0, p % 2 == 0)
+                xt(late, 1, p % 2 == 0)
+                xe(late, 0, False)

@@ -19,20 +19,15 @@ KP = K // 512
 NCH = N // 512
 FLOPS = 2 * M * K * N
 
-V_EVERY = 99
-W_FIRST = 11
-LEAD = (15, 13, 8, 6, 5, 4)
 Q_LAG = 2
 MT1 = 4
-LATE_AT = {2: 32, 3: 40}
-XE1_ON_V = False
 
 
 def tile_pvfc_kernel(tc, x, W, b, out):
     nc = tc.nc
     with ExitStack() as ctx:
         const = ctx.enter_context(tc.tile_pool(name="const", bufs=1))
-        xraw = ctx.enter_context(tc.tile_pool(name="xraw", bufs=4))
+        xraw = ctx.enter_context(tc.tile_pool(name="xraw", bufs=1))
         wraw = ctx.enter_context(tc.tile_pool(name="wraw", bufs=5))
         vpool = ctx.enter_context(tc.tile_pool(name="vpool", bufs=4))
         xgp = ctx.enter_context(tc.tile_pool(name="xgp", bufs=2))
@@ -45,22 +40,54 @@ def tile_pvfc_kernel(tc, x, W, b, out):
         psB = ctx.enter_context(tc.psum_pool(name="psB", bufs=4))
         ctx.enter_context(tc.manual_schedule())
 
+        x_v = x.rearrange("(p i) k -> p i k", i=MT)
+        W_v = W.rearrange("(g p) k -> p g k", p=P)
+        out_v = out.rearrange("(p i) n -> p i n", i=MT)
+        xr = {}
+        wr = {}
+        S = {}
+
+        def load_x(i, n):
+            t = xraw.tile([P, n * K], BF16, name="xr%d" % i)
+            nc.sync.dma_start(out=t[:].rearrange("p (l k) -> p l k", l=n), in_=x_v[:, i : i + n, :])
+            for l in range(n):
+                xr[i + l] = t[:, K * l : K * l + K]
+
+        def load_w(h, pieces):
+            t = wraw.tile([P, 2 * K], BF16, name="wr")
+            kw = K // pieces
+            for s in range(pieces):
+                nc.sync.dma_start(out=t[:].rearrange("p (g k) -> p g k", g=2)[:, :, kw * s : kw * s + kw],
+                                  in_=W_v[:, 2 * h : 2 * h + 2, kw * s : kw * s + kw])
+            wr[h] = t
+
         warm = const.tile([P, 1], F32)
         nc.vector.memset(warm[:], 1.0)
+        b_rows = const.tile([P, P], BF16)
+        nc.vector.memset(b_rows[:], 0.0)
+        nc.sync.dma_start(out=b_rows[0 : N // P, :], in_=b.rearrange("(c q) -> c q", q=P))
         warm2 = const.tile([P, 1], F32)
         nc.scalar.activation(out=warm2[:], in_=warm[:], func=ACT.Exp)
-        b_row = const.tile([P, N], BF16)
-        nc.vector.memset(b_row[:], 0.0)
-        nc.sync.dma_start(out=b_row[0:1, :], in_=b.unsqueeze(0))
-        ones_bf = const.tile([P, P], BF16)
-        nc.vector.memset(ones_bf[:], 1.0)
+        load_x(0, 1)
+        load_w(0, 2)
+        load_x(1, 1)
+        load_w(1, 1)
+        load_x(2, 2)
+        load_w(2, 1)
+        load_x(4, 2)
+        load_w(3, 1)
+        load_x(6, 2)
+        for h in range(4, 8):
+            load_w(h, 1)
         ident_f = const.tile([P, P], F32)
         make_identity(nc, ident_f[:])
         ident_bf = const.tile([P, P], BF16)
-        make_identity(nc, ident_bf[:])
-        expo3 = const.tile([P, 3, 2], F32)
-        nc.vector.memset(expo3[:, 0:2, :], 0.5)
-        nc.vector.memset(expo3[:, 2:3, :], -0.5)
+        nc.vector.tensor_copy(out=ident_bf[:], in_=ident_f[:])
+        ones_f = const.tile([P, P], F32)
+        nc.vector.memset(ones_f[:], 1.0)
+        expo3 = const.tile([P, 3], F32)
+        nc.vector.memset(expo3[:, 0:2], 0.5)
+        nc.vector.memset(expo3[:, 2:3], -0.5)
         expo2 = const.tile([P, 2], F32)
         nc.vector.memset(expo2[:, 0:1], 0.5)
         nc.vector.memset(expo2[:, 1:2], -0.5)
@@ -71,57 +98,39 @@ def tile_pvfc_kernel(tc, x, W, b, out):
         wscales = const.tile([P, NCH * KP * 512], U8, align_bytes=64)
         w_bc = const.tile([P, N], F32)
         hwh = const.tile([P, 1], F32)
-        b2p = const.tile([P, NCH], F32)
-
-        x_v = x.rearrange("(p i) k -> p i k", i=MT)
-        W_v = W.rearrange("(g p) k -> p g k", p=P)
-        out_v = out.rearrange("(p i) n -> p i n", i=MT)
-        xr = []
-        wr = []
-        S = {}
-
-        def load_x(a):
-            t = xraw.tile([P, 2 * K], BF16, name="xr")
-            nc.sync.dma_start(out=t[:].rearrange("p (l k) -> p l k", l=2), in_=x_v[:, 2 * a : 2 * a + 2, :])
-            xr.append(t)
-
-        def load_w(h, pieces):
-            t = wraw.tile([P, 2 * K], BF16, name="wr")
-            kw = K // pieces
-            for s in range(pieces):
-                nc.sync.dma_start(out=t[:].rearrange("p (g k) -> p g k", g=2)[:, :, kw * s : kw * s + kw],
-                                  in_=W_v[:, 2 * h : 2 * h + 2, kw * s : kw * s + kw])
-            wr.append(t)
 
         def b_mm(j):
-            S["bp", j] = psA.tile([P, 512], F32, tag="a", name="bp")
-            nc.tensor.matmul(S["bp", j][:], lhsT=ones_bf[:], rhs=b_row[:, 512 * j : 512 * j + 512], start=True, stop=True)
+            S["bp", j] = psB.tile([P, 4, P], F32, tag="b", name="bp")
+            for q in range(4):
+                c = 4 * j + q
+                nc.tensor.matmul(S["bp", j][:, q, :], lhsT=ident_bf[:, c : c + 1].to_broadcast([P, P]), rhs=b_rows[:],
+                                 start=True, stop=True)
 
         def b_cp(j):
-            nc.scalar.copy(out=w_bc[:, 512 * j : 512 * j + 512], in_=S["bp", j][:])
+            nc.scalar.activation(out=w_bc[:, 512 * j : 512 * j + 512], in_=S["bp", j][:].rearrange("p q n -> p (q n)"),
+                                 func=ACT.Copy, scale=S["scb"][:])
 
-        def b_sq(j):
-            sqt = junk.tile([P, 512], BF16, name="sqt")
-            nc.scalar.activation(out=sqt[:], in_=S["bp", j][:], func=ACT.Square, accum_out=b2p[:, j : j + 1])
-
-        def b_c1():
-            b2 = const.tile([P, 1], F32)
-            S["b2"] = b2
-            nc.vector.tensor_reduce(out=b2[:], in_=b2p[:], axis=AX.X, op=ALU.add)
+        def b_a():
+            b2p = const.tile([P, 1], F32)
+            bj = const.tile([P, P], F32)
+            nc.vector.scalar_tensor_tensor(out=bj[:], in0=b_rows[:], scalar=1.0, in1=b_rows[:], op0=ALU.mult, op1=ALU.mult,
+                                           accum_out=b2p[:])
+            b2 = psA.tile([P, 1], F32, tag="a", name="b2")
+            nc.tensor.matmul(b2[:], lhsT=ones_f[:], rhs=b2p[:], start=True, stop=True)
             zin = const.tile([P, 1], F32)
+            b2s = const.tile([P, 1], F32)
+            S["b2"] = b2s
             nc.vector.tensor_scalar(out=zin[:], in0=b2[:], scalar1=1e-15, scalar2=400.0, op0=ALU.max, op1=ALU.min)
+            nc.vector.tensor_copy(out=b2s[:], in_=b2[:])
             z = const.tile([P, 1], F32)
             S["z"] = z
             nc.gpsimd.tensor_tensor(out=z[:], in0=zin[:], in1=expo2[:, 0:1], op=ALU.pow)
-
-        def b_c2():
-            z = S["z"]
             eb = const.tile([P, 2], F32)
             S["eb"] = eb
             nc.scalar.activation(out=eb[:, 0:1], in_=z[:], func=ACT.Exp)
             nc.scalar.activation(out=eb[:, 1:2], in_=z[:], func=ACT.Exp, scale=-1.0)
 
-        def b_c3():
+        def b_b():
             z = S["z"]
             eb = S["eb"]
             b2 = S["b2"]
@@ -142,66 +151,60 @@ def tile_pvfc_kernel(tc, x, W, b, out):
             df = const.tile([P, 1], F32)
             nc.vector.tensor_tensor(out=df[:], in0=y0[:], in1=yb[:], op=ALU.subtract)
             sc = const.tile([P, 1], F32)
+            S["scb"] = sc
             nc.vector.scalar_tensor_tensor(out=sc[:], in0=df[:], scalar=mk[:], in1=yb[:], op0=ALU.mult, op1=ALU.add)
-            nc.vector.tensor_scalar(out=w_bc[:], in0=w_bc[:], scalar1=sc[:], scalar2=None, op0=ALU.mult)
             q = const.tile([P, 1], F32)
             nc.vector.tensor_tensor(out=q[:], in0=sc[:], in1=sc[:], op=ALU.mult)
             hin = const.tile([P, 1], F32)
             nc.vector.tensor_scalar(out=hin[:], in0=q[:], scalar1=b2[:], scalar2=1.0, op0=ALU.mult, op1=ALU.add)
             hw = const.tile([P, 1], F32)
             nc.gpsimd.tensor_tensor(out=hw[:], in0=hin[:], in1=expo2[:, 0:1], op=ALU.pow)
-            nc.vector.tensor_scalar_mul(hwh[:], hw[:], 0.5)
+            S["hw"] = hw
 
-        def xn(i):
-            a, l = divmod(i, 2)
-            if l == 0:
-                S["pin", a] = sm.tile([P, 3, 2], F32, name="pin")
-            xj = junk1.tile([P, K], F32, name="xj")
-            xs_ = xr[a][:, K * l : K * l + K]
-            nc.vector.scalar_tensor_tensor(out=xj[:], in0=xs_, scalar=1.0, in1=xs_, op0=ALU.mult, op1=ALU.mult,
-                                           accum_out=S["pin", a][:, 0, l : l + 1])
+        def b_c():
+            nc.vector.tensor_scalar_mul(hwh[:], S["hw"][:], 0.5)
 
-        def xcA(a):
-            pin = S["pin", a]
-            nc.vector.tensor_scalar_add(pin[:, 1, :], pin[:, 0, :], 1.0)
-            nc.vector.tensor_scalar_max(pin[:, 2, :], pin[:, 0, :], 1e-12)
-            S["pw", a] = sm.tile([P, 3, 2], F32, name="pw")
-            nc.gpsimd.tensor_tensor(out=S["pw", a][:], in0=pin[:], in1=expo3[:], op=ALU.pow)
+        def xn(i, on_vector):
+            S["pin", i] = sm.tile([P, 3], F32, name="pin")
+            acc = S["pin", i][:, 0:1]
+            if on_vector:
+                xj = junk1.tile([P, K], F32, name="xj")
+                nc.vector.scalar_tensor_tensor(out=xj[:], in0=xr[i], scalar=1.0, in1=xr[i], op0=ALU.mult, op1=ALU.mult,
+                                               accum_out=acc)
+            else:
+                xk = junk1.tile([P, K], BF16, name="xk")
+                nc.scalar.activation(out=xk[:], in_=xr[i], func=ACT.Square, accum_out=acc)
 
-        def xcB(a):
-            pw = S["pw", a]
-            sm2 = sm.tile([P, 2], F32, name="sm2")
-            S["sm2", a] = sm2
-            nc.vector.tensor_tensor(out=sm2[:], in0=pw[:, 0, :], in1=pw[:, 1, :], op=ALU.add)
+        def xp(i):
+            pin = S["pin", i]
+            nc.gpsimd.tensor_scalar(out=pin[:, 1:2], in0=pin[:, 0:1], scalar1=1.0, scalar2=None, op0=ALU.add)
+            nc.gpsimd.tensor_scalar(out=pin[:, 2:3], in0=pin[:, 0:1], scalar1=1e-12, scalar2=None, op0=ALU.max)
+            S["pw", i] = sm.tile([P, 3], F32, name="pw", bufs=8)
+            nc.gpsimd.tensor_tensor(out=S["pw", i][:], in0=pin[:], in1=expo3[:], op=ALU.pow)
 
-        def xcL(a):
-            S["ln", a] = sm.tile([P, 2], F32, name="ln2")
-            nc.scalar.activation(out=S["ln", a][:], in_=S["sm2", a][:], func=ACT.Ln)
-
-        def xcC(a):
-            S["coef", a] = sm.tile([P, 2], F32, name="coef")
-            nc.vector.tensor_tensor(out=S["coef", a][:], in0=S["ln", a][:], in1=S["pw", a][:, 2, :], op=ALU.mult)
+        def xl(i):
+            S["ln", i] = sm.tile([P, 1], F32, name="ln", bufs=8)
+            nc.scalar.activation(out=S["ln", i][:], in_=S["pw", i][:, 0:1], func=ACT.Ln, bias=S["pw", i][:, 1:2])
 
         def xs(i):
-            a, l = divmod(i, 2)
             S["v", i] = vpool.tile([P, K], BF16, name="v")
-            nc.vector.tensor_scalar(out=S["v", i][:], in0=xr[a][:, K * l : K * l + K],
-                                    scalar1=S["coef", a][:, l : l + 1], scalar2=None, op0=ALU.mult)
+            nc.vector.tensor_scalar(out=S["v", i][:], in0=xr[i], scalar1=S["ln", i][:], scalar2=S["pw", i][:, 2:3],
+                                    op0=ALU.mult, op1=ALU.mult)
 
         def xt(i, half, even_pool):
-            vv = S["v", i][:].rearrange("p (c q t) -> p c q t", c=KP, q=P, t=4)
-            t = (psB if even_pool else psA).tile([P, 2, 4, P], BF16, tag="b" if even_pool else "a", name="xt")
+            v32 = S["v", i][:].bitcast(F32)
+            t = (psB if even_pool else psA).tile([P, 2, 2, P], F32, tag="b" if even_pool else "a", name="xt")
             S["xt", i, half] = t
             for cl in range(2):
-                for tt in range(4):
-                    nc.tensor.matmul(t[:, cl, tt, :], lhsT=vv[:, 2 * half + cl, :, tt], rhs=ident_bf[:],
-                                     start=True, stop=True)
+                for u in range(2):
+                    col = 256 * (2 * half + cl)
+                    nc.tensor.transpose(t[:, cl, u, :], v32[:, col + u : col + 256 : 2], ident_f[:])
 
         def xe(i, half, on_vector):
             if half == 0:
-                S["xg", i] = xgp.tile([P, KP, P, 4], BF16, name="xg", align_bytes=64)
-            src = S["xt", i, half][:].rearrange("p c t r -> p c r t")
-            dst = S["xg", i][:, 2 * half : 2 * half + 2, :, :]
+                S["xg", i] = xgp.tile([P, KP * P * 4], BF16, name="xg", align_bytes=64)
+            src = S["xt", i, half][:].rearrange("p c u r -> p c r u")
+            dst = S["xg", i][:, 1024 * half : 1024 * half + 1024].bitcast(F32).rearrange("p (c r u) -> p c r u", c=2, r=P, u=2)
             if on_vector:
                 nc.vector.tensor_copy(out=dst, in_=src)
             else:
@@ -209,8 +212,7 @@ def tile_pvfc_kernel(tc, x, W, b, out):
 
         def xq(i):
             nc.vector.quantize_mx(out=vcodes[:, 512 * i : 512 * i + 512].bitcast(FP8X4),
-                                  scales=vscales[:, 512 * i : 512 * i + 512],
-                                  in_=S["xg", i][:].rearrange("p c r t -> p (c r t)"))
+                                  scales=vscales[:, 512 * i : 512 * i + 512], in_=S["xg", i][:])
 
         def wt(h, c):
             w32 = wr[h][:].bitcast(F32)
@@ -318,98 +320,102 @@ def tile_pvfc_kernel(tc, x, W, b, out):
             hs = slice(512 * j0, 512 * j1)
             nc.sync.dma_start(out=out_v[:, i, hs], in_=S["o", i][:, hs])
 
-        load_x(0)
-        load_w(0, 1)
-        load_w(1, 1)
-        load_w(2, 1)
-        load_x(1)
-        load_w(3, 1)
-        load_x(2)
-        load_w(4, 1)
-        load_x(3)
-        load_w(5, 1)
-        load_w(6, 1)
-        load_w(7, 1)
-
+        b_a()
         for j in range(NCH):
             b_mm(j)
-        for j in range(NCH):
-            b_sq(j)
-        xn(0)
-        b_c1()
-        xn(1)
-        xcA(0)
+        b_b()
+        nc.scalar.activation(out=warm2[:], in_=warm[:], func=ACT.Ln)
+        xn(0, True)
+        xp(0)
+        b_c()
         for j in range(NCH):
             b_cp(j)
-        b_c2()
-        nc.scalar.activation(out=warm2[:], in_=warm[:], func=ACT.Ln)
-        b_c3()
 
-        wbanks = [("w", h, c) for h in range(8) for c in range(KP)]
-        stream = wbanks[:W_FIRST]
-        rest = wbanks[W_FIRST:]
-        first_of = {}
-        for i in range(MT1):
-            first_of[i] = len(stream)
-            take = (len(rest) + (MT1 - i) - 1) // (MT1 - i)
-            stream.append(("x", i, 0))
-            stream.extend(rest[:1])
-            stream.append(("x", i, 1))
-            stream.extend(rest[1:take])
-            rest = rest[take:]
+        pend = []
+
+        def flush(n):
+            while len(pend) > n:
+                f, args = pend.pop(0)
+                f(*args)
+
+        def wbank(h, c):
+            wt(h, c)
+            we(h, c, False)
+            pend.append((wq, (h, c)))
+            flush(Q_LAG)
+
         hooks = {}
 
-        def hook(pos, what, arg):
-            k = max(pos, 0)
-            hooks[k] = hooks.get(k, []) + [(what, arg)]
+        def hook(s, f, *args):
+            hooks.setdefault(s, []).append((f, args))
 
-        for q in range(4):
-            at = first_of[2 * q] if 2 * q < MT1 else LATE_AT[q]
-            if q > 0:
-                hook(at - LEAD[0], xn, 2 * q)
-                hook(at - LEAD[1], xn, 2 * q + 1)
-                hook(at - LEAD[1], xcA, q)
-            hook(at - LEAD[2], xcB, q)
-            hook(at - LEAD[3], xcL, q)
-            hook(at - LEAD[4], xcC, q)
-            hook(at - LEAD[4], xs, 2 * q)
-            hook(at - LEAD[5], xs, 2 * q + 1)
-        last_w = {}
-        for k in range(len(stream)):
-            if stream[k][0] == "w":
-                last_w[stream[k][1] // 2] = k
-        for j in range(3):
-            hook(max(last_w[j], first_of[0] + 2) + Q_LAG + 3, mx, j)
-
-        def quantise(bank):
-            if bank[0] == "w":
-                wq(bank[1], bank[2])
-            elif bank[2] == 1:
-                xq(bank[1])
-
-        for k in range(len(stream) + Q_LAG):
-            if k < len(stream):
-                bank = stream[k]
-                if bank[0] == "w":
-                    wt(bank[1], bank[2])
-                    we(bank[1], bank[2], (KP * bank[1] + bank[2]) % V_EVERY == V_EVERY - 1)
-                else:
-                    xt(bank[1], bank[2], False)
-                    xe(bank[1], bank[2], False)
-            if k >= Q_LAG:
-                quantise(stream[k - Q_LAG])
-            for what, arg in hooks.get(k, []):
-                if what == mx:
-                    mx(0, arg)
-                else:
-                    what(arg)
-        for j in range(3):
-            dot(0, j)
+        hook(1, xl, 0)
+        hook(2, xs, 0)
+        hook(5, xt, 0, 0, True)
+        hook(6, xt, 0, 1, True)
+        hook(6, xe, 0, 0, True)
+        hook(7, xe, 0, 1, True)
+        hook(9, xq, 0)
+        hook(2, xn, 1, False)
+        hook(3, xp, 1)
+        hook(6, xl, 1)
+        hook(8, xs, 1)
+        hook(11, xt, 1, 0, True)
+        hook(12, xt, 1, 1, True)
+        hook(12, xe, 1, 0, True)
+        hook(13, xe, 1, 1, True)
+        hook(15, xq, 1)
+        hook(6, xn, 2, True)
+        hook(7, xp, 2)
+        hook(10, xl, 2)
+        hook(12, xs, 2)
+        hook(16, xt, 2, 0, True)
+        hook(17, xt, 2, 1, True)
+        hook(17, xe, 2, 0, True)
+        hook(18, xe, 2, 1, True)
+        hook(20, xq, 2)
+        hook(7, xn, 3, False)
+        hook(8, xp, 3)
+        hook(11, xl, 3)
+        hook(13, xs, 3)
+        hook(21, xt, 3, 0, True)
+        hook(22, xt, 3, 1, True)
+        hook(22, xe, 3, 0, True)
+        hook(23, xe, 3, 1, True)
+        hook(25, xq, 3)
+        hook(11, xn, 4, True)
+        hook(12, xp, 4)
+        hook(15, xl, 4)
+        hook(12, xn, 5, False)
+        hook(13, xp, 5)
+        hook(16, xl, 5)
+        hook(16, xn, 6, True)
+        hook(17, xp, 6)
+        hook(20, xl, 6)
+        hook(17, xn, 7, False)
+        hook(18, xp, 7)
+        hook(21, xl, 7)
+        hook(24, mx, 0, 0)
+        hook(25, mx, 0, 1)
+        hook(27, mx, 0, 2)
+        hook(27, sq, 0, 0)
+        hook(28, dot, 0, 0)
+        hook(28, sq, 0, 1)
+        hook(29, dot, 0, 1)
+        hook(26, xs, 4)
+        for s in range(8 * KP + Q_LAG):
+            if s < 8 * KP:
+                wt(s // KP, s % KP)
+                we(s // KP, s % KP, False)
+            if s >= Q_LAG:
+                wq((s - Q_LAG) // KP, (s - Q_LAG) % KP)
+            for f, args in hooks.get(s, []):
+                f(*args)
+        nc.scalar.activation(out=warm2[:], in_=warm[:], func=ACT.Exp)
+        sq(0, 2)
+        dot(0, 2)
         mx(0, 3)
-        for j in range(3):
-            sq(0, j)
         e0(0)
-
         for i in range(MT + 1):
             p = i - 1
             mid = 0 < i < MT
@@ -423,7 +429,7 @@ def tile_pvfc_kernel(tc, x, W, b, out):
                 e2(p)
                 ed(p)
             if filled:
-                xe(late - 1, 1, XE1_ON_V)
+                xe(late - 1, 1, False)
             if mid:
                 dot(i, 0)
             if p >= 0:
@@ -445,6 +451,9 @@ def tile_pvfc_kernel(tc, x, W, b, out):
                 store(p, 0, 2)
             if mid:
                 dot(i, 2)
+            if fill and late + 1 < MT:
+                xs(late + 1)
+            if mid:
                 mx(i, 3)
             if i < MT:
                 sq(i, 3)

@@ -177,8 +177,8 @@ def tile_pvfc_kernel(tc, x, W, b, out):
 
         def xp(i):
             pin = S["pin", i]
-            nc.gpsimd.tensor_scalar(out=pin[:, 1:2], in0=pin[:, 0:1], scalar1=1.0, scalar2=None, op0=ALU.add)
-            nc.gpsimd.tensor_scalar(out=pin[:, 2:3], in0=pin[:, 0:1], scalar1=1e-12, scalar2=None, op0=ALU.max)
+            nc.vector.tensor_scalar_add(pin[:, 1:2], pin[:, 0:1], 1.0)
+            nc.vector.tensor_scalar_max(pin[:, 2:3], pin[:, 0:1], 1e-12)
             S["pw", i] = sm.tile([P, 3], F32, name="pw", bufs=8)
             nc.gpsimd.tensor_tensor(out=S["pw", i][:], in0=pin[:], in1=expo3[:], op=ALU.pow)
 
@@ -186,10 +186,13 @@ def tile_pvfc_kernel(tc, x, W, b, out):
             S["ln", i] = sm.tile([P, 1], F32, name="ln", bufs=8)
             nc.scalar.activation(out=S["ln", i][:], in_=S["pw", i][:, 0:1], func=ACT.Ln, bias=S["pw", i][:, 1:2])
 
+        def xc(i):
+            S["coef", i] = sm.tile([P, 1], F32, name="coef", bufs=8)
+            nc.vector.tensor_tensor(out=S["coef", i][:], in0=S["ln", i][:], in1=S["pw", i][:, 2:3], op=ALU.mult)
+
         def xs(i):
             S["v", i] = vpool.tile([P, K], BF16, name="v")
-            nc.vector.tensor_scalar(out=S["v", i][:], in0=xr[i], scalar1=S["ln", i][:], scalar2=S["pw", i][:, 2:3],
-                                    op0=ALU.mult, op1=ALU.mult)
+            nc.vector.tensor_scalar(out=S["v", i][:], in0=xr[i], scalar1=S["coef", i][:], scalar2=None, op0=ALU.mult)
 
         def xt(i, half, even_pool):
             v32 = S["v", i][:].bitcast(F32)
@@ -350,59 +353,67 @@ def tile_pvfc_kernel(tc, x, W, b, out):
             hooks.setdefault(s, []).append((f, args))
 
         hook(1, xl, 0)
+        hook(2, xc, 0)
         hook(2, xs, 0)
+        hook(2, xn, 1, False)
+        hook(3, xp, 1)
         hook(5, xt, 0, 0, True)
         hook(6, xt, 0, 1, True)
         hook(6, xe, 0, 0, True)
-        hook(7, xe, 0, 1, True)
-        hook(9, xq, 0)
-        hook(2, xn, 1, False)
-        hook(3, xp, 1)
         hook(6, xl, 1)
+        hook(6, xn, 2, True)
+        hook(7, xc, 1)
+        hook(7, xe, 0, 1, True)
+        hook(7, xp, 2)
+        hook(7, xn, 3, False)
         hook(8, xs, 1)
+        hook(8, xp, 3)
+        hook(9, xq, 0)
+        hook(10, xl, 2)
+        hook(11, xc, 2)
         hook(11, xt, 1, 0, True)
+        hook(11, xl, 3)
+        hook(11, xn, 4, True)
+        hook(12, xc, 3)
         hook(12, xt, 1, 1, True)
         hook(12, xe, 1, 0, True)
-        hook(13, xe, 1, 1, True)
-        hook(15, xq, 1)
-        hook(6, xn, 2, True)
-        hook(7, xp, 2)
-        hook(10, xl, 2)
         hook(12, xs, 2)
+        hook(12, xp, 4)
+        hook(12, xn, 5, False)
+        hook(13, xe, 1, 1, True)
+        hook(13, xs, 3)
+        hook(13, xp, 5)
+        hook(15, xq, 1)
+        hook(15, xl, 4)
+        hook(16, xc, 4)
         hook(16, xt, 2, 0, True)
+        hook(16, xl, 5)
+        hook(16, xn, 6, True)
+        hook(17, xc, 5)
         hook(17, xt, 2, 1, True)
         hook(17, xe, 2, 0, True)
+        hook(17, xp, 6)
+        hook(17, xn, 7, False)
         hook(18, xe, 2, 1, True)
+        hook(18, xp, 7)
         hook(20, xq, 2)
-        hook(7, xn, 3, False)
-        hook(8, xp, 3)
-        hook(11, xl, 3)
-        hook(13, xs, 3)
+        hook(20, xl, 6)
+        hook(21, xc, 6)
         hook(21, xt, 3, 0, True)
+        hook(21, xl, 7)
+        hook(22, xc, 7)
         hook(22, xt, 3, 1, True)
         hook(22, xe, 3, 0, True)
         hook(23, xe, 3, 1, True)
-        hook(25, xq, 3)
-        hook(11, xn, 4, True)
-        hook(12, xp, 4)
-        hook(15, xl, 4)
-        hook(12, xn, 5, False)
-        hook(13, xp, 5)
-        hook(16, xl, 5)
-        hook(16, xn, 6, True)
-        hook(17, xp, 6)
-        hook(20, xl, 6)
-        hook(17, xn, 7, False)
-        hook(18, xp, 7)
-        hook(21, xl, 7)
         hook(24, mx, 0, 0)
+        hook(25, xq, 3)
         hook(25, mx, 0, 1)
+        hook(26, xs, 4)
         hook(27, mx, 0, 2)
         hook(27, sq, 0, 0)
         hook(28, dot, 0, 0)
         hook(28, sq, 0, 1)
         hook(29, dot, 0, 1)
-        hook(26, xs, 4)
         for s in range(8 * KP + Q_LAG):
             if s < 8 * KP:
                 wt(s // KP, s % KP)

@@ -69,15 +69,11 @@ def tile_pvfc_kernel(tc, x, W, b, out):
         warm2 = const.tile([P, 1], F32)
         nc.scalar.activation(out=warm2[:], in_=warm[:], func=ACT.Exp)
         load_x(0, 1)
-        load_w(0, 2)
         load_x(1, 1)
-        load_w(1, 1)
-        load_x(2, 2)
-        load_w(2, 1)
-        load_x(4, 2)
-        load_w(3, 1)
-        load_x(6, 2)
-        for h in range(4, 8):
+        for i in (2, 4, 6):
+            load_x(i, 2)
+        load_w(0, 2)
+        for h in range(1, 8):
             load_w(h, 1)
         ident_f = const.tile([P, P], F32)
         make_identity(nc, ident_f[:])
@@ -91,6 +87,10 @@ def tile_pvfc_kernel(tc, x, W, b, out):
         expo2 = const.tile([P, 2], F32)
         nc.vector.memset(expo2[:, 0:1], 0.5)
         nc.vector.memset(expo2[:, 1:2], -0.5)
+        half = const.tile([P, 1], F32)
+        nc.vector.memset(half[:], 0.5)
+        minus1 = const.tile([P, 1], F32)
+        nc.vector.memset(minus1[:], -1.0)
 
         vcodes = const.tile([P, MT * 512], U32, align_bytes=64)
         vscales = const.tile([P, MT * 512], U8, align_bytes=64)
@@ -100,7 +100,7 @@ def tile_pvfc_kernel(tc, x, W, b, out):
         hwh = const.tile([P, 1], F32)
 
         def b_mm(j):
-            S["bp", j] = psB.tile([P, 4, P], F32, tag="b", name="bp")
+            S["bp", j] = psA.tile([P, 4, P], F32, tag="a", name="bp")
             for q in range(4):
                 c = 4 * j + q
                 nc.tensor.matmul(S["bp", j][:, q, :], lhsT=ident_bf[:, c : c + 1].to_broadcast([P, P]), rhs=b_rows[:],
@@ -110,63 +110,50 @@ def tile_pvfc_kernel(tc, x, W, b, out):
             nc.scalar.activation(out=w_bc[:, 512 * j : 512 * j + 512], in_=S["bp", j][:].rearrange("p q n -> p (q n)"),
                                  func=ACT.Copy, scale=S["scb"][:])
 
-        def b_a():
-            b2p = const.tile([P, 1], F32)
+        def col(name):
+            S[name] = const.tile([P, 1], F32, name=name)
+            return S[name][:]
+
+        def b_norm():
+            b2p = col("b2p")
             bj = const.tile([P, P], F32)
-            nc.vector.scalar_tensor_tensor(out=bj[:], in0=b_rows[:], scalar=1.0, in1=b_rows[:], op0=ALU.mult, op1=ALU.mult,
-                                           accum_out=b2p[:])
-            b2 = psA.tile([P, 1], F32, tag="a", name="b2")
-            nc.tensor.matmul(b2[:], lhsT=ones_f[:], rhs=b2p[:], start=True, stop=True)
-            zin = const.tile([P, 1], F32)
-            b2s = const.tile([P, 1], F32)
-            S["b2"] = b2s
-            nc.vector.tensor_scalar(out=zin[:], in0=b2[:], scalar1=1e-15, scalar2=400.0, op0=ALU.max, op1=ALU.min)
-            nc.vector.tensor_copy(out=b2s[:], in_=b2[:])
-            z = const.tile([P, 1], F32)
-            S["z"] = z
-            nc.gpsimd.tensor_tensor(out=z[:], in0=zin[:], in1=expo2[:, 0:1], op=ALU.pow)
-            eb = const.tile([P, 2], F32)
-            S["eb"] = eb
-            nc.scalar.activation(out=eb[:, 0:1], in_=z[:], func=ACT.Exp)
-            nc.scalar.activation(out=eb[:, 1:2], in_=z[:], func=ACT.Exp, scale=-1.0)
+            nc.scalar.activation(out=bj[:], in_=b_rows[:], func=ACT.Square, accum_out=b2p)
+            b2_ps = psA.tile([P, 1], F32, tag="a", name="b2_ps")
+            nc.tensor.matmul(b2_ps[:], lhsT=ones_f[:], rhs=b2p, start=True, stop=True)
+            nc.scalar.copy(out=col("b2"), in_=b2_ps[:])
+            nc.gpsimd.tensor_scalar(out=col("zin"), in0=S["b2"][:], scalar1=1e-15, scalar2=400.0, op0=ALU.max, op1=ALU.min)
+            nc.gpsimd.tensor_tensor(out=col("z"), in0=S["zin"][:], in1=half[:, 0:1], op=ALU.pow)
 
-        def b_b():
-            z = S["z"]
-            eb = S["eb"]
-            b2 = S["b2"]
-            zm = const.tile([P, 1], F32)
-            nc.vector.tensor_scalar_max(zm[:], z[:], 1e-6)
-            rz = const.tile([P, 1], F32)
-            nc.vector.reciprocal(rz[:], zm[:])
-            zz = const.tile([P, 1], F32)
-            nc.vector.tensor_tensor(out=zz[:], in0=z[:], in1=z[:], op=ALU.mult)
-            y0 = const.tile([P, 1], F32)
-            nc.vector.tensor_scalar(out=y0[:], in0=zz[:], scalar1=1.0 / 6.0, scalar2=1.0, op0=ALU.mult, op1=ALU.add)
-            mk = const.tile([P, 1], F32)
-            nc.vector.tensor_scalar(out=mk[:], in0=z[:], scalar1=1e-6, scalar2=None, op0=ALU.is_lt)
-            shb = const.tile([P, 1], F32)
-            nc.vector.tensor_tensor(out=shb[:], in0=eb[:, 0:1], in1=eb[:, 1:2], op=ALU.subtract)
-            yb = const.tile([P, 1], F32)
-            nc.vector.scalar_tensor_tensor(out=yb[:], in0=shb[:], scalar=0.5, in1=rz[:], op0=ALU.mult, op1=ALU.mult)
-            df = const.tile([P, 1], F32)
-            nc.vector.tensor_tensor(out=df[:], in0=y0[:], in1=yb[:], op=ALU.subtract)
-            sc = const.tile([P, 1], F32)
-            S["scb"] = sc
-            nc.vector.scalar_tensor_tensor(out=sc[:], in0=df[:], scalar=mk[:], in1=yb[:], op0=ALU.mult, op1=ALU.add)
-            q = const.tile([P, 1], F32)
-            nc.vector.tensor_tensor(out=q[:], in0=sc[:], in1=sc[:], op=ALU.mult)
-            hin = const.tile([P, 1], F32)
-            nc.vector.tensor_scalar(out=hin[:], in0=q[:], scalar1=b2[:], scalar2=1.0, op0=ALU.mult, op1=ALU.add)
-            hw = const.tile([P, 1], F32)
-            nc.gpsimd.tensor_tensor(out=hw[:], in0=hin[:], in1=expo2[:, 0:1], op=ALU.pow)
-            S["hw"] = hw
+        def b_exp():
+            nc.scalar.activation(out=col("ep"), in_=S["z"][:], func=ACT.Exp)
+            nc.scalar.activation(out=col("em"), in_=S["z"][:], func=ACT.Exp, scale=-1.0)
 
-        def b_c():
-            nc.vector.tensor_scalar_mul(hwh[:], S["hw"][:], 0.5)
+        def b_scale():
+            nc.gpsimd.tensor_scalar(out=col("zm"), in0=S["z"][:], scalar1=1e-6, scalar2=None, op0=ALU.max)
+            nc.gpsimd.tensor_tensor(out=col("rz"), in0=S["zm"][:], in1=minus1[:], op=ALU.pow)
+            nc.gpsimd.tensor_scalar(out=col("y0"), in0=S["zin"][:], scalar1=1.0 / 6.0, scalar2=1.0, op0=ALU.mult, op1=ALU.add)
+            nc.gpsimd.tensor_scalar(out=col("mk"), in0=S["z"][:], scalar1=1e-6, scalar2=None, op0=ALU.is_lt)
+            nc.gpsimd.tensor_tensor(out=col("sh"), in0=S["ep"][:], in1=S["em"][:], op=ALU.subtract)
+            nc.gpsimd.tensor_scalar(out=col("yb"), in0=S["sh"][:], scalar1=S["rz"][:], scalar2=0.5, op0=ALU.mult, op1=ALU.mult)
+            nc.gpsimd.tensor_tensor(out=col("df"), in0=S["y0"][:], in1=S["yb"][:], op=ALU.subtract)
+            nc.gpsimd.tensor_scalar(out=col("scb"), in0=S["df"][:], scalar1=S["mk"][:], scalar2=S["yb"][:], op0=ALU.mult, op1=ALU.add)
+
+        def b_half():
+            nc.gpsimd.tensor_scalar(out=col("hq"), in0=S["scb"][:], scalar1=S["scb"][:], scalar2=S["b2"][:], op0=ALU.mult, op1=ALU.mult)
+            nc.gpsimd.tensor_scalar(out=col("hin"), in0=S["hq"][:], scalar1=1.0, scalar2=None, op0=ALU.add)
+            nc.gpsimd.tensor_tensor(out=col("hw"), in0=S["hin"][:], in1=half[:, 0:1], op=ALU.pow)
+            nc.gpsimd.tensor_scalar(out=hwh[:], in0=S["hw"][:], scalar1=0.5, scalar2=None, op0=ALU.mult)
+
+        pin = const.tile([P, MT, 3], F32)
+        pw = const.tile([P, MT, 3], F32)
+        expo = const.tile([P, MT, 3], F32)
+        nc.vector.memset(expo[:], 0.5)
+        nc.vector.memset(expo[:, :, 2:3], -0.5)
+        ln = const.tile([P, MT, 1], F32)
+        coef = const.tile([P, MT, 1], F32)
 
         def xn(i, on_vector):
-            S["pin", i] = sm.tile([P, 3], F32, name="pin")
-            acc = S["pin", i][:, 0:1]
+            acc = pin[:, i, 0:1]
             if on_vector:
                 xj = junk1.tile([P, K], F32, name="xj")
                 nc.vector.scalar_tensor_tensor(out=xj[:], in0=xr[i], scalar=1.0, in1=xr[i], op0=ALU.mult, op1=ALU.mult,
@@ -175,24 +162,20 @@ def tile_pvfc_kernel(tc, x, W, b, out):
                 xk = junk1.tile([P, K], BF16, name="xk")
                 nc.scalar.activation(out=xk[:], in_=xr[i], func=ACT.Square, accum_out=acc)
 
-        def xp(i):
-            pin = S["pin", i]
-            nc.vector.tensor_scalar_add(pin[:, 1:2], pin[:, 0:1], 1.0)
-            nc.vector.tensor_scalar_max(pin[:, 2:3], pin[:, 0:1], 1e-12)
-            S["pw", i] = sm.tile([P, 3], F32, name="pw", bufs=8)
-            nc.gpsimd.tensor_tensor(out=S["pw", i][:], in0=pin[:], in1=expo3[:], op=ALU.pow)
+        def xp(a, b):
+            nc.vector.tensor_scalar_add(pin[:, a:b, 1:2], pin[:, a:b, 0:1], 1.0)
+            nc.vector.tensor_scalar_max(pin[:, a:b, 2:3], pin[:, a:b, 0:1], 1e-12)
+            nc.gpsimd.tensor_tensor(out=pw[:, a:b, :], in0=pin[:, a:b, :], in1=expo[:, a:b, :], op=ALU.pow)
 
         def xl(i):
-            S["ln", i] = sm.tile([P, 1], F32, name="ln", bufs=8)
-            nc.scalar.activation(out=S["ln", i][:], in_=S["pw", i][:, 0:1], func=ACT.Ln, bias=S["pw", i][:, 1:2])
+            nc.scalar.activation(out=ln[:, i, :], in_=pw[:, i, 0:1], func=ACT.Ln, bias=pw[:, i, 1:2])
 
-        def xc(i):
-            S["coef", i] = sm.tile([P, 1], F32, name="coef", bufs=8)
-            nc.vector.tensor_tensor(out=S["coef", i][:], in0=S["ln", i][:], in1=S["pw", i][:, 2:3], op=ALU.mult)
+        def xc(a, b):
+            nc.vector.tensor_tensor(out=coef[:, a:b, :], in0=ln[:, a:b, :], in1=pw[:, a:b, 2:3], op=ALU.mult)
 
         def xs(i):
             S["v", i] = vpool.tile([P, K], BF16, name="v")
-            nc.vector.tensor_scalar(out=S["v", i][:], in0=xr[i], scalar1=S["coef", i][:], scalar2=None, op0=ALU.mult)
+            nc.vector.tensor_scalar(out=S["v", i][:], in0=xr[i], scalar1=coef[:, i, :], scalar2=None, op0=ALU.mult)
 
         def xt(i, half, even_pool):
             v32 = S["v", i][:].bitcast(F32)
@@ -323,160 +306,104 @@ def tile_pvfc_kernel(tc, x, W, b, out):
             hs = slice(512 * j0, 512 * j1)
             nc.sync.dma_start(out=out_v[:, i, hs], in_=S["o", i][:, hs])
 
-        b_a()
-        for j in range(NCH):
-            b_mm(j)
-        b_b()
-        nc.scalar.activation(out=warm2[:], in_=warm[:], func=ACT.Ln)
+        b_norm()
         xn(0, True)
-        xp(0)
-        b_c()
-        for j in range(NCH):
-            b_cp(j)
-
-        pend = []
-
-        def flush(n):
-            while len(pend) > n:
-                f, args = pend.pop(0)
-                f(*args)
-
-        def wbank(h, c):
-            wt(h, c)
-            we(h, c, False)
-            pend.append((wq, (h, c)))
-            flush(Q_LAG)
+        xn(1, False)
+        b_exp()
+        nc.scalar.activation(out=warm2[:], in_=warm[:], func=ACT.Ln)
+        xn(2, True)
+        xp(0, 2)
+        xn(3, False)
+        xn(4, True)
+        xp(2, 4)
+        xn(5, False)
+        xl(0)
+        xl(1)
+        xc(0, 2)
+        xs(0)
+        xn(6, True)
+        xp(4, 6)
+        xn(7, False)
+        b_scale()
+        b_half()
 
         hooks = {}
 
         def hook(s, f, *args):
             hooks.setdefault(s, []).append((f, args))
 
-        hook(1, xl, 0)
-        hook(2, xc, 0)
-        hook(2, xs, 0)
-        hook(2, xn, 1, False)
-        hook(3, xp, 1)
-        hook(5, xt, 0, 0, True)
-        hook(6, xt, 0, 1, True)
-        hook(6, xe, 0, 0, True)
-        hook(6, xl, 1)
-        hook(6, xn, 2, True)
-        hook(7, xc, 1)
-        hook(7, xe, 0, 1, True)
-        hook(7, xp, 2)
-        hook(7, xn, 3, False)
-        hook(8, xs, 1)
-        hook(8, xp, 3)
-        hook(9, xq, 0)
-        hook(10, xl, 2)
-        hook(11, xc, 2)
-        hook(11, xt, 1, 0, True)
-        hook(11, xl, 3)
-        hook(11, xn, 4, True)
-        hook(12, xc, 3)
-        hook(12, xt, 1, 1, True)
-        hook(12, xe, 1, 0, True)
-        hook(12, xs, 2)
-        hook(12, xp, 4)
-        hook(12, xn, 5, False)
-        hook(13, xe, 1, 1, True)
-        hook(13, xs, 3)
-        hook(13, xp, 5)
-        hook(15, xq, 1)
-        hook(15, xl, 4)
-        hook(16, xc, 4)
-        hook(16, xt, 2, 0, True)
-        hook(16, xl, 5)
-        hook(16, xn, 6, True)
-        hook(17, xc, 5)
-        hook(17, xt, 2, 1, True)
-        hook(17, xe, 2, 0, True)
-        hook(17, xp, 6)
-        hook(17, xn, 7, False)
-        hook(18, xe, 2, 1, True)
-        hook(18, xp, 7)
-        hook(20, xq, 2)
-        hook(20, xl, 6)
-        hook(21, xc, 6)
-        hook(21, xt, 3, 0, True)
-        hook(21, xl, 7)
-        hook(22, xc, 7)
-        hook(22, xt, 3, 1, True)
-        hook(22, xe, 3, 0, True)
-        hook(23, xe, 3, 1, True)
-        hook(24, mx, 0, 0)
-        hook(25, xq, 3)
-        hook(25, mx, 0, 1)
-        hook(26, xs, 4)
-        hook(27, mx, 0, 2)
-        hook(27, sq, 0, 0)
-        hook(28, dot, 0, 0)
-        hook(28, sq, 0, 1)
-        hook(29, dot, 0, 1)
+        hook(0, xp, 6, 8)
+        for j in range(NCH):
+            hook(18 + j, b_mm, j)
+            hook(18 + j, b_cp, j)
+        hook(2, xl, 2)
+        hook(2, xl, 3)
+        hook(3, xc, 2, 4)
+        hook(5, xs, 1)
+        hook(11, xs, 2)
+        hook(5, xs, 3)
+        for i in range(MT1, MT):
+            hook(30, xl, i)
+        hook(31, xc, MT1, MT)
+        TURN = (0, 9, 16, 15)
+        for i in range(MT1):
+            a = TURN[i]
+            hook(a, xt, i, 0, True)
+            hook(a + 2, xt, i, 1, True)
+            hook(a + 1, xe, i, 0, True)
+            hook(a + 3, xe, i, 1, True)
+            hook(a + 5, xq, i)
+        for j in range(2):
+            hook(19, mx, 0, j)
+            hook(19, sq, 0, j)
+            hook(22, dot, 0, j)
+        hook(33, mx, 0, 2)
+        hook(33, xs, MT1)
         for s in range(8 * KP + Q_LAG):
             if s < 8 * KP:
                 wt(s // KP, s % KP)
-                we(s // KP, s % KP, False)
+                we(s // KP, s % KP, s % KP == KP - 1 and s > 22)
             if s >= Q_LAG:
                 wq((s - Q_LAG) // KP, (s - Q_LAG) % KP)
             for f, args in hooks.get(s, []):
                 f(*args)
         nc.scalar.activation(out=warm2[:], in_=warm[:], func=ACT.Exp)
-        sq(0, 2)
-        dot(0, 2)
         mx(0, 3)
-        e0(0)
         for i in range(MT + 1):
             p = i - 1
-            mid = 0 < i < MT
             late = MT1 + p
             fill = 0 <= p and late < MT
-            filled = 0 <= p - 1 and late - 1 < MT
-            if mid:
-                mx(i, 0)
-                sq(i, 0)
             if p >= 0:
                 e2(p)
                 ed(p)
-            if filled:
-                xe(late - 1, 1, False)
-            if mid:
-                dot(i, 0)
-            if p >= 0:
                 e3(p)
-                fin(p, 0, False)
-                fin(p, 1, False)
-            if mid:
-                mx(i, 1)
-                sq(i, 1)
-                dot(i, 1)
-            if filled:
-                xq(late - 1)
-            if mid:
-                mx(i, 2)
-                sq(i, 2)
-                e0(i)
-            if p >= 0:
-                fin(p, 2, p < MT - 1)
-                store(p, 0, 2)
-            if mid:
-                dot(i, 2)
-            if fill and late + 1 < MT:
-                xs(late + 1)
-            if mid:
-                mx(i, 3)
-            if i < MT:
-                sq(i, 3)
-                e1(i)
-            if p == MT - 1:
-                store(p, 2, 3)
-            if p >= 0:
-                fin(p, 3, True)
-                store(p, 2 if p < MT - 1 else 3, 4)
-            if i < MT:
-                dot(i, 3)
+            for j in range(NCH):
+                if p >= 0:
+                    fin(p, j, p < MT - 1 and j == NCH - 1)
+                    if j % 2 == 1 or p == MT - 1:
+                        store(p, j - 1 if p < MT - 1 else j, j + 1)
+                if fill and j < 2:
+                    xt(late, j, p % 2 == 0)
+                if i + 1 < MT and not fill:
+                    mx(i + 1, j)
+                if fill and j >= 2:
+                    mx(i + 1, j - 2)
+                    xe(late, j - 2, False)
+                if j == 1 and i < MT:
+                    sq(i, 2)
+                    sq(i, 3)
+                    e0(i)
+                    e1(i)
+                if j >= 2 and i < MT:
+                    dot(i, j)
             if fill:
-                xt(late, 0, p % 2 == 0)
-                xt(late, 1, p % 2 == 0)
-                xe(late, 0, False)
+                mx(i + 1, 2)
+                mx(i + 1, 3)
+                xq(late)
+            if p >= 0 and late + 1 < MT:
+                xs(late + 1)
+            if i + 1 < MT:
+                sq(i + 1, 0)
+                dot(i + 1, 0)
+                sq(i + 1, 1)
+                dot(i + 1, 1)

@@ -68,13 +68,9 @@ def tile_pvfc_kernel(tc, x, W, b, out):
         nc.sync.dma_start(out=b_rows[0 : N // P, :], in_=b.rearrange("(c q) -> c q", q=P))
         warm2 = const.tile([P, 1], F32)
         nc.scalar.activation(out=warm2[:], in_=warm[:], func=ACT.Exp)
-        load_x(0, 1)
-        load_x(1, 1)
-        for i in (2, 4, 6):
-            load_x(i, 2)
-        load_w(0, 2)
-        for h in range(1, 8):
-            load_w(h, 1)
+        for u in range(MT):
+            load_x(u, 1)
+            load_w(u, 2 if u == 0 else 1)
         ident_f = const.tile([P, P], F32)
         make_identity(nc, ident_f[:])
         ident_bf = const.tile([P, P], BF16)
@@ -120,8 +116,8 @@ def tile_pvfc_kernel(tc, x, W, b, out):
             nc.scalar.activation(out=bj[:], in_=b_rows[:], func=ACT.Square, accum_out=b2p)
             b2_ps = psA.tile([P, 1], F32, tag="a", name="b2_ps")
             nc.tensor.matmul(b2_ps[:], lhsT=ones_f[:], rhs=b2p, start=True, stop=True)
+            nc.vector.tensor_scalar(out=col("zin"), in0=b2_ps[:], scalar1=1e-15, scalar2=400.0, op0=ALU.max, op1=ALU.min)
             nc.scalar.copy(out=col("b2"), in_=b2_ps[:])
-            nc.gpsimd.tensor_scalar(out=col("zin"), in0=S["b2"][:], scalar1=1e-15, scalar2=400.0, op0=ALU.max, op1=ALU.min)
             nc.gpsimd.tensor_tensor(out=col("z"), in0=S["zin"][:], in1=half[:, 0:1], op=ALU.pow)
 
         def b_exp():
@@ -129,26 +125,26 @@ def tile_pvfc_kernel(tc, x, W, b, out):
             nc.scalar.activation(out=col("em"), in_=S["z"][:], func=ACT.Exp, scale=-1.0)
 
         def b_scale():
-            nc.gpsimd.tensor_scalar(out=col("zm"), in0=S["z"][:], scalar1=1e-6, scalar2=None, op0=ALU.max)
-            nc.gpsimd.tensor_tensor(out=col("rz"), in0=S["zm"][:], in1=minus1[:], op=ALU.pow)
-            nc.gpsimd.tensor_scalar(out=col("y0"), in0=S["zin"][:], scalar1=1.0 / 6.0, scalar2=1.0, op0=ALU.mult, op1=ALU.add)
-            nc.gpsimd.tensor_scalar(out=col("mk"), in0=S["z"][:], scalar1=1e-6, scalar2=None, op0=ALU.is_lt)
-            nc.gpsimd.tensor_tensor(out=col("sh"), in0=S["ep"][:], in1=S["em"][:], op=ALU.subtract)
-            nc.gpsimd.tensor_scalar(out=col("yb"), in0=S["sh"][:], scalar1=S["rz"][:], scalar2=0.5, op0=ALU.mult, op1=ALU.mult)
-            nc.gpsimd.tensor_tensor(out=col("df"), in0=S["y0"][:], in1=S["yb"][:], op=ALU.subtract)
-            nc.gpsimd.tensor_scalar(out=col("scb"), in0=S["df"][:], scalar1=S["mk"][:], scalar2=S["yb"][:], op0=ALU.mult, op1=ALU.add)
+            nc.vector.tensor_scalar_max(col("zm"), S["z"][:], 1e-6)
+            nc.vector.tensor_scalar(out=col("y0"), in0=S["zin"][:], scalar1=1.0 / 6.0, scalar2=1.0, op0=ALU.mult, op1=ALU.add)
+            nc.vector.tensor_scalar(out=col("mk"), in0=S["z"][:], scalar1=1e-6, scalar2=None, op0=ALU.is_lt)
+            nc.vector.reciprocal(col("rz"), S["zm"][:])
+            nc.vector.tensor_tensor(out=col("sh"), in0=S["ep"][:], in1=S["em"][:], op=ALU.subtract)
+            nc.vector.tensor_scalar(out=col("yb"), in0=S["sh"][:], scalar1=S["rz"][:], scalar2=0.5, op0=ALU.mult, op1=ALU.mult)
+            nc.vector.tensor_tensor(out=col("df"), in0=S["y0"][:], in1=S["yb"][:], op=ALU.subtract)
+            nc.vector.tensor_scalar(out=col("scb"), in0=S["df"][:], scalar1=S["mk"][:], scalar2=S["yb"][:], op0=ALU.mult, op1=ALU.add)
+            nc.vector.tensor_scalar(out=col("hq"), in0=S["scb"][:], scalar1=S["scb"][:], scalar2=S["b2"][:], op0=ALU.mult, op1=ALU.mult)
+            nc.vector.tensor_scalar_add(col("hin"), S["hq"][:], 1.0)
 
         def b_half():
-            nc.gpsimd.tensor_scalar(out=col("hq"), in0=S["scb"][:], scalar1=S["scb"][:], scalar2=S["b2"][:], op0=ALU.mult, op1=ALU.mult)
-            nc.gpsimd.tensor_scalar(out=col("hin"), in0=S["hq"][:], scalar1=1.0, scalar2=None, op0=ALU.add)
             nc.gpsimd.tensor_tensor(out=col("hw"), in0=S["hin"][:], in1=half[:, 0:1], op=ALU.pow)
-            nc.gpsimd.tensor_scalar(out=hwh[:], in0=S["hw"][:], scalar1=0.5, scalar2=None, op0=ALU.mult)
+            nc.vector.tensor_scalar_mul(hwh[:], S["hw"][:], 0.5)
 
-        pin = const.tile([P, MT, 3], F32)
-        pw = const.tile([P, MT, 3], F32)
-        expo = const.tile([P, MT, 3], F32)
+        pin = const.tile([P, MT, 2], F32)
+        pw = const.tile([P, MT, 2], F32)
+        expo = const.tile([P, MT, 2], F32)
         nc.vector.memset(expo[:], 0.5)
-        nc.vector.memset(expo[:, :, 2:3], -0.5)
+        rcp = const.tile([P, MT, 1], F32)
         ln = const.tile([P, MT, 1], F32)
         coef = const.tile([P, MT, 1], F32)
 
@@ -164,14 +160,15 @@ def tile_pvfc_kernel(tc, x, W, b, out):
 
         def xp(a, b):
             nc.vector.tensor_scalar_add(pin[:, a:b, 1:2], pin[:, a:b, 0:1], 1.0)
-            nc.vector.tensor_scalar_max(pin[:, a:b, 2:3], pin[:, a:b, 0:1], 1e-12)
             nc.gpsimd.tensor_tensor(out=pw[:, a:b, :], in0=pin[:, a:b, :], in1=expo[:, a:b, :], op=ALU.pow)
 
         def xl(i):
             nc.scalar.activation(out=ln[:, i, :], in_=pw[:, i, 0:1], func=ACT.Ln, bias=pw[:, i, 1:2])
 
         def xc(a, b):
-            nc.vector.tensor_tensor(out=coef[:, a:b, :], in0=ln[:, a:b, :], in1=pw[:, a:b, 2:3], op=ALU.mult)
+            nc.vector.tensor_scalar_max(rcp[:, a:b, :], pw[:, a:b, 0:1], 1e-6)
+            nc.vector.reciprocal(rcp[:, a:b, :], rcp[:, a:b, :])
+            nc.vector.tensor_tensor(out=coef[:, a:b, :], in0=ln[:, a:b, :], in1=rcp[:, a:b, :], op=ALU.mult)
 
         def xs(i):
             S["v", i] = vpool.tile([P, K], BF16, name="v")
@@ -307,68 +304,55 @@ def tile_pvfc_kernel(tc, x, W, b, out):
             nc.sync.dma_start(out=out_v[:, i, hs], in_=S["o", i][:, hs])
 
         b_norm()
-        xn(0, True)
-        xn(1, False)
-        b_exp()
-        nc.scalar.activation(out=warm2[:], in_=warm[:], func=ACT.Ln)
-        xn(2, True)
-        xp(0, 2)
-        xn(3, False)
-        xn(4, True)
-        xp(2, 4)
-        xn(5, False)
-        xl(0)
-        xl(1)
-        xc(0, 2)
-        xs(0)
-        xn(6, True)
-        xp(4, 6)
-        xn(7, False)
-        b_scale()
-        b_half()
-
         hooks = {}
 
         def hook(s, f, *args):
             hooks.setdefault(s, []).append((f, args))
 
-        hook(0, xp, 6, 8)
-        for j in range(NCH):
-            hook(18 + j, b_mm, j)
-            hook(18 + j, b_cp, j)
-        hook(2, xl, 2)
-        hook(2, xl, 3)
-        hook(3, xc, 2, 4)
-        hook(5, xs, 1)
-        hook(11, xs, 2)
-        hook(5, xs, 3)
-        for i in range(MT1, MT):
-            hook(30, xl, i)
-        hook(31, xc, MT1, MT)
-        TURN = (0, 9, 16, 15)
-        for i in range(MT1):
-            a = TURN[i]
-            hook(a, xt, i, 0, True)
-            hook(a + 2, xt, i, 1, True)
-            hook(a + 1, xe, i, 0, True)
-            hook(a + 3, xe, i, 1, True)
-            hook(a + 5, xq, i)
-        for j in range(2):
-            hook(19, mx, 0, j)
-            hook(19, sq, 0, j)
-            hook(22, dot, 0, j)
-        hook(33, mx, 0, 2)
-        hook(33, xs, MT1)
-        for s in range(8 * KP + Q_LAG):
-            if s < 8 * KP:
+        b_exp()
+        nc.scalar.activation(out=warm2[:], in_=warm[:], func=ACT.Ln)
+        xn(0, True)
+        b_scale()
+        for u in range(MT):
+            n = 4 * u - 1
+            if u > 0:
+                hook(n, xn, u, u % 2 == 0)
+            hook(n + 2, xp, u, u + 1)
+            hook(n + 6, xl, u)
+            hook(n + 7, xc, u, u + 1)
+            if u < MT1:
+                hook(n + 7, xs, u)
+                a = n + 13
+                hook(a, xt, u, 0, True)
+                hook(a + 1, xt, u, 1, True)
+                hook(a + 1, xe, u, 0, u % 2 == 1)
+                hook(a + 2, xe, u, 1, u % 2 == 1)
+                hook(a + 6, xq, u)
+        hook(30, xs, MT1)
+        hook(16, b_half)
+        for j in range(4):
+            hook(26 + j, b_mm, j)
+            hook(26 + j, b_cp, j)
+        for j in range(3):
+            m = 28 + 2 * j
+            hook(m, mx, 0, j)
+            if j < 2:
+                hook(m, sq, 0, j)
+                hook(m + 6, dot, 0, j)
+        for s in range(-1, 8 * KP + Q_LAG + 3):
+            if 0 <= s < 8 * KP:
                 wt(s // KP, s % KP)
-                we(s // KP, s % KP, s % KP == KP - 1 and s > 22)
-            if s >= Q_LAG:
+                we(s // KP, s % KP, s >= 13 and s % 8 == 7)
+            if Q_LAG <= s < 8 * KP + Q_LAG:
                 wq((s - Q_LAG) // KP, (s - Q_LAG) % KP)
             for f, args in hooks.get(s, []):
                 f(*args)
         nc.scalar.activation(out=warm2[:], in_=warm[:], func=ACT.Exp)
         mx(0, 3)
+
+        def on_gpsimd(p, j):
+            return p < MT - 1 and j >= 2
+
         for i in range(MT + 1):
             p = i - 1
             late = MT1 + p
@@ -379,9 +363,13 @@ def tile_pvfc_kernel(tc, x, W, b, out):
                 e3(p)
             for j in range(NCH):
                 if p >= 0:
-                    fin(p, j, p < MT - 1 and j == NCH - 1)
+                    fin(p, j, on_gpsimd(p, j))
                     if j % 2 == 1 or p == MT - 1:
                         store(p, j - 1 if p < MT - 1 else j, j + 1)
+                if j == 1 and 0 <= p - 1 and late - 1 < MT:
+                    xq(late - 1)
+                if j == 2 and p >= 0 and late + 1 < MT:
+                    xs(late + 1)
                 if fill and j < 2:
                     xt(late, j, p % 2 == 0)
                 if i + 1 < MT and not fill:
@@ -399,9 +387,6 @@ def tile_pvfc_kernel(tc, x, W, b, out):
             if fill:
                 mx(i + 1, 2)
                 mx(i + 1, 3)
-                xq(late)
-            if p >= 0 and late + 1 < MT:
-                xs(late + 1)
             if i + 1 < MT:
                 sq(i + 1, 0)
                 dot(i + 1, 0)

@@ -338,7 +338,7 @@ def tile_pvfc_kernel(tc, x, W, b, out):
             hook(m, mx, 0, j)
             if j < 2:
                 hook(m, sq, 0, j)
-                hook(m + 6, dot, 0, j)
+                hook(m + 5, dot, 0, j)
         for s in range(-1, 8 * KP + Q_LAG + 3):
             if 0 <= s < 8 * KP:
                 wt(s // KP, s % KP)
@@ -348,47 +348,61 @@ def tile_pvfc_kernel(tc, x, W, b, out):
             for f, args in hooks.get(s, []):
                 f(*args)
         nc.scalar.activation(out=warm2[:], in_=warm[:], func=ACT.Exp)
+        sq(0, 2)
+        dot(0, 2)
         mx(0, 3)
-
-        def on_gpsimd(p, j):
-            return p < MT - 1 and j >= 2
+        e0(0)
 
         for i in range(MT + 1):
             p = i - 1
+            mid = 0 < i < MT
             late = MT1 + p
             fill = 0 <= p and late < MT
+            filled = 0 <= p - 1 and late - 1 < MT
+            if mid:
+                mx(i, 0)
+                sq(i, 0)
             if p >= 0:
                 e2(p)
                 ed(p)
+            if filled:
+                xe(late - 1, 1, False)
+            if mid:
+                dot(i, 0)
+            if p >= 0:
                 e3(p)
-            for j in range(NCH):
-                if p >= 0:
-                    fin(p, j, on_gpsimd(p, j))
-                    if j % 2 == 1 or p == MT - 1:
-                        store(p, j - 1 if p < MT - 1 else j, j + 1)
-                if j == 1 and 0 <= p - 1 and late - 1 < MT:
-                    xq(late - 1)
-                if j == 2 and p >= 0 and late + 1 < MT:
-                    xs(late + 1)
-                if fill and j < 2:
-                    xt(late, j, p % 2 == 0)
-                if i + 1 < MT and not fill:
-                    mx(i + 1, j)
-                if fill and j >= 2:
-                    mx(i + 1, j - 2)
-                    xe(late, j - 2, False)
-                if j == 1 and i < MT:
-                    sq(i, 2)
-                    sq(i, 3)
-                    e0(i)
-                    e1(i)
-                if j >= 2 and i < MT:
-                    dot(i, j)
+                fin(p, 0, False)
+                fin(p, 1, False)
+            if mid:
+                mx(i, 1)
+                sq(i, 1)
+                dot(i, 1)
+            if filled:
+                xq(late - 1)
+            if mid:
+                mx(i, 2)
+                sq(i, 2)
+                e0(i)
+            if p >= 0:
+                fin(p, 2, p < MT - 1)
+                store(p, 0, 2)
+            if mid:
+                dot(i, 2)
+            if fill and late + 1 < MT:
+                xs(late + 1)
+            if mid:
+                mx(i, 3)
+            if i < MT:
+                sq(i, 3)
+                e1(i)
+            if p == MT - 1:
+                store(p, 2, 3)
+            if p >= 0:
+                fin(p, 3, True)
+                store(p, 2 if p < MT - 1 else 3, 4)
+            if i < MT:
+                dot(i, 3)
             if fill:
-                mx(i + 1, 2)
-                mx(i + 1, 3)
-            if i + 1 < MT:
-                sq(i + 1, 0)
-                dot(i + 1, 0)
-                sq(i + 1, 1)
-                dot(i + 1, 1)
+                xt(late, 0, p % 2 == 0)
+                xt(late, 1, p % 2 == 0)
+                xe(late, 0, False)

@@ -1,3 +1,4 @@
+import math
 from contextlib import ExitStack
 
 import concourse.mybir as mybir
@@ -17,10 +18,46 @@ M, K, N = 1024, 2048, 2048
 MT = M // P
 KP = K // 512
 NCH = N // 512
+NSLOT = 8 * KP
 FLOPS = 2 * M * K * N
 
 Q_LAG = 2
+X0 = 1
+XP = 3
+PAIR = 1
+LP = 2
+LL = 6
+LC = 7
+LS = 1
+LD = 4
+LT = 4
+LQ = 4
 MT1 = 4
+XE0 = False
+XE1 = True
+XS4 = 32
+B0 = 4
+BW = 28
+M00 = 32
+M01 = 32
+M02 = 32
+M10 = 50
+M11 = 50
+DS = 1
+DD = 2
+WV0 = 40
+WVM = 4
+WVR = 3
+EXPS = True
+EXB = 0
+TL = 1
+XL0 = False
+XL1 = False
+SG2 = True
+XSP = 1
+LV = True
+BBC = True
+LOADS = (("w", 0), ("x", 0), ("w", 1), ("x", 1), ("x", 2), ("w", 2), ("x", 3), ("w", 3), ("x", 4), ("w", 4), ("x", 5), ("x", 6), ("w", 5), ("x", 7), ("w", 6), ("w", 7))
 
 
 def tile_pvfc_kernel(tc, x, W, b, out):
@@ -30,14 +67,13 @@ def tile_pvfc_kernel(tc, x, W, b, out):
         xraw = ctx.enter_context(tc.tile_pool(name="xraw", bufs=1))
         wraw = ctx.enter_context(tc.tile_pool(name="wraw", bufs=5))
         vpool = ctx.enter_context(tc.tile_pool(name="vpool", bufs=4))
-        xgp = ctx.enter_context(tc.tile_pool(name="xgp", bufs=2))
+        xgp = ctx.enter_context(tc.tile_pool(name="xgp", bufs=3))
         wgp = ctx.enter_context(tc.tile_pool(name="wgp", bufs=6))
         junk = ctx.enter_context(tc.tile_pool(name="junk", bufs=2))
         junk1 = ctx.enter_context(tc.tile_pool(name="junk1", bufs=1))
         opool = ctx.enter_context(tc.tile_pool(name="opool", bufs=3))
         sm = ctx.enter_context(tc.tile_pool(name="sm", bufs=3))
-        psA = ctx.enter_context(tc.psum_pool(name="psA", bufs=4))
-        psB = ctx.enter_context(tc.psum_pool(name="psB", bufs=4))
+        psum = ctx.enter_context(tc.psum_pool(name="psum", bufs=1))
         ctx.enter_context(tc.manual_schedule())
 
         x_v = x.rearrange("(p i) k -> p i k", i=MT)
@@ -47,11 +83,22 @@ def tile_pvfc_kernel(tc, x, W, b, out):
         wr = {}
         S = {}
 
-        def load_x(i, n):
-            t = xraw.tile([P, n * K], BF16, name="xr%d" % i)
-            nc.sync.dma_start(out=t[:].rearrange("p (l k) -> p l k", l=n), in_=x_v[:, i : i + n, :])
-            for l in range(n):
-                xr[i + l] = t[:, K * l : K * l + K]
+        free_banks = list(range(8))
+        in_bank = {}
+
+        def bank(key, shape):
+            n = free_banks.pop(0)
+            in_bank[key] = n
+            S[key] = psum.tile(shape, F32, tag="bank%d" % n, name="bank%d" % n)
+            return S[key]
+
+        def release(key):
+            free_banks.append(in_bank[key])
+
+        def load_x(i):
+            t = xraw.tile([P, K], BF16, name="xr%d" % i)
+            nc.sync.dma_start(out=t[:], in_=x_v[:, i, :])
+            xr[i] = t[:]
 
         def load_w(h, pieces):
             t = wraw.tile([P, 2 * K], BF16, name="wr")
@@ -67,91 +114,91 @@ def tile_pvfc_kernel(tc, x, W, b, out):
         nc.vector.memset(b_rows[:], 0.0)
         nc.sync.dma_start(out=b_rows[0 : N // P, :], in_=b.rearrange("(c q) -> c q", q=P))
         warm2 = const.tile([P, 1], F32)
-        nc.scalar.activation(out=warm2[:], in_=warm[:], func=ACT.Exp)
-        for u in range(MT):
-            load_x(u, 1)
-            load_w(u, 2 if u == 0 else 1)
+        nc.scalar.activation(out=warm2[:], in_=warm[:], func=ACT.Exp if EXB else ACT.Ln)
+        for kind, i in LOADS:
+            if kind == "x":
+                load_x(i)
+            else:
+                load_w(i, 2 if i == 0 else 1)
+        if BBC:
+            b_bc = const.tile([P, N], BF16)
+            nc.sync.dma_start(out=b_bc[:], in_=b.partition_broadcast(P))
         ident_f = const.tile([P, P], F32)
         make_identity(nc, ident_f[:])
         ident_bf = const.tile([P, P], BF16)
         nc.vector.tensor_copy(out=ident_bf[:], in_=ident_f[:])
         ones_f = const.tile([P, P], F32)
         nc.vector.memset(ones_f[:], 1.0)
-        expo3 = const.tile([P, 3], F32)
-        nc.vector.memset(expo3[:, 0:2], 0.5)
-        nc.vector.memset(expo3[:, 2:3], -0.5)
         expo2 = const.tile([P, 2], F32)
         nc.vector.memset(expo2[:, 0:1], 0.5)
         nc.vector.memset(expo2[:, 1:2], -0.5)
-        half = const.tile([P, 1], F32)
-        nc.vector.memset(half[:], 0.5)
-        minus1 = const.tile([P, 1], F32)
-        nc.vector.memset(minus1[:], -1.0)
+        base2 = const.tile([P, 2], F32)
+        nc.vector.tensor_scalar(out=base2[:, 0:1], in0=warm[:], scalar1=math.e, scalar2=None, op0=ALU.mult)
+        nc.vector.tensor_scalar(out=base2[:, 1:2], in0=warm[:], scalar1=math.exp(-1.0), scalar2=None, op0=ALU.mult)
 
-        vcodes = const.tile([P, MT * 512], U32, align_bytes=64)
-        vscales = const.tile([P, MT * 512], U8, align_bytes=64)
-        wcodes = const.tile([P, NCH * KP * 512], U32, align_bytes=64)
-        wscales = const.tile([P, NCH * KP * 512], U8, align_bytes=64)
+        vcodes = const.tile([P, MT * 512], U32, align_bytes=256)
+        vscales = const.tile([P, MT * 512], U8, align_bytes=256)
+        wcodes = const.tile([P, NCH * KP * 512], U32, align_bytes=256)
+        wscales = const.tile([P, NCH * KP * 512], U8, align_bytes=256)
         w_bc = const.tile([P, N], F32)
         hwh = const.tile([P, 1], F32)
 
+        def col(name, n=1):
+            S[name] = const.tile([P, n], F32, name=name)
+            return S[name][:]
+
         def b_mm(j):
-            S["bp", j] = psA.tile([P, 4, P], F32, tag="a", name="bp")
+            bp = bank(("bp", j), [P, 4, P])
             for q in range(4):
                 c = 4 * j + q
-                nc.tensor.matmul(S["bp", j][:, q, :], lhsT=ident_bf[:, c : c + 1].to_broadcast([P, P]), rhs=b_rows[:],
+                nc.tensor.matmul(bp[:, q, :], lhsT=ident_bf[:, c : c + 1].to_broadcast([P, P]), rhs=b_rows[:],
                                  start=True, stop=True)
 
         def b_cp(j):
             nc.scalar.activation(out=w_bc[:, 512 * j : 512 * j + 512], in_=S["bp", j][:].rearrange("p q n -> p (q n)"),
                                  func=ACT.Copy, scale=S["scb"][:])
-
-        def col(name):
-            S[name] = const.tile([P, 1], F32, name=name)
-            return S[name][:]
+            release(("bp", j))
 
         def b_norm():
             b2p = col("b2p")
             bj = const.tile([P, P], F32)
             nc.scalar.activation(out=bj[:], in_=b_rows[:], func=ACT.Square, accum_out=b2p)
-            b2_ps = psA.tile([P, 1], F32, tag="a", name="b2_ps")
+            b2_ps = bank("b2_ps", [P, 1])
             nc.tensor.matmul(b2_ps[:], lhsT=ones_f[:], rhs=b2p, start=True, stop=True)
-            nc.vector.tensor_scalar(out=col("zin"), in0=b2_ps[:], scalar1=1e-15, scalar2=400.0, op0=ALU.max, op1=ALU.min)
-            nc.scalar.copy(out=col("b2"), in_=b2_ps[:])
-            nc.gpsimd.tensor_tensor(out=col("z"), in0=S["zin"][:], in1=half[:, 0:1], op=ALU.pow)
-
-        def b_exp():
-            nc.scalar.activation(out=col("ep"), in_=S["z"][:], func=ACT.Exp)
-            nc.scalar.activation(out=col("em"), in_=S["z"][:], func=ACT.Exp, scale=-1.0)
+            zin = col("zin", 2)
+            nc.vector.tensor_scalar(out=zin[:, 0:1], in0=b2_ps[:], scalar1=1e-15, scalar2=400.0, op0=ALU.max, op1=ALU.min)
+            nc.vector.tensor_scalar(out=zin[:, 1:2], in0=b2_ps[:], scalar1=1e-12, scalar2=400.0, op0=ALU.max, op1=ALU.min)
+            nc.vector.tensor_copy(out=col("b2"), in_=b2_ps[:])
+            release("b2_ps")
+            nc.gpsimd.tensor_tensor(out=col("z", 2), in0=zin, in1=expo2[:], op=ALU.pow)
+            nc.gpsimd.tensor_tensor(out=col("bee", 2), in0=base2[:], in1=S["z"][:, 0:1].to_broadcast([P, 2]), op=ALU.pow)
 
         def b_scale():
-            nc.vector.tensor_scalar_max(col("zm"), S["z"][:], 1e-6)
-            nc.vector.tensor_scalar(out=col("y0"), in0=S["zin"][:], scalar1=1.0 / 6.0, scalar2=1.0, op0=ALU.mult, op1=ALU.add)
-            nc.vector.tensor_scalar(out=col("mk"), in0=S["z"][:], scalar1=1e-6, scalar2=None, op0=ALU.is_lt)
-            nc.vector.reciprocal(col("rz"), S["zm"][:])
-            nc.vector.tensor_tensor(out=col("sh"), in0=S["ep"][:], in1=S["em"][:], op=ALU.subtract)
-            nc.vector.tensor_scalar(out=col("yb"), in0=S["sh"][:], scalar1=S["rz"][:], scalar2=0.5, op0=ALU.mult, op1=ALU.mult)
-            nc.vector.tensor_tensor(out=col("df"), in0=S["y0"][:], in1=S["yb"][:], op=ALU.subtract)
-            nc.vector.tensor_scalar(out=col("scb"), in0=S["df"][:], scalar1=S["mk"][:], scalar2=S["yb"][:], op0=ALU.mult, op1=ALU.add)
+            ee = S["bee"]
+            nc.vector.tensor_scalar(out=col("y0"), in0=S["zin"][:, 0:1], scalar1=1.0 / 6.0, scalar2=1.0, op0=ALU.mult, op1=ALU.add)
+            nc.vector.tensor_scalar(out=col("yb"), in0=ee[:, 0:1], scalar1=ee[:, 1:2], scalar2=S["z"][:, 1:2],
+                                    op0=ALU.subtract, op1=ALU.mult)
+            nc.vector.tensor_scalar(out=col("scb"), in0=S["yb"][:], scalar1=0.5, scalar2=S["y0"][:], op0=ALU.mult, op1=ALU.max)
             nc.vector.tensor_scalar(out=col("hq"), in0=S["scb"][:], scalar1=S["scb"][:], scalar2=S["b2"][:], op0=ALU.mult, op1=ALU.mult)
-            nc.vector.tensor_scalar_add(col("hin"), S["hq"][:], 1.0)
+            nc.vector.tensor_scalar(out=col("hin"), in0=S["hq"][:], scalar1=0.25, scalar2=0.25, op0=ALU.mult, op1=ALU.add)
+            nc.gpsimd.tensor_tensor(out=hwh[:], in0=S["hin"][:], in1=expo2[:, 0:1], op=ALU.pow)
 
-        def b_half():
-            nc.gpsimd.tensor_tensor(out=col("hw"), in0=S["hin"][:], in1=half[:, 0:1], op=ALU.pow)
-            nc.vector.tensor_scalar_mul(hwh[:], S["hw"][:], 0.5)
+        def b_w(j):
+            js = slice(1024 * j, 1024 * j + 1024)
+            nc.vector.tensor_scalar(out=w_bc[:, js], in0=b_bc[:, js], scalar1=S["scb"][:], scalar2=None, op0=ALU.mult)
 
-        pin = const.tile([P, MT, 2], F32)
-        pw = const.tile([P, MT, 2], F32)
-        expo = const.tile([P, MT, 2], F32)
+        pin = const.tile([P, MT, 3], F32)
+        pw = const.tile([P, MT, 3], F32)
+        expo = const.tile([P, MT, 3], F32)
         nc.vector.memset(expo[:], 0.5)
-        rcp = const.tile([P, MT, 1], F32)
+        nc.vector.memset(expo[:, :, 2:3], -0.5)
         ln = const.tile([P, MT, 1], F32)
         coef = const.tile([P, MT, 1], F32)
 
         def xn(i, on_vector):
             acc = pin[:, i, 0:1]
             if on_vector:
-                xj = junk1.tile([P, K], F32, name="xj")
+                xj = junk1.tile([P, K], BF16, name="xj")
                 nc.vector.scalar_tensor_tensor(out=xj[:], in0=xr[i], scalar=1.0, in1=xr[i], op0=ALU.mult, op1=ALU.mult,
                                                accum_out=acc)
             else:
@@ -160,28 +207,26 @@ def tile_pvfc_kernel(tc, x, W, b, out):
 
         def xp(a, b):
             nc.vector.tensor_scalar_add(pin[:, a:b, 1:2], pin[:, a:b, 0:1], 1.0)
+            nc.vector.tensor_scalar_max(pin[:, a:b, 2:3], pin[:, a:b, 0:1], 1e-12)
             nc.gpsimd.tensor_tensor(out=pw[:, a:b, :], in0=pin[:, a:b, :], in1=expo[:, a:b, :], op=ALU.pow)
 
         def xl(i):
             nc.scalar.activation(out=ln[:, i, :], in_=pw[:, i, 0:1], func=ACT.Ln, bias=pw[:, i, 1:2])
 
         def xc(a, b):
-            nc.vector.tensor_scalar_max(rcp[:, a:b, :], pw[:, a:b, 0:1], 1e-6)
-            nc.vector.reciprocal(rcp[:, a:b, :], rcp[:, a:b, :])
-            nc.vector.tensor_tensor(out=coef[:, a:b, :], in0=ln[:, a:b, :], in1=rcp[:, a:b, :], op=ALU.mult)
+            nc.vector.tensor_tensor(out=coef[:, a:b, :], in0=ln[:, a:b, :], in1=pw[:, a:b, 2:3], op=ALU.mult)
 
         def xs(i):
             S["v", i] = vpool.tile([P, K], BF16, name="v")
             nc.vector.tensor_scalar(out=S["v", i][:], in0=xr[i], scalar1=coef[:, i, :], scalar2=None, op0=ALU.mult)
 
-        def xt(i, half, even_pool):
+        def xt(i, half):
             v32 = S["v", i][:].bitcast(F32)
-            t = (psB if even_pool else psA).tile([P, 2, 2, P], F32, tag="b" if even_pool else "a", name="xt")
-            S["xt", i, half] = t
+            t = bank(("xt", i, half), [P, 2, 2, P])
             for cl in range(2):
                 for u in range(2):
-                    col = 256 * (2 * half + cl)
-                    nc.tensor.transpose(t[:, cl, u, :], v32[:, col + u : col + 256 : 2], ident_f[:])
+                    c0 = 256 * (2 * half + cl)
+                    nc.tensor.transpose(t[:, cl, u, :], v32[:, c0 + u : c0 + 256 : 2], ident_f[:])
 
         def xe(i, half, on_vector):
             if half == 0:
@@ -192,6 +237,7 @@ def tile_pvfc_kernel(tc, x, W, b, out):
                 nc.vector.tensor_copy(out=dst, in_=src)
             else:
                 nc.scalar.copy(out=dst, in_=src)
+            release(("xt", i, half))
 
         def xq(i):
             nc.vector.quantize_mx(out=vcodes[:, 512 * i : 512 * i + 512].bitcast(FP8X4),
@@ -199,12 +245,11 @@ def tile_pvfc_kernel(tc, x, W, b, out):
 
         def wt(h, c):
             w32 = wr[h][:].bitcast(F32)
-            t = psA.tile([P, 2, 2, P], F32, tag="a", name="wt")
-            S["wt", h, c] = t
+            t = bank(("wt", h, c), [P, 2, 2, P])
             for gl in range(2):
                 for u in range(2):
-                    col = 1024 * gl + 256 * c
-                    nc.tensor.transpose(t[:, gl, u, :], w32[:, col + u : col + 256 : 2], ident_f[:])
+                    c0 = 1024 * gl + 256 * c
+                    nc.tensor.transpose(t[:, gl, u, :], w32[:, c0 + u : c0 + 256 : 2], ident_f[:])
 
         def we(h, c, on_vector):
             S["wg", h, c] = wgp.tile([P, 1024], BF16, name="wg", align_bytes=64)
@@ -214,6 +259,7 @@ def tile_pvfc_kernel(tc, x, W, b, out):
                 nc.vector.tensor_copy(out=dst, in_=src)
             else:
                 nc.scalar.copy(out=dst, in_=src)
+            release(("wt", h, c))
 
         def wq(h, c):
             col0 = ((h // 2) * KP + c) * 512 + 256 * (h % 2)
@@ -221,8 +267,7 @@ def tile_pvfc_kernel(tc, x, W, b, out):
                                   scales=wscales[:, col0 : col0 + 256], in_=S["wg", h, c][:])
 
         def mx(i, j):
-            acc = (psB if i % 2 == 0 else psA).tile([P, 512], F32, tag="b" if i % 2 == 0 else "a", name="acc")
-            S["acc", i, j] = acc
+            acc = bank(("acc", i, j), [P, 512])
             for c in range(KP):
                 lc = 512 * i + P * c
                 rc = (j * KP + c) * 512
@@ -251,41 +296,60 @@ def tile_pvfc_kernel(tc, x, W, b, out):
             nc.scalar.activation(out=j3[:], in_=S["s4", i][:, 0:3], func=ACT.Identity, accum_out=S["s3", i][:])
 
         def e1(i):
-            pin = sm.tile([P, 2], F32, name="pin2")
-            nc.vector.tensor_scalar(out=pin[:, 0:1], in0=S["s4", i][:, 3:4], scalar1=S["s3", i][:], scalar2=400.0,
+            pin2 = sm.tile([P, 2], F32, name="pin2")
+            nc.vector.tensor_scalar(out=pin2[:, 0:1], in0=S["s4", i][:, 3:4], scalar1=S["s3", i][:], scalar2=400.0,
                                     op0=ALU.add, op1=ALU.min)
-            nc.vector.tensor_scalar(out=pin[:, 1:2], in0=S["s4", i][:, 3:4], scalar1=S["s3", i][:], scalar2=1e-12,
+            nc.vector.tensor_scalar(out=pin2[:, 1:2], in0=S["s4", i][:, 3:4], scalar1=S["s3", i][:], scalar2=1e-12,
                                     op0=ALU.add, op1=ALU.max)
-            pw = sm.tile([P, 2], F32, name="pw2")
-            S["pw2", i] = pw
-            nc.gpsimd.tensor_tensor(out=pw[:], in0=pin[:], in1=expo2[:], op=ALU.pow)
-
-        def e2(i):
-            pw = S["pw2", i]
+            pw2 = sm.tile([P, 2], F32, name="pw2")
+            S["pw2", i] = pw2
+            nc.gpsimd.tensor_tensor(out=pw2[:], in0=pin2[:], in1=expo2[:], op=ALU.pow)
             ee = sm.tile([P, 3], F32, name="ee")
             S["ee", i] = ee
-            nc.scalar.activation(out=ee[:, 0:1], in_=pw[:, 0:1], func=ACT.Exp)
-            nc.scalar.activation(out=ee[:, 1:2], in_=pw[:, 0:1], func=ACT.Exp, scale=-1.0)
-            nc.scalar.activation(out=ee[:, 2:3], in_=pw[:, 0:1], func=ACT.Tanh, scale=0.5)
+            if EXPS:
+                return
+            nc.gpsimd.tensor_tensor(out=ee[:, 0:2], in0=base2[:], in1=pw2[:, 0:1].to_broadcast([P, 2]), op=ALU.pow)
+
+        def e2(i):
+            pw2 = S["pw2", i]
+            ee = S["ee", i]
+            if not EXPS:
+                return
+            nc.scalar.activation(out=ee[:, 0:1], in_=pw2[:, 0:1], func=ACT.Exp)
+            nc.scalar.activation(out=ee[:, 1:2], in_=pw2[:, 0:1], func=ACT.Exp, scale=-1.0)
+            nc.scalar.activation(out=ee[:, 2:3], in_=pw2[:, 0:1], func=ACT.Tanh, scale=0.5)
 
         def ed(i):
             S["d1", i] = sm.tile([P, 1], F32, name="d1")
-            j4 = sm.tile([P, NCH], F32, name="j4")
-            nc.scalar.activation(out=j4[:], in_=S["d4", i][:], func=ACT.Identity, accum_out=S["d1", i][:])
+            nc.vector.reduce_sum(out=S["d1", i][:], in_=S["d4", i][:], axis=AX.X)
 
         def e3(i):
-            pw = S["pw2", i]
+            pw2 = S["pw2", i]
             ee = S["ee", i]
+            S["o", i] = opool.tile([P, N], F32, name="o")
+            if EXPS:
+                cy2 = sm.tile([P, 1], F32, name="cy2")
+                nc.vector.tensor_scalar(out=cy2[:], in0=ee[:, 0:1], scalar1=ee[:, 1:2], scalar2=pw2[:, 1:2],
+                                        op0=ALU.subtract, op1=ALU.mult)
+                t1 = sm.tile([P, 1], F32, name="t1")
+                nc.vector.tensor_scalar(out=t1[:], in0=ee[:, 2:3], scalar1=pw2[:, 1:2], scalar2=S["d1", i][:],
+                                        op0=ALU.mult, op1=ALU.mult)
+                aa = sm.tile([P, 1], F32, name="aa")
+                S["aa", i] = aa
+                nc.vector.scalar_tensor_tensor(out=aa[:], in0=t1[:], scalar=hwh[:], in1=cy2[:], op0=ALU.add, op1=ALU.mult)
+                return
+            qq = sm.tile([P, 1], F32, name="qq")
+            nc.vector.tensor_scalar(out=qq[:], in0=ee[:, 0:1], scalar1=ee[:, 1:2], scalar2=2.0, op0=ALU.add, op1=ALU.add)
             cy2 = sm.tile([P, 1], F32, name="cy2")
-            nc.vector.tensor_scalar(out=cy2[:], in0=ee[:, 0:1], scalar1=ee[:, 1:2], scalar2=pw[:, 1:2],
+            nc.vector.tensor_scalar(out=cy2[:], in0=ee[:, 0:1], scalar1=ee[:, 1:2], scalar2=pw2[:, 1:2],
                                     op0=ALU.subtract, op1=ALU.mult)
+            rq = sm.tile([P, 1], F32, name="rq")
+            nc.vector.reciprocal(rq[:], qq[:])
             t1 = sm.tile([P, 1], F32, name="t1")
-            nc.vector.tensor_scalar(out=t1[:], in0=ee[:, 2:3], scalar1=pw[:, 1:2], scalar2=S["d1", i][:],
-                                    op0=ALU.mult, op1=ALU.mult)
+            nc.vector.tensor_scalar(out=t1[:], in0=cy2[:], scalar1=rq[:], scalar2=S["d1", i][:], op0=ALU.mult, op1=ALU.mult)
             aa = sm.tile([P, 1], F32, name="aa")
             S["aa", i] = aa
             nc.vector.scalar_tensor_tensor(out=aa[:], in0=t1[:], scalar=hwh[:], in1=cy2[:], op0=ALU.add, op1=ALU.mult)
-            S["o", i] = opool.tile([P, N], F32, name="o")
 
         def fin(i, j, sg):
             js = slice(512 * j, 512 * j + 512)
@@ -298,61 +362,71 @@ def tile_pvfc_kernel(tc, x, W, b, out):
             else:
                 nc.vector.scalar_tensor_tensor(out=o[:, js], in0=acc[:], scalar=S["aa", i][:], in1=w_bc[:, js],
                                                op0=ALU.mult, op1=ALU.add)
+            release(("acc", i, j))
 
         def store(i, j0, j1):
             hs = slice(512 * j0, 512 * j1)
             nc.sync.dma_start(out=out_v[:, i, hs], in_=S["o", i][:, hs])
 
-        b_norm()
         hooks = {}
 
         def hook(s, f, *args):
             hooks.setdefault(s, []).append((f, args))
 
-        b_exp()
-        nc.scalar.activation(out=warm2[:], in_=warm[:], func=ACT.Ln)
-        xn(0, True)
-        b_scale()
+        b_norm()
+        hook(B0, b_scale)
+        pres = {}
+
+        def pre(s, f, *args):
+            pres.setdefault(s, []).append((f, args))
+
         for u in range(MT):
-            n = 4 * u - 1
-            if u > 0:
-                hook(n, xn, u, u % 2 == 0)
-            hook(n + 2, xp, u, u + 1)
-            hook(n + 6, xl, u)
-            hook(n + 7, xc, u, u + 1)
-            if u < MT1:
-                hook(n + 7, xs, u)
-                a = n + 13
-                hook(a, xt, u, 0, True)
-                hook(a + 1, xt, u, 1, True)
-                hook(a + 1, xe, u, 0, u % 2 == 1)
-                hook(a + 2, xe, u, 1, u % 2 == 1)
-                hook(a + 6, xq, u)
-        hook(30, xs, MT1)
-        hook(16, b_half)
-        for j in range(4):
-            hook(26 + j, b_mm, j)
-            hook(26 + j, b_cp, j)
-        for j in range(3):
-            m = 28 + 2 * j
-            hook(m, mx, 0, j)
-            if j < 2:
-                hook(m, sq, 0, j)
-                hook(m + 5, dot, 0, j)
-        for s in range(-1, 8 * KP + Q_LAG + 3):
-            if 0 <= s < 8 * KP:
+            hook(X0 + XP * u, xn, u, u % 2 == 0)
+        for g in range(0, MT, PAIR):
+            n = X0 + XP * (g + PAIR - 1)
+            pre(n + LP, xp, g, g + PAIR)
+            for u in range(g, g + PAIR):
+                hook(n + LL, xl, u)
+            hook(n + LC, xc, g, g + PAIR)
+            for u in range(g, min(g + PAIR, MT1)):
+                e = u - g
+                hook(n + LC + LS + LD * e, xs, u)
+                a = n + LC + LT + LD * e
+                hook(a, xt, u, 0)
+                hook(a + 1, xt, u, 1)
+                hook(a + 1, xe, u, 0, XE0)
+                hook(a + 2, xe, u, 1, XE1)
+                hook(a + 2 + LQ, xq, u)
+        hook(XS4, xs, MT1)
+        hook(BW, b_w, 0)
+        hook(BW + 2, b_w, 1)
+        early = []
+        for i, j, m in ((0, 0, M00), (0, 1, M01), (0, 2, M02), (1, 0, M10), (1, 1, M11)):
+            if m > 40:
+                continue
+            early.append((i, j))
+            hook(m, mx, i, j)
+            if i == 0 and j < 2:
+                hook(m + DS, sq, i, j)
+                hook(max(m + DD, BW + 3), dot, i, j)
+        last = max(list(hooks) + [NSLOT + Q_LAG - 1])
+        last = max(list(pres) + [last])
+        for s in range(min(list(hooks) + [0]), last + 1):
+            for f, args in pres.get(s, []):
+                f(*args)
+            if 0 <= s < NSLOT:
                 wt(s // KP, s % KP)
-                we(s // KP, s % KP, s >= 13 and s % 8 == 7)
-            if Q_LAG <= s < 8 * KP + Q_LAG:
+                we(s // KP, s % KP, s >= WV0 and s % WVM == WVR)
+            if Q_LAG <= s < NSLOT + Q_LAG:
                 wq((s - Q_LAG) // KP, (s - Q_LAG) % KP)
             for f, args in hooks.get(s, []):
                 f(*args)
-        nc.scalar.activation(out=warm2[:], in_=warm[:], func=ACT.Exp)
+        if EXPS and TL == 0:
+            nc.scalar.activation(out=warm2[:], in_=warm[:], func=ACT.Exp)
         sq(0, 2)
         dot(0, 2)
         mx(0, 3)
         e0(0)
-
         for i in range(MT + 1):
             p = i - 1
             mid = 0 < i < MT
@@ -360,21 +434,26 @@ def tile_pvfc_kernel(tc, x, W, b, out):
             fill = 0 <= p and late < MT
             filled = 0 <= p - 1 and late - 1 < MT
             if mid:
-                mx(i, 0)
+                if (i, 0) not in early:
+                    mx(i, 0)
                 sq(i, 0)
+            if p == 0 and EXPS and TL == 1:
+                nc.scalar.activation(out=warm2[:], in_=warm[:], func=ACT.Exp)
             if p >= 0:
                 e2(p)
                 ed(p)
             if filled:
-                xe(late - 1, 1, False)
+                xe(late - 1, 1, XL1)
             if mid:
                 dot(i, 0)
             if p >= 0:
                 e3(p)
-                fin(p, 0, False)
-                fin(p, 1, False)
+                if i < MT:
+                    fin(p, 0, False)
+                    fin(p, 1, False)
             if mid:
-                mx(i, 1)
+                if (i, 1) not in early:
+                    mx(i, 1)
                 sq(i, 1)
                 dot(i, 1)
             if filled:
@@ -383,26 +462,33 @@ def tile_pvfc_kernel(tc, x, W, b, out):
                 mx(i, 2)
                 sq(i, 2)
                 e0(i)
-            if p >= 0:
-                fin(p, 2, p < MT - 1)
+            if p >= 0 and i < MT:
+                fin(p, 2, SG2)
                 store(p, 0, 2)
             if mid:
                 dot(i, 2)
-            if fill and late + 1 < MT:
+            if fill and late + 1 < MT and XSP == 0:
                 xs(late + 1)
             if mid:
                 mx(i, 3)
             if i < MT:
                 sq(i, 3)
                 e1(i)
+            if p >= 0 and i < MT:
+                fin(p, 3, p < MT - 2 or not LV)
+                store(p, 2, 4)
             if p == MT - 1:
-                store(p, 2, 3)
-            if p >= 0:
-                fin(p, 3, True)
-                store(p, 2 if p < MT - 1 else 3, 4)
+                fin(p, 0, True)
+                for j in range(1, NCH):
+                    fin(p, j, False)
+                    store(p, j, j + 1)
+                    if j == 2:
+                        store(p, 0, 1)
             if i < MT:
                 dot(i, 3)
+            if fill and late + 1 < MT and XSP == 1:
+                xs(late + 1)
             if fill:
-                xt(late, 0, p % 2 == 0)
-                xt(late, 1, p % 2 == 0)
-                xe(late, 0, False)
+                xt(late, 0)
+                xt(late, 1)
+                xe(late, 0, XL0)

@@ -57,7 +57,14 @@ SG2 = True
 XSP = 1
 LV = True
 BBC = True
-LOADS = (("w", 0), ("x", 0), ("w", 1), ("x", 1), ("x", 2), ("w", 2), ("x", 3), ("w", 3), ("x", 4), ("w", 4), ("x", 5), ("x", 6), ("w", 5), ("x", 7), ("w", 6), ("w", 7))
+NX0 = 0
+NX1 = 8
+LOADS = (("p", 0), ("b", 0), ("x", 0), ("p", 1), ("w", 1), ("x", 1), ("x", 2), ("w", 2), ("x", 3), ("w", 3), ("x", 4), ("w", 4), ("x", 5), ("x", 6), ("w", 5), ("x", 7), ("w", 6), ("w", 7))
+W0P = 2
+TAIL = True
+TS2 = True
+FH = 1
+DF = True
 
 
 def tile_pvfc_kernel(tc, x, W, b, out):
@@ -100,26 +107,30 @@ def tile_pvfc_kernel(tc, x, W, b, out):
             nc.sync.dma_start(out=t[:], in_=x_v[:, i, :])
             xr[i] = t[:]
 
-        def load_w(h, pieces):
-            t = wraw.tile([P, 2 * K], BF16, name="wr")
+        def load_w(h, s, pieces):
+            if s == 0:
+                wr[h] = wraw.tile([P, 2 * K], BF16, name="wr")
+            t = wr[h]
             kw = K // pieces
-            for s in range(pieces):
+            if True:
                 nc.sync.dma_start(out=t[:].rearrange("p (g k) -> p g k", g=2)[:, :, kw * s : kw * s + kw],
                                   in_=W_v[:, 2 * h : 2 * h + 2, kw * s : kw * s + kw])
-            wr[h] = t
 
         warm = const.tile([P, 1], F32)
         nc.vector.memset(warm[:], 1.0)
         b_rows = const.tile([P, P], BF16)
         nc.vector.memset(b_rows[:], 0.0)
-        nc.sync.dma_start(out=b_rows[0 : N // P, :], in_=b.rearrange("(c q) -> c q", q=P))
         warm2 = const.tile([P, 1], F32)
         nc.scalar.activation(out=warm2[:], in_=warm[:], func=ACT.Exp if EXB else ACT.Ln)
         for kind, i in LOADS:
             if kind == "x":
                 load_x(i)
+            elif kind == "b":
+                nc.sync.dma_start(out=b_rows[0 : N // P, :], in_=b.rearrange("(c q) -> c q", q=P))
+            elif kind == "w":
+                load_w(i, 0, 1)
             else:
-                load_w(i, 2 if i == 0 else 1)
+                load_w(0, i, W0P)
         if BBC:
             b_bc = const.tile([P, N], BF16)
             nc.sync.dma_start(out=b_bc[:], in_=b.partition_broadcast(P))
@@ -136,10 +147,13 @@ def tile_pvfc_kernel(tc, x, W, b, out):
         nc.vector.tensor_scalar(out=base2[:, 0:1], in0=warm[:], scalar1=math.e, scalar2=None, op0=ALU.mult)
         nc.vector.tensor_scalar(out=base2[:, 1:2], in0=warm[:], scalar1=math.exp(-1.0), scalar2=None, op0=ALU.mult)
 
-        vcodes = const.tile([P, MT * 512], U32, align_bytes=256)
-        vscales = const.tile([P, MT * 512], U8, align_bytes=256)
+        vcodes_t = const.tile([P, 32 + MT * 512], U32, name="vcodes_t", align_bytes=256)
+        vcodes = vcodes_t[:, 32:]
+        vscales_t = const.tile([P, 192 + MT * 512], U8, name="vscales_t", align_bytes=256)
+        vscales = vscales_t[:, 192:]
         wcodes = const.tile([P, NCH * KP * 512], U32, align_bytes=256)
-        wscales = const.tile([P, NCH * KP * 512], U8, align_bytes=256)
+        wscales_t = const.tile([P, 64 + NCH * KP * 512], U8, name="wscales_t", align_bytes=256)
+        wscales = wscales_t[:, 64:]
         w_bc = const.tile([P, N], F32)
         hwh = const.tile([P, 1], F32)
 
@@ -364,6 +378,12 @@ def tile_pvfc_kernel(tc, x, W, b, out):
                                                op0=ALU.mult, op1=ALU.add)
             release(("acc", i, j))
 
+        def fin_part(i, j, a, b):
+            js = slice(512 * j + a, 512 * j + b)
+            ts = junk.tile([P, 512], F32, name="ts")
+            nc.scalar.activation(out=ts[:, a:b], in_=S["acc", i, j][:, a:b], func=ACT.Copy, scale=S["aa", i][:])
+            nc.gpsimd.tensor_tensor(out=S["o", i][:, js], in0=ts[:, a:b], in1=w_bc[:, js], op=ALU.add)
+
         def store(i, j0, j1):
             hs = slice(512 * j0, 512 * j1)
             nc.sync.dma_start(out=out_v[:, i, hs], in_=S["o", i][:, hs])
@@ -381,7 +401,7 @@ def tile_pvfc_kernel(tc, x, W, b, out):
             pres.setdefault(s, []).append((f, args))
 
         for u in range(MT):
-            hook(X0 + XP * u, xn, u, u % 2 == 0)
+            hook(X0 + XP * u, xn, u, u % 2 == 0 and u >= NX0 and u < NX1)
         for g in range(0, MT, PAIR):
             n = X0 + XP * (g + PAIR - 1)
             pre(n + LP, xp, g, g + PAIR)
@@ -446,11 +466,15 @@ def tile_pvfc_kernel(tc, x, W, b, out):
                 xe(late - 1, 1, XL1)
             if mid:
                 dot(i, 0)
+            if fill and late + 1 < MT and XSP == 3:
+                xs(late + 1)
             if p >= 0:
                 e3(p)
                 if i < MT:
                     fin(p, 0, False)
                     fin(p, 1, False)
+            if fill and late + 1 < MT and XSP == 2:
+                xs(late + 1)
             if mid:
                 if (i, 1) not in early:
                     mx(i, 1)
@@ -463,9 +487,10 @@ def tile_pvfc_kernel(tc, x, W, b, out):
                 sq(i, 2)
                 e0(i)
             if p >= 0 and i < MT:
-                fin(p, 2, SG2)
+                if i < MT - 1 or not TAIL:
+                    fin(p, 2, SG2)
                 store(p, 0, 2)
-            if mid:
+            if mid and (i < MT - 1 or not TAIL):
                 dot(i, 2)
             if fill and late + 1 < MT and XSP == 0:
                 xs(late + 1)
@@ -475,15 +500,27 @@ def tile_pvfc_kernel(tc, x, W, b, out):
                 sq(i, 3)
                 e1(i)
             if p >= 0 and i < MT:
-                fin(p, 3, p < MT - 2 or not LV)
+                if i == MT - 1 and TAIL:
+                    if DF:
+                        dot(i, 2)
+                    fin(p, 2, TS2)
+                    fin(p, 3, False)
+                else:
+                    fin(p, 3, p < MT - 2 or not LV)
                 store(p, 2, 4)
             if p == MT - 1:
-                fin(p, 0, True)
+                if FH == 0:
+                    fin(p, 0, True)
+                elif FH == 1:
+                    fin_part(p, 0, 0, 256)
+                    fin_part(p, 0, 256, 512)
                 for j in range(1, NCH):
                     fin(p, j, False)
                     store(p, j, j + 1)
                     if j == 2:
                         store(p, 0, 1)
+            if i == MT - 1 and TAIL and not DF:
+                dot(i, 2)
             if i < MT:
                 dot(i, 3)
             if fill and late + 1 < MT and XSP == 1:

@@ -21,19 +21,15 @@ NCH = N // 512
 NSLOT = 8 * KP
 FLOPS = 2 * M * K * N
 
-Q_LAG = 2
-X0 = 1
+Q_LAG = 1
+X0 = 0
 XP = 3
-PAIR = 1
 LP = 2
-LL = 6
-LC = 7
+LL = 0
 LS = 1
-LD = 4
-LT = 4
-LQ = 4
+LQ = 2
 MT1 = 4
-XE0 = False
+XE0 = True
 XE1 = True
 XS4 = 32
 B0 = 4
@@ -45,12 +41,12 @@ M10 = 50
 M11 = 50
 DS = 1
 DD = 2
-WV0 = 40
+WV0 = 20
 WVM = 4
-WVR = 3
+WVR = 1
 EXPS = True
 EXB = 0
-TL = 1
+TL = 0
 XL0 = False
 XL1 = False
 SG2 = True
@@ -58,13 +54,26 @@ XSP = 1
 LV = True
 BBC = True
 NX0 = 0
-NX1 = 8
-LOADS = (("p", 0), ("b", 0), ("x", 0), ("p", 1), ("w", 1), ("x", 1), ("x", 2), ("w", 2), ("x", 3), ("w", 3), ("x", 4), ("w", 4), ("x", 5), ("x", 6), ("w", 5), ("x", 7), ("w", 6), ("w", 7))
+NX1 = 6
+LOADS = (("p", 0), ("b", 0), ("x", 0), ("p", 1), ("x", 1), ("w", 1), ("x", 2), ("w", 2), ("x", 3), ("w", 3), ("x", 4), ("x", 5), ("w", 4), ("x", 6), ("w", 5), ("x", 7), ("w", 6), ("w", 7))
 W0P = 2
 TAIL = True
 TS2 = True
 FH = 1
 DF = True
+BN = 0
+LA = 3
+LCA = 5
+LCB = 6
+LTA = 5
+LTB = 4
+LLP = False
+XSM = True
+XEM0 = False
+XEM1 = True
+XD0 = 0
+XD1 = 0
+NXM = 3
 
 
 def tile_pvfc_kernel(tc, x, W, b, out):
@@ -147,13 +156,10 @@ def tile_pvfc_kernel(tc, x, W, b, out):
         nc.vector.tensor_scalar(out=base2[:, 0:1], in0=warm[:], scalar1=math.e, scalar2=None, op0=ALU.mult)
         nc.vector.tensor_scalar(out=base2[:, 1:2], in0=warm[:], scalar1=math.exp(-1.0), scalar2=None, op0=ALU.mult)
 
-        vcodes_t = const.tile([P, 32 + MT * 512], U32, name="vcodes_t", align_bytes=256)
-        vcodes = vcodes_t[:, 32:]
-        vscales_t = const.tile([P, 192 + MT * 512], U8, name="vscales_t", align_bytes=256)
-        vscales = vscales_t[:, 192:]
+        vcodes = const.tile([P, MT * 512], U32, align_bytes=256)
+        vscales = const.tile([P, MT * 512], U8, align_bytes=256)
         wcodes = const.tile([P, NCH * KP * 512], U32, align_bytes=256)
-        wscales_t = const.tile([P, 64 + NCH * KP * 512], U8, name="wscales_t", align_bytes=256)
-        wscales = wscales_t[:, 64:]
+        wscales = const.tile([P, NCH * KP * 512], U8, align_bytes=256)
         w_bc = const.tile([P, N], F32)
         hwh = const.tile([P, 1], F32)
 
@@ -401,22 +407,26 @@ def tile_pvfc_kernel(tc, x, W, b, out):
             pres.setdefault(s, []).append((f, args))
 
         for u in range(MT):
-            hook(X0 + XP * u, xn, u, u % 2 == 0 and u >= NX0 and u < NX1)
-        for g in range(0, MT, PAIR):
-            n = X0 + XP * (g + PAIR - 1)
-            pre(n + LP, xp, g, g + PAIR)
-            for u in range(g, g + PAIR):
-                hook(n + LL, xl, u)
-            hook(n + LC, xc, g, g + PAIR)
-            for u in range(g, min(g + PAIR, MT1)):
-                e = u - g
-                hook(n + LC + LS + LD * e, xs, u)
-                a = n + LC + LT + LD * e
+            hook(X0 + XP * u, xn, u, u % NXM == 0 and u >= NX0 and u < NX1)
+        mids = {}
+
+        def mid(s, f, *args):
+            mids.setdefault(s, []).append((f, args))
+
+        for u in range(MT):
+            n = X0 + XP * u
+            lc = LCA if u < LA else LCB
+            pre(n + LP, xp, u, u + 1)
+            (pre if LLP else hook)(n + lc + LL, xl, u)
+            hook(n + lc, xc, u, u + 1)
+            if u < MT1:
+                (mid if XSM else hook)(n + lc + LS, xs, u)
+                a = n + lc + (LTA if u < LA else LTB)
                 hook(a, xt, u, 0)
                 hook(a + 1, xt, u, 1)
-                hook(a + 1, xe, u, 0, XE0)
-                hook(a + 2, xe, u, 1, XE1)
-                hook(a + 2 + LQ, xq, u)
+                (mid if XEM0 else hook)(a + 1 + XD0, xe, u, 0, XE0)
+                (mid if XEM1 else hook)(a + 2 + XD1, xe, u, 1, XE1)
+                hook(a + 2 + max(XD0, XD1) + LQ, xq, u)
         hook(XS4, xs, MT1)
         hook(BW, b_w, 0)
         hook(BW + 2, b_w, 1)
@@ -430,9 +440,9 @@ def tile_pvfc_kernel(tc, x, W, b, out):
                 hook(m + DS, sq, i, j)
                 hook(max(m + DD, BW + 3), dot, i, j)
         last = max(list(hooks) + [NSLOT + Q_LAG - 1])
-        last = max(list(pres) + [last])
-        for s in range(min(list(hooks) + [0]), last + 1):
-            for f, args in pres.get(s, []):
+        last = max(list(pres) + list(mids) + [last])
+        for s in range(min(list(hooks) + list(pres) + [0]), last + 1):
+            for f, args in pres.get(s, []) + mids.get(s, []):
                 f(*args)
             if 0 <= s < NSLOT:
                 wt(s // KP, s % KP)
@@ -449,11 +459,11 @@ def tile_pvfc_kernel(tc, x, W, b, out):
         e0(0)
         for i in range(MT + 1):
             p = i - 1
-            mid = 0 < i < MT
+            inner = 0 < i < MT
             late = MT1 + p
             fill = 0 <= p and late < MT
             filled = 0 <= p - 1 and late - 1 < MT
-            if mid:
+            if inner:
                 if (i, 0) not in early:
                     mx(i, 0)
                 sq(i, 0)
@@ -464,7 +474,7 @@ def tile_pvfc_kernel(tc, x, W, b, out):
                 ed(p)
             if filled:
                 xe(late - 1, 1, XL1)
-            if mid:
+            if inner:
                 dot(i, 0)
             if fill and late + 1 < MT and XSP == 3:
                 xs(late + 1)
@@ -475,14 +485,14 @@ def tile_pvfc_kernel(tc, x, W, b, out):
                     fin(p, 1, False)
             if fill and late + 1 < MT and XSP == 2:
                 xs(late + 1)
-            if mid:
+            if inner:
                 if (i, 1) not in early:
                     mx(i, 1)
                 sq(i, 1)
                 dot(i, 1)
             if filled:
                 xq(late - 1)
-            if mid:
+            if inner:
                 mx(i, 2)
                 sq(i, 2)
                 e0(i)
@@ -490,11 +500,11 @@ def tile_pvfc_kernel(tc, x, W, b, out):
                 if i < MT - 1 or not TAIL:
                     fin(p, 2, SG2)
                 store(p, 0, 2)
-            if mid and (i < MT - 1 or not TAIL):
+            if inner and (i < MT - 1 or not TAIL):
                 dot(i, 2)
             if fill and late + 1 < MT and XSP == 0:
                 xs(late + 1)
-            if mid:
+            if inner:
                 mx(i, 3)
             if i < MT:
                 sq(i, 3)

@@ -15,65 +15,18 @@ AX = mybir.AxisListType
 
 P = 128
 M, K, N = 1024, 2048, 2048
-MT = M // P
-KP = K // 512
-NCH = N // 512
-NSLOT = 8 * KP
+ROW_TILES = M // P
+PASSES = K // 512
+COL_BANKS = N // 512
+W_BLOCKS = N // 256
+SLOTS = W_BLOCKS * PASSES
 FLOPS = 2 * M * K * N
 
-Q_LAG = 1
-X0 = 0
-XP = 3
-LP = 2
-LL = 0
-LS = 1
-LQ = 2
-MT1 = 4
-XE0 = True
-XE1 = True
-XS4 = 32
-B0 = 4
-BW = 28
-M00 = 32
-M01 = 32
-M02 = 32
-M10 = 50
-M11 = 50
-DS = 1
-DD = 2
-WV0 = 20
-WVM = 4
-WVR = 1
-EXPS = True
-EXB = 0
-TL = 0
-XL0 = False
-XL1 = False
-SG2 = True
-XSP = 1
-LV = True
-BBC = True
-NX0 = 0
-NX1 = 6
-LOADS = (("p", 0), ("b", 0), ("x", 0), ("p", 1), ("x", 1), ("w", 1), ("x", 2), ("w", 2), ("x", 3), ("w", 3), ("x", 4), ("x", 5), ("w", 4), ("x", 6), ("w", 5), ("x", 7), ("w", 6), ("w", 7))
-W0P = 2
-TAIL = True
-TS2 = True
-FH = 1
-DF = True
-BN = 0
-LA = 3
-LCA = 5
-LCB = 6
-LTA = 5
-LTB = 4
-LLP = False
-XSM = True
-XEM0 = False
-XEM1 = True
-XD0 = 0
-XD1 = 0
-NXM = 3
+X_EVERY = 3
+POWERS, LOG, SCALE, TURN, QUANTISE = 3, 6, 7, 11, 14
+W_LAG = 2
+TURNED_EARLY = 4
+NORMS_ON_VECTOR = (0, 3)
 
 
 def tile_pvfc_kernel(tc, x, W, b, out):
@@ -88,454 +41,371 @@ def tile_pvfc_kernel(tc, x, W, b, out):
         junk = ctx.enter_context(tc.tile_pool(name="junk", bufs=2))
         junk1 = ctx.enter_context(tc.tile_pool(name="junk1", bufs=1))
         opool = ctx.enter_context(tc.tile_pool(name="opool", bufs=3))
-        sm = ctx.enter_context(tc.tile_pool(name="sm", bufs=3))
+        small = ctx.enter_context(tc.tile_pool(name="small", bufs=3))
         psum = ctx.enter_context(tc.psum_pool(name="psum", bufs=1))
         ctx.enter_context(tc.manual_schedule())
 
-        x_v = x.rearrange("(p i) k -> p i k", i=MT)
+        x_v = x.rearrange("(p i) k -> p i k", i=ROW_TILES)
         W_v = W.rearrange("(g p) k -> p g k", p=P)
-        out_v = out.rearrange("(p i) n -> p i n", i=MT)
+        out_v = out.rearrange("(p i) n -> p i n", i=ROW_TILES)
         xr = {}
         wr = {}
         S = {}
 
         free_banks = list(range(8))
-        in_bank = {}
+        bank_of = {}
 
         def bank(key, shape):
             n = free_banks.pop(0)
-            in_bank[key] = n
+            bank_of[key] = n
             S[key] = psum.tile(shape, F32, tag="bank%d" % n, name="bank%d" % n)
             return S[key]
 
         def release(key):
-            free_banks.append(in_bank[key])
+            free_banks.append(bank_of[key])
 
         def load_x(i):
             t = xraw.tile([P, K], BF16, name="xr%d" % i)
             nc.sync.dma_start(out=t[:], in_=x_v[:, i, :])
             xr[i] = t[:]
 
-        def load_w(h, s, pieces):
-            if s == 0:
+        def load_w(h, k0, k1):
+            if k0 == 0:
                 wr[h] = wraw.tile([P, 2 * K], BF16, name="wr")
-            t = wr[h]
-            kw = K // pieces
-            if True:
-                nc.sync.dma_start(out=t[:].rearrange("p (g k) -> p g k", g=2)[:, :, kw * s : kw * s + kw],
-                                  in_=W_v[:, 2 * h : 2 * h + 2, kw * s : kw * s + kw])
+            nc.sync.dma_start(out=wr[h][:].rearrange("p (g k) -> p g k", g=2)[:, :, k0:k1],
+                              in_=W_v[:, 2 * h : 2 * h + 2, k0:k1])
 
         warm = const.tile([P, 1], F32)
         nc.vector.memset(warm[:], 1.0)
         b_rows = const.tile([P, P], BF16)
         nc.vector.memset(b_rows[:], 0.0)
         warm2 = const.tile([P, 1], F32)
-        nc.scalar.activation(out=warm2[:], in_=warm[:], func=ACT.Exp if EXB else ACT.Ln)
-        for kind, i in LOADS:
-            if kind == "x":
-                load_x(i)
-            elif kind == "b":
-                nc.sync.dma_start(out=b_rows[0 : N // P, :], in_=b.rearrange("(c q) -> c q", q=P))
-            elif kind == "w":
-                load_w(i, 0, 1)
-            else:
-                load_w(0, i, W0P)
-        if BBC:
-            b_bc = const.tile([P, N], BF16)
-            nc.sync.dma_start(out=b_bc[:], in_=b.partition_broadcast(P))
-        ident_f = const.tile([P, P], F32)
-        make_identity(nc, ident_f[:])
-        ident_bf = const.tile([P, P], BF16)
-        nc.vector.tensor_copy(out=ident_bf[:], in_=ident_f[:])
-        ones_f = const.tile([P, P], F32)
-        nc.vector.memset(ones_f[:], 1.0)
-        expo2 = const.tile([P, 2], F32)
-        nc.vector.memset(expo2[:, 0:1], 0.5)
-        nc.vector.memset(expo2[:, 1:2], -0.5)
-        base2 = const.tile([P, 2], F32)
-        nc.vector.tensor_scalar(out=base2[:, 0:1], in0=warm[:], scalar1=math.e, scalar2=None, op0=ALU.mult)
-        nc.vector.tensor_scalar(out=base2[:, 1:2], in0=warm[:], scalar1=math.exp(-1.0), scalar2=None, op0=ALU.mult)
+        nc.scalar.activation(out=warm2[:], in_=warm[:], func=ACT.Ln)
+        load_w(0, 0, K // 2)
+        nc.sync.dma_start(out=b_rows[0 : N // P, :], in_=b.rearrange("(c q) -> c q", q=P))
+        load_x(0)
+        load_w(0, K // 2, K)
+        for s in range(1, SLOTS):
+            if s % PASSES == 0:
+                load_w(s // PASSES, 0, K)
+            if s % X_EVERY == 0 and s // X_EVERY < ROW_TILES:
+                load_x(s // X_EVERY)
+        b_all = const.tile([P, N], BF16)
+        nc.sync.dma_start(out=b_all[:], in_=b.partition_broadcast(P))
 
-        vcodes = const.tile([P, MT * 512], U32, align_bytes=256)
-        vscales = const.tile([P, MT * 512], U8, align_bytes=256)
-        wcodes = const.tile([P, NCH * KP * 512], U32, align_bytes=256)
-        wscales = const.tile([P, NCH * KP * 512], U8, align_bytes=256)
-        w_bc = const.tile([P, N], F32)
-        hwh = const.tile([P, 1], F32)
+        ident = const.tile([P, P], F32)
+        make_identity(nc, ident[:])
+        ones = const.tile([P, P], F32)
+        nc.vector.memset(ones[:], 1.0)
+        half_powers = const.tile([P, 2], F32)
+        nc.vector.memset(half_powers[:, 0:1], 0.5)
+        nc.vector.memset(half_powers[:, 1:2], -0.5)
+        bases = const.tile([P, 2], F32)
+        nc.vector.tensor_scalar(out=bases[:, 0:1], in0=warm[:], scalar1=math.e, scalar2=None, op0=ALU.mult)
+        nc.vector.tensor_scalar(out=bases[:, 1:2], in0=warm[:], scalar1=math.exp(-1.0), scalar2=None, op0=ALU.mult)
+
+        vcodes = const.tile([P, ROW_TILES * 512], U32, align_bytes=256)
+        vscales = const.tile([P, ROW_TILES * 512], U8, align_bytes=256)
+        wcodes = const.tile([P, COL_BANKS * PASSES * 512], U32, align_bytes=256)
+        wscales = const.tile([P, COL_BANKS * PASSES * 512], U8, align_bytes=256)
+        sc_b = const.tile([P, N], F32)
+        half_root = const.tile([P, 1], F32)
 
         def col(name, n=1):
             S[name] = const.tile([P, n], F32, name=name)
             return S[name][:]
 
-        def b_mm(j):
-            bp = bank(("bp", j), [P, 4, P])
-            for q in range(4):
-                c = 4 * j + q
-                nc.tensor.matmul(bp[:, q, :], lhsT=ident_bf[:, c : c + 1].to_broadcast([P, P]), rhs=b_rows[:],
-                                 start=True, stop=True)
-
-        def b_cp(j):
-            nc.scalar.activation(out=w_bc[:, 512 * j : 512 * j + 512], in_=S["bp", j][:].rearrange("p q n -> p (q n)"),
-                                 func=ACT.Copy, scale=S["scb"][:])
-            release(("bp", j))
-
         def b_norm():
-            b2p = col("b2p")
-            bj = const.tile([P, P], F32)
-            nc.scalar.activation(out=bj[:], in_=b_rows[:], func=ACT.Square, accum_out=b2p)
+            part = col("b_part")
+            squares = const.tile([P, P], F32)
+            nc.scalar.activation(out=squares[:], in_=b_rows[:], func=ACT.Square, accum_out=part)
             b2_ps = bank("b2_ps", [P, 1])
-            nc.tensor.matmul(b2_ps[:], lhsT=ones_f[:], rhs=b2p, start=True, stop=True)
-            zin = col("zin", 2)
-            nc.vector.tensor_scalar(out=zin[:, 0:1], in0=b2_ps[:], scalar1=1e-15, scalar2=400.0, op0=ALU.max, op1=ALU.min)
-            nc.vector.tensor_scalar(out=zin[:, 1:2], in0=b2_ps[:], scalar1=1e-12, scalar2=400.0, op0=ALU.max, op1=ALU.min)
+            nc.tensor.matmul(b2_ps[:], lhsT=ones[:], rhs=part, start=True, stop=True)
+            zz = col("zz", 2)
+            nc.vector.tensor_scalar(out=zz[:, 0:1], in0=b2_ps[:], scalar1=1e-15, scalar2=400.0, op0=ALU.max, op1=ALU.min)
+            nc.vector.tensor_scalar(out=zz[:, 1:2], in0=b2_ps[:], scalar1=1e-12, scalar2=400.0, op0=ALU.max, op1=ALU.min)
             nc.vector.tensor_copy(out=col("b2"), in_=b2_ps[:])
             release("b2_ps")
-            nc.gpsimd.tensor_tensor(out=col("z", 2), in0=zin, in1=expo2[:], op=ALU.pow)
-            nc.gpsimd.tensor_tensor(out=col("bee", 2), in0=base2[:], in1=S["z"][:, 0:1].to_broadcast([P, 2]), op=ALU.pow)
+            nc.gpsimd.tensor_tensor(out=col("z", 2), in0=zz, in1=half_powers[:], op=ALU.pow)
+            nc.gpsimd.tensor_tensor(out=col("exps", 2), in0=bases[:], in1=S["z"][:, 0:1].to_broadcast([P, 2]), op=ALU.pow)
 
         def b_scale():
-            ee = S["bee"]
-            nc.vector.tensor_scalar(out=col("y0"), in0=S["zin"][:, 0:1], scalar1=1.0 / 6.0, scalar2=1.0, op0=ALU.mult, op1=ALU.add)
+            ee = S["exps"]
+            nc.vector.tensor_scalar(out=col("y0"), in0=S["zz"][:, 0:1], scalar1=1.0 / 6.0, scalar2=1.0, op0=ALU.mult, op1=ALU.add)
             nc.vector.tensor_scalar(out=col("yb"), in0=ee[:, 0:1], scalar1=ee[:, 1:2], scalar2=S["z"][:, 1:2],
                                     op0=ALU.subtract, op1=ALU.mult)
-            nc.vector.tensor_scalar(out=col("scb"), in0=S["yb"][:], scalar1=0.5, scalar2=S["y0"][:], op0=ALU.mult, op1=ALU.max)
-            nc.vector.tensor_scalar(out=col("hq"), in0=S["scb"][:], scalar1=S["scb"][:], scalar2=S["b2"][:], op0=ALU.mult, op1=ALU.mult)
-            nc.vector.tensor_scalar(out=col("hin"), in0=S["hq"][:], scalar1=0.25, scalar2=0.25, op0=ALU.mult, op1=ALU.add)
-            nc.gpsimd.tensor_tensor(out=hwh[:], in0=S["hin"][:], in1=expo2[:, 0:1], op=ALU.pow)
+            nc.vector.tensor_scalar(out=col("sc"), in0=S["yb"][:], scalar1=0.5, scalar2=S["y0"][:], op0=ALU.mult, op1=ALU.max)
+            nc.vector.tensor_scalar(out=col("w2"), in0=S["sc"][:], scalar1=S["sc"][:], scalar2=S["b2"][:], op0=ALU.mult, op1=ALU.mult)
+            nc.vector.tensor_scalar(out=col("w2q"), in0=S["w2"][:], scalar1=0.25, scalar2=0.25, op0=ALU.mult, op1=ALU.add)
+            nc.gpsimd.tensor_tensor(out=half_root[:], in0=S["w2q"][:], in1=half_powers[:, 0:1], op=ALU.pow)
 
-        def b_w(j):
-            js = slice(1024 * j, 1024 * j + 1024)
-            nc.vector.tensor_scalar(out=w_bc[:, js], in0=b_bc[:, js], scalar1=S["scb"][:], scalar2=None, op0=ALU.mult)
+        def b_spread(half):
+            js = slice(1024 * half, 1024 * half + 1024)
+            nc.vector.tensor_scalar(out=sc_b[:, js], in0=b_all[:, js], scalar1=S["sc"][:], scalar2=None, op0=ALU.mult)
 
-        pin = const.tile([P, MT, 3], F32)
-        pw = const.tile([P, MT, 3], F32)
-        expo = const.tile([P, MT, 3], F32)
-        nc.vector.memset(expo[:], 0.5)
-        nc.vector.memset(expo[:, :, 2:3], -0.5)
-        ln = const.tile([P, MT, 1], F32)
-        coef = const.tile([P, MT, 1], F32)
+        q = const.tile([P, ROW_TILES, 1], F32)
+        q_in = const.tile([P, ROW_TILES, 2], F32)
+        q_pow = const.tile([P, ROW_TILES, 2], F32)
+        q21 = const.tile([P, ROW_TILES, 1], F32)
+        ln = const.tile([P, ROW_TILES, 1], F32)
+        coef = const.tile([P, ROW_TILES, 1], F32)
 
-        def xn(i, on_vector):
-            acc = pin[:, i, 0:1]
-            if on_vector:
-                xj = junk1.tile([P, K], BF16, name="xj")
-                nc.vector.scalar_tensor_tensor(out=xj[:], in0=xr[i], scalar=1.0, in1=xr[i], op0=ALU.mult, op1=ALU.mult,
-                                               accum_out=acc)
+        def x_norm(i):
+            if i in NORMS_ON_VECTOR:
+                unread = junk1.tile([P, K], BF16, name="unread_v")
+                nc.vector.scalar_tensor_tensor(out=unread[:], in0=xr[i], scalar=1.0, in1=xr[i], op0=ALU.mult, op1=ALU.mult,
+                                               accum_out=q[:, i, :])
             else:
-                xk = junk1.tile([P, K], BF16, name="xk")
-                nc.scalar.activation(out=xk[:], in_=xr[i], func=ACT.Square, accum_out=acc)
+                unread = junk1.tile([P, K], BF16, name="unread_s")
+                nc.scalar.activation(out=unread[:], in_=xr[i], func=ACT.Square, accum_out=q[:, i, :])
 
-        def xp(a, b):
-            nc.vector.tensor_scalar_add(pin[:, a:b, 1:2], pin[:, a:b, 0:1], 1.0)
-            nc.vector.tensor_scalar_max(pin[:, a:b, 2:3], pin[:, a:b, 0:1], 1e-12)
-            nc.gpsimd.tensor_tensor(out=pw[:, a:b, :], in0=pin[:, a:b, :], in1=expo[:, a:b, :], op=ALU.pow)
+        def x_powers(i):
+            nc.vector.tensor_scalar(out=q_in[:, i, 0:1], in0=q[:, i, :], scalar1=1.0, scalar2=q[:, i, :], op0=ALU.add, op1=ALU.mult)
+            nc.vector.tensor_scalar_max(q_in[:, i, 1:2], q[:, i, :], 1e-12)
+            nc.gpsimd.tensor_tensor(out=q_pow[:, i, :], in0=q_in[:, i, :], in1=half_powers[:], op=ALU.pow)
+            nc.vector.tensor_scalar(out=q21[:, i, :], in0=q[:, i, :], scalar1=2.0, scalar2=1.0, op0=ALU.mult, op1=ALU.add)
 
-        def xl(i):
-            nc.scalar.activation(out=ln[:, i, :], in_=pw[:, i, 0:1], func=ACT.Ln, bias=pw[:, i, 1:2])
+        def x_log(i):
+            nc.scalar.activation(out=ln[:, i, :], in_=q_pow[:, i, 0:1], func=ACT.Ln, bias=q21[:, i, :], scale=2.0)
 
-        def xc(a, b):
-            nc.vector.tensor_tensor(out=coef[:, a:b, :], in0=ln[:, a:b, :], in1=pw[:, a:b, 2:3], op=ALU.mult)
+        def x_coef(i):
+            nc.vector.tensor_scalar(out=coef[:, i, :], in0=ln[:, i, :], scalar1=0.5, scalar2=q_pow[:, i, 1:2], op0=ALU.mult, op1=ALU.mult)
 
-        def xs(i):
+        def x_scale(i):
             S["v", i] = vpool.tile([P, K], BF16, name="v")
             nc.vector.tensor_scalar(out=S["v", i][:], in0=xr[i], scalar1=coef[:, i, :], scalar2=None, op0=ALU.mult)
 
-        def xt(i, half):
-            v32 = S["v", i][:].bitcast(F32)
+        def x_turn(i, half):
+            words = S["v", i][:].bitcast(F32)
             t = bank(("xt", i, half), [P, 2, 2, P])
-            for cl in range(2):
+            for c in range(2):
                 for u in range(2):
-                    c0 = 256 * (2 * half + cl)
-                    nc.tensor.transpose(t[:, cl, u, :], v32[:, c0 + u : c0 + 256 : 2], ident_f[:])
+                    m0 = 256 * (2 * half + c)
+                    nc.tensor.transpose(t[:, c, u, :], words[:, m0 + u : m0 + 256 : 2], ident[:])
 
-        def xe(i, half, on_vector):
+        def x_copy(i, half, copy):
             if half == 0:
-                S["xg", i] = xgp.tile([P, KP * P * 4], BF16, name="xg", align_bytes=64)
+                S["xg", i] = xgp.tile([P, PASSES * P * 4], BF16, name="xg", align_bytes=64)
             src = S["xt", i, half][:].rearrange("p c u r -> p c r u")
             dst = S["xg", i][:, 1024 * half : 1024 * half + 1024].bitcast(F32).rearrange("p (c r u) -> p c r u", c=2, r=P, u=2)
-            if on_vector:
-                nc.vector.tensor_copy(out=dst, in_=src)
-            else:
-                nc.scalar.copy(out=dst, in_=src)
+            copy(out=dst, in_=src)
             release(("xt", i, half))
 
-        def xq(i):
+        def x_quantise(i):
             nc.vector.quantize_mx(out=vcodes[:, 512 * i : 512 * i + 512].bitcast(FP8X4),
                                   scales=vscales[:, 512 * i : 512 * i + 512], in_=S["xg", i][:])
 
-        def wt(h, c):
-            w32 = wr[h][:].bitcast(F32)
+        def w_turn(h, c):
+            words = wr[h][:].bitcast(F32)
             t = bank(("wt", h, c), [P, 2, 2, P])
-            for gl in range(2):
+            for g in range(2):
                 for u in range(2):
-                    c0 = 1024 * gl + 256 * c
-                    nc.tensor.transpose(t[:, gl, u, :], w32[:, c0 + u : c0 + 256 : 2], ident_f[:])
+                    m0 = 1024 * g + 256 * c
+                    nc.tensor.transpose(t[:, g, u, :], words[:, m0 + u : m0 + 256 : 2], ident[:])
 
-        def we(h, c, on_vector):
+        def w_copy(h, c, copy):
             S["wg", h, c] = wgp.tile([P, 1024], BF16, name="wg", align_bytes=64)
             dst = S["wg", h, c][:].bitcast(F32).rearrange("p (g n u) -> p g n u", g=2, n=P, u=2)
-            src = S["wt", h, c][:].rearrange("p g u n -> p g n u")
-            if on_vector:
-                nc.vector.tensor_copy(out=dst, in_=src)
-            else:
-                nc.scalar.copy(out=dst, in_=src)
+            copy(out=dst, in_=S["wt", h, c][:].rearrange("p g u n -> p g n u"))
             release(("wt", h, c))
 
-        def wq(h, c):
-            col0 = ((h // 2) * KP + c) * 512 + 256 * (h % 2)
+        def w_quantise(h, c):
+            col0 = ((h // 2) * PASSES + c) * 512 + 256 * (h % 2)
             nc.vector.quantize_mx(out=wcodes[:, col0 : col0 + 256].bitcast(FP8X4),
                                   scales=wscales[:, col0 : col0 + 256], in_=S["wg", h, c][:])
 
-        def mx(i, j):
+        def product(i, j):
             acc = bank(("acc", i, j), [P, 512])
-            for c in range(KP):
-                lc = 512 * i + P * c
-                rc = (j * KP + c) * 512
-                nc.tensor.matmul_mx(out=acc[:], lhsT=vcodes[:, lc : lc + P].bitcast(FP8X4),
-                                    lhsT_scale=vscales[:, lc : lc + P],
-                                    rhs=wcodes[:, rc : rc + 512].bitcast(FP8X4),
-                                    rhs_scale=wscales[:, rc : rc + 512],
-                                    start=(c == 0), stop=(c == KP - 1))
+            for c in range(PASSES):
+                v0 = 512 * i + P * c
+                w0 = (j * PASSES + c) * 512
+                nc.tensor.matmul_mx(out=acc[:], lhsT=vcodes[:, v0 : v0 + P].bitcast(FP8X4),
+                                    lhsT_scale=vscales[:, v0 : v0 + P],
+                                    rhs=wcodes[:, w0 : w0 + 512].bitcast(FP8X4),
+                                    rhs_scale=wscales[:, w0 : w0 + 512],
+                                    start=(c == 0), stop=(c == PASSES - 1))
 
-        def sq(i, j):
+        def squares_of(i, j):
             if j == 0:
-                S["s4", i] = sm.tile([P, NCH], F32, name="s4")
-            sqt = junk.tile([P, 512], BF16, name="sqt")
-            nc.scalar.activation(out=sqt[:], in_=S["acc", i, j][:], func=ACT.Square, accum_out=S["s4", i][:, j : j + 1])
+                S["s4", i] = small.tile([P, COL_BANKS], F32, name="s4")
+            unread = junk.tile([P, 512], BF16, name="unread_sq")
+            nc.scalar.activation(out=unread[:], in_=S["acc", i, j][:], func=ACT.Square, accum_out=S["s4", i][:, j : j + 1])
 
-        def dot(i, j):
+        def dot_of(i, j):
             if j == 0:
-                S["d4", i] = sm.tile([P, NCH], F32, name="d4")
-            dj = junk.tile([P, 512], F32, name="dj")
-            nc.vector.scalar_tensor_tensor(out=dj[:], in0=S["acc", i, j][:], scalar=0.5, in1=w_bc[:, 512 * j : 512 * j + 512],
+                S["d4", i] = small.tile([P, COL_BANKS], F32, name="d4")
+            unread = junk.tile([P, 512], F32, name="unread_dot")
+            nc.vector.scalar_tensor_tensor(out=unread[:], in0=S["acc", i, j][:], scalar=0.5, in1=sc_b[:, 512 * j : 512 * j + 512],
                                            op0=ALU.mult, op1=ALU.mult, accum_out=S["d4", i][:, j : j + 1])
 
-        def e0(i):
-            S["s3", i] = sm.tile([P, 1], F32, name="s3")
-            j3 = sm.tile([P, 3], F32, name="j3")
-            nc.scalar.activation(out=j3[:], in_=S["s4", i][:, 0:3], func=ACT.Identity, accum_out=S["s3", i][:])
+        def first_squares(i):
+            S["s3", i] = small.tile([P, 1], F32, name="s3")
+            unread = small.tile([P, 3], F32, name="unread_s3")
+            nc.scalar.activation(out=unread[:], in_=S["s4", i][:, 0:3], func=ACT.Identity, accum_out=S["s3", i][:])
 
-        def e1(i):
-            pin2 = sm.tile([P, 2], F32, name="pin2")
-            nc.vector.tensor_scalar(out=pin2[:, 0:1], in0=S["s4", i][:, 3:4], scalar1=S["s3", i][:], scalar2=400.0,
+        def root(i):
+            u2 = small.tile([P, 2], F32, name="u2")
+            nc.vector.tensor_scalar(out=u2[:, 0:1], in0=S["s4", i][:, 3:4], scalar1=S["s3", i][:], scalar2=400.0,
                                     op0=ALU.add, op1=ALU.min)
-            nc.vector.tensor_scalar(out=pin2[:, 1:2], in0=S["s4", i][:, 3:4], scalar1=S["s3", i][:], scalar2=1e-12,
+            nc.vector.tensor_scalar(out=u2[:, 1:2], in0=S["s4", i][:, 3:4], scalar1=S["s3", i][:], scalar2=1e-12,
                                     op0=ALU.add, op1=ALU.max)
-            pw2 = sm.tile([P, 2], F32, name="pw2")
-            S["pw2", i] = pw2
-            nc.gpsimd.tensor_tensor(out=pw2[:], in0=pin2[:], in1=expo2[:], op=ALU.pow)
-            ee = sm.tile([P, 3], F32, name="ee")
+            S["r", i] = small.tile([P, 2], F32, name="r")
+            nc.gpsimd.tensor_tensor(out=S["r", i][:], in0=u2[:], in1=half_powers[:], op=ALU.pow)
+
+        def exps_of(i):
+            ee = small.tile([P, 3], F32, name="ee")
             S["ee", i] = ee
-            if EXPS:
-                return
-            nc.gpsimd.tensor_tensor(out=ee[:, 0:2], in0=base2[:], in1=pw2[:, 0:1].to_broadcast([P, 2]), op=ALU.pow)
+            r = S["r", i][:, 0:1]
+            nc.scalar.activation(out=ee[:, 0:1], in_=r, func=ACT.Exp)
+            nc.scalar.activation(out=ee[:, 1:2], in_=r, func=ACT.Exp, scale=-1.0)
+            nc.scalar.activation(out=ee[:, 2:3], in_=r, func=ACT.Tanh, scale=0.5)
 
-        def e2(i):
-            pw2 = S["pw2", i]
+        def dot_sum(i):
+            S["d", i] = small.tile([P, 1], F32, name="d")
+            nc.vector.reduce_sum(out=S["d", i][:], in_=S["d4", i][:], axis=AX.X)
+
+        def factor(i):
             ee = S["ee", i]
-            if not EXPS:
-                return
-            nc.scalar.activation(out=ee[:, 0:1], in_=pw2[:, 0:1], func=ACT.Exp)
-            nc.scalar.activation(out=ee[:, 1:2], in_=pw2[:, 0:1], func=ACT.Exp, scale=-1.0)
-            nc.scalar.activation(out=ee[:, 2:3], in_=pw2[:, 0:1], func=ACT.Tanh, scale=0.5)
-
-        def ed(i):
-            S["d1", i] = sm.tile([P, 1], F32, name="d1")
-            nc.vector.reduce_sum(out=S["d1", i][:], in_=S["d4", i][:], axis=AX.X)
-
-        def e3(i):
-            pw2 = S["pw2", i]
-            ee = S["ee", i]
+            inv = S["r", i][:, 1:2]
             S["o", i] = opool.tile([P, N], F32, name="o")
-            if EXPS:
-                cy2 = sm.tile([P, 1], F32, name="cy2")
-                nc.vector.tensor_scalar(out=cy2[:], in0=ee[:, 0:1], scalar1=ee[:, 1:2], scalar2=pw2[:, 1:2],
-                                        op0=ALU.subtract, op1=ALU.mult)
-                t1 = sm.tile([P, 1], F32, name="t1")
-                nc.vector.tensor_scalar(out=t1[:], in0=ee[:, 2:3], scalar1=pw2[:, 1:2], scalar2=S["d1", i][:],
-                                        op0=ALU.mult, op1=ALU.mult)
-                aa = sm.tile([P, 1], F32, name="aa")
-                S["aa", i] = aa
-                nc.vector.scalar_tensor_tensor(out=aa[:], in0=t1[:], scalar=hwh[:], in1=cy2[:], op0=ALU.add, op1=ALU.mult)
-                return
-            qq = sm.tile([P, 1], F32, name="qq")
-            nc.vector.tensor_scalar(out=qq[:], in0=ee[:, 0:1], scalar1=ee[:, 1:2], scalar2=2.0, op0=ALU.add, op1=ALU.add)
-            cy2 = sm.tile([P, 1], F32, name="cy2")
-            nc.vector.tensor_scalar(out=cy2[:], in0=ee[:, 0:1], scalar1=ee[:, 1:2], scalar2=pw2[:, 1:2],
+            two_sinhc = small.tile([P, 1], F32, name="two_sinhc")
+            nc.vector.tensor_scalar(out=two_sinhc[:], in0=ee[:, 0:1], scalar1=ee[:, 1:2], scalar2=inv,
                                     op0=ALU.subtract, op1=ALU.mult)
-            rq = sm.tile([P, 1], F32, name="rq")
-            nc.vector.reciprocal(rq[:], qq[:])
-            t1 = sm.tile([P, 1], F32, name="t1")
-            nc.vector.tensor_scalar(out=t1[:], in0=cy2[:], scalar1=rq[:], scalar2=S["d1", i][:], op0=ALU.mult, op1=ALU.mult)
-            aa = sm.tile([P, 1], F32, name="aa")
-            S["aa", i] = aa
-            nc.vector.scalar_tensor_tensor(out=aa[:], in0=t1[:], scalar=hwh[:], in1=cy2[:], op0=ALU.add, op1=ALU.mult)
+            along = small.tile([P, 1], F32, name="along")
+            nc.vector.tensor_scalar(out=along[:], in0=ee[:, 2:3], scalar1=inv, scalar2=S["d", i][:], op0=ALU.mult, op1=ALU.mult)
+            S["a", i] = small.tile([P, 1], F32, name="a")
+            nc.vector.scalar_tensor_tensor(out=S["a", i][:], in0=along[:], scalar=half_root[:], in1=two_sinhc[:],
+                                           op0=ALU.add, op1=ALU.mult)
 
-        def fin(i, j, sg):
+        def last_on_vector(i, j):
             js = slice(512 * j, 512 * j + 512)
-            acc = S["acc", i, j]
-            o = S["o", i]
-            if sg:
-                ts = junk.tile([P, 512], F32, name="ts")
-                nc.scalar.activation(out=ts[:], in_=acc[:], func=ACT.Copy, scale=S["aa", i][:])
-                nc.gpsimd.tensor_tensor(out=o[:, js], in0=ts[:], in1=w_bc[:, js], op=ALU.add)
-            else:
-                nc.vector.scalar_tensor_tensor(out=o[:, js], in0=acc[:], scalar=S["aa", i][:], in1=w_bc[:, js],
-                                               op0=ALU.mult, op1=ALU.add)
+            nc.vector.scalar_tensor_tensor(out=S["o", i][:, js], in0=S["acc", i, j][:], scalar=S["a", i][:], in1=sc_b[:, js],
+                                           op0=ALU.mult, op1=ALU.add)
             release(("acc", i, j))
 
-        def fin_part(i, j, a, b):
-            js = slice(512 * j + a, 512 * j + b)
-            ts = junk.tile([P, 512], F32, name="ts")
-            nc.scalar.activation(out=ts[:, a:b], in_=S["acc", i, j][:, a:b], func=ACT.Copy, scale=S["aa", i][:])
-            nc.gpsimd.tensor_tensor(out=S["o", i][:, js], in0=ts[:, a:b], in1=w_bc[:, js], op=ALU.add)
+        def last_on_scalar_and_gpsimd(i, j):
+            js = slice(512 * j, 512 * j + 512)
+            au = junk.tile([P, 512], F32, name="au")
+            nc.scalar.activation(out=au[:], in_=S["acc", i, j][:], func=ACT.Copy, scale=S["a", i][:])
+            nc.gpsimd.tensor_tensor(out=S["o", i][:, js], in0=au[:], in1=sc_b[:, js], op=ALU.add)
+            release(("acc", i, j))
 
         def store(i, j0, j1):
             hs = slice(512 * j0, 512 * j1)
             nc.sync.dma_start(out=out_v[:, i, hs], in_=S["o", i][:, hs])
 
-        hooks = {}
-
-        def hook(s, f, *args):
-            hooks.setdefault(s, []).append((f, args))
-
         b_norm()
-        hook(B0, b_scale)
-        pres = {}
+        for s in range(SLOTS + W_LAG + 1):
+            for i in range(ROW_TILES):
+                after = s - X_EVERY * i
+                if after == POWERS:
+                    x_powers(i)
+                if after == LOG:
+                    x_log(i)
+                if after == TURN + 2 and i < TURNED_EARLY:
+                    x_copy(i, 1, nc.vector.tensor_copy)
+            if s < SLOTS:
+                w_turn(s // PASSES, s % PASSES)
+                on_vector = s >= 20 and s % 5 == 0
+                w_copy(s // PASSES, s % PASSES, nc.vector.tensor_copy if on_vector else nc.scalar.copy)
+            if W_LAG <= s < SLOTS + W_LAG:
+                w_quantise((s - W_LAG) // PASSES, (s - W_LAG) % PASSES)
+            if s == 4:
+                b_scale()
+            if s % X_EVERY == 0 and s // X_EVERY < ROW_TILES:
+                x_norm(s // X_EVERY)
+            for i in range(ROW_TILES):
+                after = s - X_EVERY * i
+                if after == LOG:
+                    x_coef(i)
+                if i < TURNED_EARLY:
+                    if after == SCALE:
+                        x_scale(i)
+                    if after == TURN:
+                        x_turn(i, 0)
+                    if after == TURN + 1:
+                        x_turn(i, 1)
+                        x_copy(i, 0, nc.vector.tensor_copy)
+                    if after == QUANTISE:
+                        x_quantise(i)
+            if s == 18:
+                product(0, 0)
+            if s == SLOTS - 2:
+                b_spread(0)
+            if s == SLOTS - 1:
+                product(0, 1)
+            if s == SLOTS:
+                b_spread(1)
+                squares_of(0, 0)
+                squares_of(0, 1)
+                product(0, 2)
+            if s == SLOTS + 1:
+                dot_of(0, 0)
+            if s == SLOTS + 2:
+                x_scale(TURNED_EARLY)
+                dot_of(0, 1)
+        nc.scalar.activation(out=warm2[:], in_=warm[:], func=ACT.Exp)
+        squares_of(0, 2)
+        dot_of(0, 2)
+        product(0, 3)
+        first_squares(0)
+        squares_of(0, 3)
+        root(0)
+        dot_of(0, 3)
 
-        def pre(s, f, *args):
-            pres.setdefault(s, []).append((f, args))
-
-        for u in range(MT):
-            hook(X0 + XP * u, xn, u, u % NXM == 0 and u >= NX0 and u < NX1)
-        mids = {}
-
-        def mid(s, f, *args):
-            mids.setdefault(s, []).append((f, args))
-
-        for u in range(MT):
-            n = X0 + XP * u
-            lc = LCA if u < LA else LCB
-            pre(n + LP, xp, u, u + 1)
-            (pre if LLP else hook)(n + lc + LL, xl, u)
-            hook(n + lc, xc, u, u + 1)
-            if u < MT1:
-                (mid if XSM else hook)(n + lc + LS, xs, u)
-                a = n + lc + (LTA if u < LA else LTB)
-                hook(a, xt, u, 0)
-                hook(a + 1, xt, u, 1)
-                (mid if XEM0 else hook)(a + 1 + XD0, xe, u, 0, XE0)
-                (mid if XEM1 else hook)(a + 2 + XD1, xe, u, 1, XE1)
-                hook(a + 2 + max(XD0, XD1) + LQ, xq, u)
-        hook(XS4, xs, MT1)
-        hook(BW, b_w, 0)
-        hook(BW + 2, b_w, 1)
-        early = []
-        for i, j, m in ((0, 0, M00), (0, 1, M01), (0, 2, M02), (1, 0, M10), (1, 1, M11)):
-            if m > 40:
-                continue
-            early.append((i, j))
-            hook(m, mx, i, j)
-            if i == 0 and j < 2:
-                hook(m + DS, sq, i, j)
-                hook(max(m + DD, BW + 3), dot, i, j)
-        last = max(list(hooks) + [NSLOT + Q_LAG - 1])
-        last = max(list(pres) + list(mids) + [last])
-        for s in range(min(list(hooks) + list(pres) + [0]), last + 1):
-            for f, args in pres.get(s, []) + mids.get(s, []):
-                f(*args)
-            if 0 <= s < NSLOT:
-                wt(s // KP, s % KP)
-                we(s // KP, s % KP, s >= WV0 and s % WVM == WVR)
-            if Q_LAG <= s < NSLOT + Q_LAG:
-                wq((s - Q_LAG) // KP, (s - Q_LAG) % KP)
-            for f, args in hooks.get(s, []):
-                f(*args)
-        if EXPS and TL == 0:
-            nc.scalar.activation(out=warm2[:], in_=warm[:], func=ACT.Exp)
-        sq(0, 2)
-        dot(0, 2)
-        mx(0, 3)
-        e0(0)
-        for i in range(MT + 1):
+        for i in range(1, ROW_TILES + 1):
             p = i - 1
-            inner = 0 < i < MT
-            late = MT1 + p
-            fill = 0 <= p and late < MT
-            filled = 0 <= p - 1 and late - 1 < MT
-            if inner:
-                if (i, 0) not in early:
-                    mx(i, 0)
-                sq(i, 0)
-            if p == 0 and EXPS and TL == 1:
-                nc.scalar.activation(out=warm2[:], in_=warm[:], func=ACT.Exp)
-            if p >= 0:
-                e2(p)
-                ed(p)
-            if filled:
-                xe(late - 1, 1, XL1)
-            if inner:
-                dot(i, 0)
-            if fill and late + 1 < MT and XSP == 3:
-                xs(late + 1)
-            if p >= 0:
-                e3(p)
-                if i < MT:
-                    fin(p, 0, False)
-                    fin(p, 1, False)
-            if fill and late + 1 < MT and XSP == 2:
-                xs(late + 1)
-            if inner:
-                if (i, 1) not in early:
-                    mx(i, 1)
-                sq(i, 1)
-                dot(i, 1)
-            if filled:
-                xq(late - 1)
-            if inner:
-                mx(i, 2)
-                sq(i, 2)
-                e0(i)
-            if p >= 0 and i < MT:
-                if i < MT - 1 or not TAIL:
-                    fin(p, 2, SG2)
-                store(p, 0, 2)
-            if inner and (i < MT - 1 or not TAIL):
-                dot(i, 2)
-            if fill and late + 1 < MT and XSP == 0:
-                xs(late + 1)
-            if inner:
-                mx(i, 3)
-            if i < MT:
-                sq(i, 3)
-                e1(i)
-            if p >= 0 and i < MT:
-                if i == MT - 1 and TAIL:
-                    if DF:
-                        dot(i, 2)
-                    fin(p, 2, TS2)
-                    fin(p, 3, False)
-                else:
-                    fin(p, 3, p < MT - 2 or not LV)
-                store(p, 2, 4)
-            if p == MT - 1:
-                if FH == 0:
-                    fin(p, 0, True)
-                elif FH == 1:
-                    fin_part(p, 0, 0, 256)
-                    fin_part(p, 0, 256, 512)
-                for j in range(1, NCH):
-                    fin(p, j, False)
+            turning = TURNED_EARLY + p
+            turned = turning - 1
+            copying = p > 0 and turned < ROW_TILES
+            ending = i == ROW_TILES - 1
+            if i < ROW_TILES:
+                product(i, 0)
+                squares_of(i, 0)
+            exps_of(p)
+            dot_sum(p)
+            if copying:
+                x_copy(turned, 1, nc.scalar.copy)
+            if i < ROW_TILES:
+                dot_of(i, 0)
+            factor(p)
+            if i == ROW_TILES:
+                last_on_scalar_and_gpsimd(p, 0)
+                for j in range(1, COL_BANKS):
+                    last_on_vector(p, j)
                     store(p, j, j + 1)
                     if j == 2:
                         store(p, 0, 1)
-            if i == MT - 1 and TAIL and not DF:
-                dot(i, 2)
-            if i < MT:
-                dot(i, 3)
-            if fill and late + 1 < MT and XSP == 1:
-                xs(late + 1)
-            if fill:
-                xt(late, 0)
-                xt(late, 1)
-                xe(late, 0, XL0)
+                continue
+            last_on_vector(p, 0)
+            last_on_vector(p, 1)
+            product(i, 1)
+            squares_of(i, 1)
+            dot_of(i, 1)
+            if copying:
+                x_quantise(turned)
+            product(i, 2)
+            squares_of(i, 2)
+            first_squares(i)
+            if not ending:
+                last_on_scalar_and_gpsimd(p, 2)
+            store(p, 0, 2)
+            if not ending:
+                dot_of(i, 2)
+            product(i, 3)
+            squares_of(i, 3)
+            root(i)
+            if ending:
+                dot_of(i, 2)
+                last_on_scalar_and_gpsimd(p, 2)
+                last_on_vector(p, 3)
+            else:
+                last_on_scalar_and_gpsimd(p, 3)
+            store(p, 2, 4)
+            dot_of(i, 3)
+            if turning + 1 < ROW_TILES:
+                x_scale(turning + 1)
+            if turning < ROW_TILES:
+                x_turn(turning, 0)
+                x_turn(turning, 1)
+                x_copy(turning, 0, nc.scalar.copy)

import math
from contextlib import ExitStack

import concourse.mybir as mybir
from concourse.masks import make_identity

F32 = mybir.dt.float32
BF16 = mybir.dt.bfloat16
U32 = mybir.dt.uint32
U8 = mybir.dt.uint8
FP8X4 = mybir.dt.float8_e4m3fn_x4
ALU = mybir.AluOpType
ACT = mybir.ActivationFunctionType
AX = mybir.AxisListType

P = 128
M, K, N = 1024, 2048, 2048
ROW_TILES = M // P
PASSES = K // 512
COL_BANKS = N // 512
W_BLOCKS = N // 256
SLOTS = W_BLOCKS * PASSES
FLOPS = 2 * M * K * N

X_EVERY = 3
POWERS, LOG, SCALE, TURN, QUANTISE = 3, 6, 7, 11, 14
W_LAG = 2
TURNED_EARLY = 4
NORMS_ON_VECTOR = (0, 3)


def tile_pvfc_kernel(tc, x, W, b, out):
    nc = tc.nc
    with ExitStack() as ctx:
        const = ctx.enter_context(tc.tile_pool(name="const", bufs=1))
        xraw = ctx.enter_context(tc.tile_pool(name="xraw", bufs=1))
        wraw = ctx.enter_context(tc.tile_pool(name="wraw", bufs=5))
        vpool = ctx.enter_context(tc.tile_pool(name="vpool", bufs=4))
        xgp = ctx.enter_context(tc.tile_pool(name="xgp", bufs=3))
        wgp = ctx.enter_context(tc.tile_pool(name="wgp", bufs=6))
        junk = ctx.enter_context(tc.tile_pool(name="junk", bufs=2))
        junk1 = ctx.enter_context(tc.tile_pool(name="junk1", bufs=1))
        opool = ctx.enter_context(tc.tile_pool(name="opool", bufs=3))
        small = ctx.enter_context(tc.tile_pool(name="small", bufs=3))
        psum = ctx.enter_context(tc.psum_pool(name="psum", bufs=1))
        ctx.enter_context(tc.manual_schedule())

        x_v = x.rearrange("(p i) k -> p i k", i=ROW_TILES)
        W_v = W.rearrange("(g p) k -> p g k", p=P)
        out_v = out.rearrange("(p i) n -> p i n", i=ROW_TILES)
        xr = {}
        wr = {}
        S = {}

        free_banks = list(range(8))
        bank_of = {}

        def bank(key, shape):
            n = free_banks.pop(0)
            bank_of[key] = n
            S[key] = psum.tile(shape, F32, tag="bank%d" % n, name="bank%d" % n)
            return S[key]

        def release(key):
            free_banks.append(bank_of[key])

        def load_x(i):
            t = xraw.tile([P, K], BF16, name="xr%d" % i)
            nc.sync.dma_start(out=t[:], in_=x_v[:, i, :])
            xr[i] = t[:]

        def load_w(h, k0, k1):
            if k0 == 0:
                wr[h] = wraw.tile([P, 2 * K], BF16, name="wr")
            nc.sync.dma_start(out=wr[h][:].rearrange("p (g k) -> p g k", g=2)[:, :, k0:k1],
                              in_=W_v[:, 2 * h : 2 * h + 2, k0:k1])

        warm = const.tile([P, 1], F32)
        nc.vector.memset(warm[:], 1.0)
        b_rows = const.tile([P, P], BF16)
        nc.vector.memset(b_rows[:], 0.0)
        warm2 = const.tile([P, 1], F32)
        nc.scalar.activation(out=warm2[:], in_=warm[:], func=ACT.Ln)
        load_w(0, 0, K // 2)
        nc.sync.dma_start(out=b_rows[0 : N // P, :], in_=b.rearrange("(c q) -> c q", q=P))
        load_x(0)
        load_w(0, K // 2, K)
        for s in range(1, SLOTS):
            if s % PASSES == 0:
                load_w(s // PASSES, 0, K)
            if s % X_EVERY == 0 and s // X_EVERY < ROW_TILES:
                load_x(s // X_EVERY)
        b_all = const.tile([P, N], BF16)
        nc.sync.dma_start(out=b_all[:], in_=b.partition_broadcast(P))

        ident = const.tile([P, P], F32)
        make_identity(nc, ident[:])
        ones = const.tile([P, P], F32)
        nc.vector.memset(ones[:], 1.0)
        half_powers = const.tile([P, 2], F32)
        nc.vector.memset(half_powers[:, 0:1], 0.5)
        nc.vector.memset(half_powers[:, 1:2], -0.5)
        bases = const.tile([P, 2], F32)
        nc.vector.tensor_scalar(out=bases[:, 0:1], in0=warm[:], scalar1=math.e, scalar2=None, op0=ALU.mult)
        nc.vector.tensor_scalar(out=bases[:, 1:2], in0=warm[:], scalar1=math.exp(-1.0), scalar2=None, op0=ALU.mult)

        vcodes = const.tile([P, ROW_TILES * 512], U32, align_bytes=256)
        vscales = const.tile([P, ROW_TILES * 512], U8, align_bytes=256)
        wcodes = const.tile([P, COL_BANKS * PASSES * 512], U32, align_bytes=256)
        wscales = const.tile([P, COL_BANKS * PASSES * 512], U8, align_bytes=256)
        sc_b = const.tile([P, N], F32)
        half_root = const.tile([P, 1], F32)

        def col(name, n=1):
            S[name] = const.tile([P, n], F32, name=name)
            return S[name][:]

        def b_norm():
            part = col("b_part")
            squares = const.tile([P, P], F32)
            nc.scalar.activation(out=squares[:], in_=b_rows[:], func=ACT.Square, accum_out=part)
            b2_ps = bank("b2_ps", [P, 1])
            nc.tensor.matmul(b2_ps[:], lhsT=ones[:], rhs=part, start=True, stop=True)
            zz = col("zz", 2)
            nc.vector.tensor_scalar(out=zz[:, 0:1], in0=b2_ps[:], scalar1=1e-15, scalar2=400.0, op0=ALU.max, op1=ALU.min)
            nc.vector.tensor_scalar(out=zz[:, 1:2], in0=b2_ps[:], scalar1=1e-12, scalar2=400.0, op0=ALU.max, op1=ALU.min)
            nc.vector.tensor_copy(out=col("b2"), in_=b2_ps[:])
            release("b2_ps")
            nc.gpsimd.tensor_tensor(out=col("z", 2), in0=zz, in1=half_powers[:], op=ALU.pow)
            nc.gpsimd.tensor_tensor(out=col("exps", 2), in0=bases[:], in1=S["z"][:, 0:1].to_broadcast([P, 2]), op=ALU.pow)

        def b_scale():
            ee = S["exps"]
            nc.vector.tensor_scalar(out=col("y0"), in0=S["zz"][:, 0:1], scalar1=1.0 / 6.0, scalar2=1.0, op0=ALU.mult, op1=ALU.add)
            nc.vector.tensor_scalar(out=col("yb"), in0=ee[:, 0:1], scalar1=ee[:, 1:2], scalar2=S["z"][:, 1:2],
                                    op0=ALU.subtract, op1=ALU.mult)
            nc.vector.tensor_scalar(out=col("sc"), in0=S["yb"][:], scalar1=0.5, scalar2=S["y0"][:], op0=ALU.mult, op1=ALU.max)
            nc.vector.tensor_scalar(out=col("w2"), in0=S["sc"][:], scalar1=S["sc"][:], scalar2=S["b2"][:], op0=ALU.mult, op1=ALU.mult)
            nc.vector.tensor_scalar(out=col("w2q"), in0=S["w2"][:], scalar1=0.25, scalar2=0.25, op0=ALU.mult, op1=ALU.add)
            nc.gpsimd.tensor_tensor(out=half_root[:], in0=S["w2q"][:], in1=half_powers[:, 0:1], op=ALU.pow)

        def b_spread(half):
            js = slice(1024 * half, 1024 * half + 1024)
            nc.vector.tensor_scalar(out=sc_b[:, js], in0=b_all[:, js], scalar1=S["sc"][:], scalar2=None, op0=ALU.mult)

        q = const.tile([P, ROW_TILES, 1], F32)
        q_in = const.tile([P, ROW_TILES, 2], F32)
        q_pow = const.tile([P, ROW_TILES, 2], F32)
        q21 = const.tile([P, ROW_TILES, 1], F32)
        ln = const.tile([P, ROW_TILES, 1], F32)
        coef = const.tile([P, ROW_TILES, 1], F32)

        def x_norm(i):
            if i in NORMS_ON_VECTOR:
                unread = junk1.tile([P, K], BF16, name="unread_v")
                nc.vector.scalar_tensor_tensor(out=unread[:], in0=xr[i], scalar=1.0, in1=xr[i], op0=ALU.mult, op1=ALU.mult,
                                               accum_out=q[:, i, :])
            else:
                unread = junk1.tile([P, K], BF16, name="unread_s")
                nc.scalar.activation(out=unread[:], in_=xr[i], func=ACT.Square, accum_out=q[:, i, :])

        def x_powers(i):
            nc.vector.tensor_scalar(out=q_in[:, i, 0:1], in0=q[:, i, :], scalar1=1.0, scalar2=q[:, i, :], op0=ALU.add, op1=ALU.mult)
            nc.vector.tensor_scalar_max(q_in[:, i, 1:2], q[:, i, :], 1e-12)
            nc.gpsimd.tensor_tensor(out=q_pow[:, i, :], in0=q_in[:, i, :], in1=half_powers[:], op=ALU.pow)
            nc.vector.tensor_scalar(out=q21[:, i, :], in0=q[:, i, :], scalar1=2.0, scalar2=1.0, op0=ALU.mult, op1=ALU.add)

        def x_log(i):
            nc.scalar.activation(out=ln[:, i, :], in_=q_pow[:, i, 0:1], func=ACT.Ln, bias=q21[:, i, :], scale=2.0)

        def x_coef(i):
            nc.vector.tensor_scalar(out=coef[:, i, :], in0=ln[:, i, :], scalar1=0.5, scalar2=q_pow[:, i, 1:2], op0=ALU.mult, op1=ALU.mult)

        def x_scale(i):
            S["v", i] = vpool.tile([P, K], BF16, name="v")
            nc.vector.tensor_scalar(out=S["v", i][:], in0=xr[i], scalar1=coef[:, i, :], scalar2=None, op0=ALU.mult)

        def x_turn(i, half):
            words = S["v", i][:].bitcast(F32)
            t = bank(("xt", i, half), [P, 2, 2, P])
            for c in range(2):
                for u in range(2):
                    m0 = 256 * (2 * half + c)
                    nc.tensor.transpose(t[:, c, u, :], words[:, m0 + u : m0 + 256 : 2], ident[:])

        def x_copy(i, half, copy):
            if half == 0:
                S["xg", i] = xgp.tile([P, PASSES * P * 4], BF16, name="xg", align_bytes=64)
            src = S["xt", i, half][:].rearrange("p c u r -> p c r u")
            dst = S["xg", i][:, 1024 * half : 1024 * half + 1024].bitcast(F32).rearrange("p (c r u) -> p c r u", c=2, r=P, u=2)
            copy(out=dst, in_=src)
            release(("xt", i, half))

        def x_quantise(i):
            nc.vector.quantize_mx(out=vcodes[:, 512 * i : 512 * i + 512].bitcast(FP8X4),
                                  scales=vscales[:, 512 * i : 512 * i + 512], in_=S["xg", i][:])

        def w_turn(h, c):
            words = wr[h][:].bitcast(F32)
            t = bank(("wt", h, c), [P, 2, 2, P])
            for g in range(2):
                for u in range(2):
                    m0 = 1024 * g + 256 * c
                    nc.tensor.transpose(t[:, g, u, :], words[:, m0 + u : m0 + 256 : 2], ident[:])

        def w_copy(h, c, copy):
            S["wg", h, c] = wgp.tile([P, 1024], BF16, name="wg", align_bytes=64)
            dst = S["wg", h, c][:].bitcast(F32).rearrange("p (g n u) -> p g n u", g=2, n=P, u=2)
            copy(out=dst, in_=S["wt", h, c][:].rearrange("p g u n -> p g n u"))
            release(("wt", h, c))

        def w_quantise(h, c):
            col0 = ((h // 2) * PASSES + c) * 512 + 256 * (h % 2)
            nc.vector.quantize_mx(out=wcodes[:, col0 : col0 + 256].bitcast(FP8X4),
                                  scales=wscales[:, col0 : col0 + 256], in_=S["wg", h, c][:])

        def product(i, j):
            acc = bank(("acc", i, j), [P, 512])
            for c in range(PASSES):
                v0 = 512 * i + P * c
                w0 = (j * PASSES + c) * 512
                nc.tensor.matmul_mx(out=acc[:], lhsT=vcodes[:, v0 : v0 + P].bitcast(FP8X4),
                                    lhsT_scale=vscales[:, v0 : v0 + P],
                                    rhs=wcodes[:, w0 : w0 + 512].bitcast(FP8X4),
                                    rhs_scale=wscales[:, w0 : w0 + 512],
                                    start=(c == 0), stop=(c == PASSES - 1))

        def squares_of(i, j):
            if j == 0:
                S["s4", i] = small.tile([P, COL_BANKS], F32, name="s4")
            unread = junk.tile([P, 512], BF16, name="unread_sq")
            nc.scalar.activation(out=unread[:], in_=S["acc", i, j][:], func=ACT.Square, accum_out=S["s4", i][:, j : j + 1])

        def dot_of(i, j):
            if j == 0:
                S["d4", i] = small.tile([P, COL_BANKS], F32, name="d4")
            unread = junk.tile([P, 512], F32, name="unread_dot")
            nc.vector.scalar_tensor_tensor(out=unread[:], in0=S["acc", i, j][:], scalar=0.5, in1=sc_b[:, 512 * j : 512 * j + 512],
                                           op0=ALU.mult, op1=ALU.mult, accum_out=S["d4", i][:, j : j + 1])

        def first_squares(i):
            S["s3", i] = small.tile([P, 1], F32, name="s3")
            unread = small.tile([P, 3], F32, name="unread_s3")
            nc.scalar.activation(out=unread[:], in_=S["s4", i][:, 0:3], func=ACT.Identity, accum_out=S["s3", i][:])

        def root(i):
            u2 = small.tile([P, 2], F32, name="u2")
            nc.vector.tensor_scalar(out=u2[:, 0:1], in0=S["s4", i][:, 3:4], scalar1=S["s3", i][:], scalar2=400.0,
                                    op0=ALU.add, op1=ALU.min)
            nc.vector.tensor_scalar(out=u2[:, 1:2], in0=S["s4", i][:, 3:4], scalar1=S["s3", i][:], scalar2=1e-12,
                                    op0=ALU.add, op1=ALU.max)
            S["r", i] = small.tile([P, 2], F32, name="r")
            nc.gpsimd.tensor_tensor(out=S["r", i][:], in0=u2[:], in1=half_powers[:], op=ALU.pow)

        def exps_of(i):
            ee = small.tile([P, 3], F32, name="ee")
            S["ee", i] = ee
            r = S["r", i][:, 0:1]
            nc.scalar.activation(out=ee[:, 0:1], in_=r, func=ACT.Exp)
            nc.scalar.activation(out=ee[:, 1:2], in_=r, func=ACT.Exp, scale=-1.0)
            nc.scalar.activation(out=ee[:, 2:3], in_=r, func=ACT.Tanh, scale=0.5)

        def dot_sum(i):
            S["d", i] = small.tile([P, 1], F32, name="d")
            nc.vector.reduce_sum(out=S["d", i][:], in_=S["d4", i][:], axis=AX.X)

        def factor(i):
            ee = S["ee", i]
            inv = S["r", i][:, 1:2]
            S["o", i] = opool.tile([P, N], F32, name="o")
            two_sinhc = small.tile([P, 1], F32, name="two_sinhc")
            nc.vector.tensor_scalar(out=two_sinhc[:], in0=ee[:, 0:1], scalar1=ee[:, 1:2], scalar2=inv,
                                    op0=ALU.subtract, op1=ALU.mult)
            along = small.tile([P, 1], F32, name="along")
            nc.vector.tensor_scalar(out=along[:], in0=ee[:, 2:3], scalar1=inv, scalar2=S["d", i][:], op0=ALU.mult, op1=ALU.mult)
            S["a", i] = small.tile([P, 1], F32, name="a")
            nc.vector.scalar_tensor_tensor(out=S["a", i][:], in0=along[:], scalar=half_root[:], in1=two_sinhc[:],
                                           op0=ALU.add, op1=ALU.mult)

        def last_on_vector(i, j):
            js = slice(512 * j, 512 * j + 512)
            nc.vector.scalar_tensor_tensor(out=S["o", i][:, js], in0=S["acc", i, j][:], scalar=S["a", i][:], in1=sc_b[:, js],
                                           op0=ALU.mult, op1=ALU.add)
            release(("acc", i, j))

        def last_on_scalar_and_gpsimd(i, j):
            js = slice(512 * j, 512 * j + 512)
            au = junk.tile([P, 512], F32, name="au")
            nc.scalar.activation(out=au[:], in_=S["acc", i, j][:], func=ACT.Copy, scale=S["a", i][:])
            nc.gpsimd.tensor_tensor(out=S["o", i][:, js], in0=au[:], in1=sc_b[:, js], op=ALU.add)
            release(("acc", i, j))

        def store(i, j0, j1):
            hs = slice(512 * j0, 512 * j1)
            nc.sync.dma_start(out=out_v[:, i, hs], in_=S["o", i][:, hs])

        b_norm()
        for s in range(SLOTS + W_LAG + 1):
            for i in range(ROW_TILES):
                after = s - X_EVERY * i
                if after == POWERS:
                    x_powers(i)
                if after == LOG:
                    x_log(i)
                if after == TURN + 2 and i < TURNED_EARLY:
                    x_copy(i, 1, nc.vector.tensor_copy)
            if s < SLOTS:
                w_turn(s // PASSES, s % PASSES)
                on_vector = s >= 20 and s % 5 == 0
                w_copy(s // PASSES, s % PASSES, nc.vector.tensor_copy if on_vector else nc.scalar.copy)
            if W_LAG <= s < SLOTS + W_LAG:
                w_quantise((s - W_LAG) // PASSES, (s - W_LAG) % PASSES)
            if s == 4:
                b_scale()
            if s % X_EVERY == 0 and s // X_EVERY < ROW_TILES:
                x_norm(s // X_EVERY)
            for i in range(ROW_TILES):
                after = s - X_EVERY * i
                if after == LOG:
                    x_coef(i)
                if i < TURNED_EARLY:
                    if after == SCALE:
                        x_scale(i)
                    if after == TURN:
                        x_turn(i, 0)
                    if after == TURN + 1:
                        x_turn(i, 1)
                        x_copy(i, 0, nc.vector.tensor_copy)
                    if after == QUANTISE:
                        x_quantise(i)
            if s == 18:
                product(0, 0)
            if s == SLOTS - 2:
                b_spread(0)
            if s == SLOTS - 1:
                product(0, 1)
            if s == SLOTS:
                b_spread(1)
                squares_of(0, 0)
                squares_of(0, 1)
                product(0, 2)
            if s == SLOTS + 1:
                dot_of(0, 0)
            if s == SLOTS + 2:
                x_scale(TURNED_EARLY)
                dot_of(0, 1)
        nc.scalar.activation(out=warm2[:], in_=warm[:], func=ACT.Exp)
        squares_of(0, 2)
        dot_of(0, 2)
        product(0, 3)
        first_squares(0)
        squares_of(0, 3)
        root(0)
        dot_of(0, 3)

        for i in range(1, ROW_TILES + 1):
            p = i - 1
            turning = TURNED_EARLY + p
            turned = turning - 1
            copying = p > 0 and turned < ROW_TILES
            ending = i == ROW_TILES - 1
            if i < ROW_TILES:
                product(i, 0)
                squares_of(i, 0)
            exps_of(p)
            dot_sum(p)
            if copying:
                x_copy(turned, 1, nc.scalar.copy)
            if i < ROW_TILES:
                dot_of(i, 0)
            factor(p)
            if i == ROW_TILES:
                last_on_scalar_and_gpsimd(p, 0)
                for j in range(1, COL_BANKS):
                    last_on_vector(p, j)
                    store(p, j, j + 1)
                    if j == 2:
                        store(p, 0, 1)
                continue
            last_on_vector(p, 0)
            last_on_vector(p, 1)
            product(i, 1)
            squares_of(i, 1)
            dot_of(i, 1)
            if copying:
                x_quantise(turned)
            product(i, 2)
            squares_of(i, 2)
            first_squares(i)
            if not ending:
                last_on_scalar_and_gpsimd(p, 2)
            store(p, 0, 2)
            if not ending:
                dot_of(i, 2)
            product(i, 3)
            squares_of(i, 3)
            root(i)
            if ending:
                dot_of(i, 2)
                last_on_scalar_and_gpsimd(p, 2)
                last_on_vector(p, 3)
            else:
                last_on_scalar_and_gpsimd(p, 3)
            store(p, 2, 4)
            dot_of(i, 3)
            if turning + 1 < ROW_TILES:
                x_scale(turning + 1)
            if turning < ROW_TILES:
                x_turn(turning, 0)
                x_turn(turning, 1)
                x_copy(turning, 0, nc.scalar.copy)
